import numpy as np
import ml_dtypes


def mxq(x, axis, fmt="e4m3"):
    dtype, down = {"e4m3": (ml_dtypes.float8_e4m3fn, 7), "e5m2": (ml_dtypes.float8_e5m2, 14)}[fmt]
    v = np.moveaxis(np.asarray(x, np.float32).astype(ml_dtypes.bfloat16).astype(np.float64), axis, -1)
    blocks = v.reshape(v.shape[:-1] + (-1, 32))
    amax = np.abs(blocks).max(-1, keepdims=True)
    byte = np.maximum(np.where(amax > 0, np.frexp(amax)[1] - 1 + 127, 0) - down, 1)
    scale = np.exp2(byte - 127.0)
    codes = (blocks / scale).astype(np.float32).astype(dtype).astype(np.float64)
    return np.moveaxis((codes * scale).reshape(v.shape), -1, axis)


WIDE = False


def mx_kscale(k):
    if not WIDE:
        return np.ones(k)
    levels = np.array([10, -10, 5, -5, 0])
    a = np.random.permutation(np.resize(levels, k // 512 * 4)).reshape(k // 512, 4)
    idx = np.arange(k)
    return np.exp2(a[idx // 512, idx % 128 // 32])


BF16 = ml_dtypes.bfloat16


def bf(x):
    return np.asarray(x, np.float32).astype(BF16)


def f64(x):
    return np.asarray(x).astype(np.float64)


B, N, C0, C1, C2, O0, O1, O2 = 16, 32, 512, 256, 256, 512, 2048, 256
G = C1 + C2
K = 2 * G


def sigmoid(v):
    return 1.0 / (1.0 + np.exp(-v))


def setup_inputs():
    s = mx_kscale(G)
    ss = np.concatenate([s, s])
    return {"x1": bf(np.random.random((B, N, C1)) * s[:C1]),
            "x2": bf(np.random.random((B, N, N, C2)) * s[C1:]),
            "W2": bf(np.random.standard_normal((K, O2)) * 2.0 / np.sqrt(K) / ss[:, None]),
            "b2": bf(np.random.standard_normal(O2) * 0.3)}


def reference(x1, x2, W2, b2):
    x1, x2 = f64(x1), f64(x2)
    e1 = np.broadcast_to(x1[:, :, None, :], (B, N, N, C1))
    g = np.concatenate([e1, x2], axis=-1)
    f2 = np.concatenate([g, np.swapaxes(g, 1, 2)], axis=-1)
    return sigmoid((mxq(f2, 3, "e4m3") @ mxq(f64(W2), 0, "e4m3")) + f64(b2))

@@ -1,0 +1,293 @@
+from contextlib import ExitStack
+
+import concourse.mybir as mybir
+from concourse.masks import make_identity
+
+F32 = mybir.dt.float32
+BF16 = mybir.dt.bfloat16
+I32 = mybir.dt.int32
+U32 = mybir.dt.uint32
+U8 = mybir.dt.uint8
+FP8X4 = mybir.dt.float8_e4m3fn_x4
+ADD = mybir.AluOpType.add
+SIGMOID = mybir.ActivationFunctionType.Sigmoid
+
+P = 128
+O = 256
+FLOPS = 2 * 16 * 32 * 32 * 1024 * 256
+R = 2
+
+
+def half_rounds():
+    rs = []
+    for u in range(8):
+        if u % 2 == 0:
+            rs.append(((u, u), (u + 1, u + 1)))
+        for v in range(u + 1, 8):
+            rs.append(((u, v), (v, u)))
+    return rs
+
+
+def tile_differentiablelogicmachine_pa_t_kernel(tc, x1, x2, W2, b2, out):
+    nc = tc.nc
+    with ExitStack() as ctx:
+        const = ctx.enter_context(tc.tile_pool(name="const", bufs=1))
+        xpool = ctx.enter_context(tc.tile_pool(name="xpool", bufs=8))
+        gpool = ctx.enter_context(tc.tile_pool(name="gpool", bufs=3))
+        upool = ctx.enter_context(tc.tile_pool(name="upool", bufs=2))
+        psum_t = ctx.enter_context(tc.psum_pool(name="psum_t", bufs=4))
+        psum_o = ctx.enter_context(tc.psum_pool(name="psum_o", bufs=4))
+        ctx.enter_context(tc.manual_schedule())
+
+        wraw = const.tile([P, 4, 2, O], BF16)
+        nc.sync.dma_start(out=wraw[:], in_=W2.rearrange("(k p e) o -> p k e o", k=4, p=P, e=2))
+        x1s = const.tile([P, 4, O], BF16)
+        nc.sync.dma_start(out=x1s[:], in_=x1.rearrange("b (q r) c -> (b q) r c", r=4))
+        brow = const.tile([P, O], BF16)
+        nc.vector.memset(brow[:], 0.0)
+        nc.sync.dma_start(out=brow[0:1, :], in_=b2.rearrange("(a o) -> a o", a=1))
+        xview = x2.rearrange(
+            "(h B) (I q e) (J v) c -> h q J (B I) e (v c)", h=2, B=8, I=4, q=4, e=2, J=4, v=8
+        )
+        xs32 = {}
+        for h in range(2):
+            for q in range(4):
+                xs = xpool.tile([P, 2, 8 * O], BF16)
+                for J in range(4):
+                    nc.sync.dma_start(out=xs[J:P:4, :, :], in_=xview[h, q, J])
+                xs32[(h, q)] = xs[:].bitcast(F32)
+        oview = out.rearrange("(h B) (I u) (J v) o -> h J (B I) u v o", h=2, B=8, I=4, u=8, J=4, v=8)
+
+        ident = const.tile([P, P], F32)
+        make_identity(nc, ident[:])
+        ones = const.tile([P, P], BF16)
+        nc.vector.memset(ones[:], 1.0)
+        warm = const.tile([P, 1], F32)
+        nc.vector.memset(warm[:], 0.0)
+        warm2 = const.tile([P, 1], F32)
+        nc.scalar.activation(out=warm2[:], in_=warm[:], func=SIGMOID)
+        gwx = const.tile([P, 2, O, 2, 2], BF16, align_bytes=64)
+        nc.vector.memset(gwx[:], 0.0)
+        x1z = const.tile([P, 2, 8, 32, 2], F32, align_bytes=64)
+        nc.vector.memset(x1z[:], 0.0)
+        perm = const.tile([P, P], F32)
+        nc.vector.tensor_copy(
+            out=perm[:].rearrange("p (B I J) -> p B I J", B=8, I=4, J=4),
+            in_=ident[:].rearrange("p (B J I) -> p B I J", B=8, J=4, I=4),
+        )
+
+        gwa = const.tile([P, O, 2, 2], BF16, align_bytes=64)
+        nc.vector.tensor_copy(out=gwa[:], in_=wraw[:, 1:4:2, :, :].rearrange("p s e o -> p o s e"))
+        for x in range(2):
+            nc.vector.tensor_copy(
+                out=gwx[:, x, :, 0, :], in_=wraw[:, 2 * x, :, :].rearrange("p e o -> p o e")
+            )
+        waq = const.tile([P, O], U32, align_bytes=64)
+        was = const.tile([P, O], U8, align_bytes=64)
+        nc.vector.quantize_mx(
+            out=waq[:].bitcast(FP8X4), scales=was[:], in_=gwa[:].rearrange("p o s e -> p (o s e)")
+        )
+        wxq = const.tile([P, 2 * O], U32, align_bytes=64)
+        wxs = const.tile([P, 2 * O], U8, align_bytes=64)
+        nc.vector.quantize_mx(
+            out=wxq[:].bitcast(FP8X4), scales=wxs[:], in_=gwx[:].rearrange("p x o s e -> p (x o s e)")
+        )
+
+        x1t = psum_t.tile([P, 4, P], F32, name="xt")
+        for r in range(4):
+            nc.tensor.transpose(out=x1t[:, r, :], in_=x1s[:, r, :].bitcast(F32), identity=ident[:])
+        for h in range(2):
+            nc.vector.tensor_copy(
+                out=x1z[:, h, :, :, 0].rearrange("p (t r) m -> p t r m", t=2),
+                in_=x1t[:].rearrange("p r (h m t) -> p h t r m", h=2, m=32, t=2)[:, h, :, :, :],
+            )
+        psb = psum_o.tile([P, 2 * O], F32, name="ps")
+        nc.tensor.matmul(out=psb[:, 0:O], lhsT=ones[:], rhs=brow[:], start=True, stop=True)
+        bias = const.tile([P, O], F32)
+        nc.vector.tensor_copy(out=bias[:], in_=psb[:, 0:O])
+
+        q1c = const.tile([P, 512], U32, align_bytes=64)
+        q1s = const.tile([P, 512], U8, align_bytes=64)
+        nc.vector.memset(q1s[:].bitcast(I32), 0)
+        nc.vector.quantize_mx(
+            out=q1c[:].bitcast(FP8X4),
+            scales=q1s[:],
+            in_=x1z[:].rearrange("p h t m w -> p (h t m w)").bitcast(BF16),
+        )
+        scj = const.tile([P, 2, 8, P], U32, align_bytes=64)
+        ssj = const.tile([P, 2, 8, P], U8, align_bytes=64)
+        nc.vector.tensor_copy(
+            out=scj[:].rearrange("p h t (B I J) -> p (h t B) I J", B=8, I=4, J=4).bitcast(I32),
+            in_=q1c[:].rearrange("p (g J) -> p g J", J=4).bitcast(I32).unsqueeze(2).to_broadcast([P, P, 4, 4]),
+        )
+        nc.vector.tensor_copy(
+            out=ssj[:].rearrange("p h t c -> p (h t c)").bitcast(I32).rearrange("p (g I) -> p g I", I=4),
+            in_=q1s[:].bitcast(I32).unsqueeze(2).to_broadcast([P, P, 4]),
+        )
+
+        sci = const.tile([P, 2, 8, P], U32, align_bytes=64)
+        ssi = const.tile([P, 2, 8, P], U8, align_bytes=64)
+        zall = const.tile([P, 2, 8, O], F32)
+        psz = {}
+
+        def unit_quantise(j):
+            h, t0 = j // 2, 4 * (j % 2)
+            gx = upool.tile([P, 4, 32, 4, 2], F32, align_bytes=64)
+            nc.vector.tensor_copy(
+                out=gx[:], in_=x1z[:, h, t0 : t0 + 4, :, :].unsqueeze(3).to_broadcast([P, 4, 32, 4, 2])
+            )
+            nc.vector.quantize_mx(
+                out=sci[:, h, t0 : t0 + 4, :].rearrange("p t c -> p (t c)").bitcast(FP8X4),
+                scales=ssi[:, h, t0 : t0 + 4, :].rearrange("p t c -> p (t c)"),
+                in_=gx[:].rearrange("p t m J w -> p (t m J w)").bitcast(BF16),
+            )
+
+        def unit_matmul(j):
+            h, t0 = j // 2, 4 * (j % 2)
+            for i in range(2):
+                pz = psum_o.tile([P, 2 * O], F32, name="ps")
+                for tt in range(2):
+                    t = t0 + 2 * i + tt
+                    nc.tensor.matmul_mx(
+                        out=pz[:, tt * O : (tt + 1) * O],
+                        lhsT=sci[:, h, t, :].bitcast(FP8X4),
+                        lhsT_scale=ssi[:, h, t, :],
+                        rhs=wxq[:, 0:O].bitcast(FP8X4),
+                        rhs_scale=wxs[:, 0:O],
+                        start=True,
+                        stop=True,
+                    )
+                psz[(j, i)] = pz
+
+        def unit_exit(j):
+            h, t0 = j // 2, 4 * (j % 2)
+            for i in range(2):
+                nc.vector.tensor_tensor(
+                    out=zall[:, h, t0 + 2 * i : t0 + 2 * i + 2, :],
+                    in0=psz[(j, i)][:].rearrange("p (t o) -> p t o", t=2),
+                    in1=bias[:].unsqueeze(1).to_broadcast([P, 2, O]),
+                    op=ADD,
+                )
+
+        rounds = [(h, pair) for h in range(2) for pair in half_rounds()]
+        n_groups = len(rounds) // R
+        obuf = const.tile([P, 8, 8, O], F32)
+        oflat = obuf[:].rearrange("p a c o -> p (a c) o")
+        xts, gts, qcs, qss, pss, left, right = {}, {}, {}, {}, {}, {}, {}
+
+        def grp(h, a, c):
+            return xs32[(h, a // 2)][:, a % 2, c * P : (c + 1) * P]
+
+        def oslots(pair):
+            i0, i1 = 8 * pair[0][0] + pair[0][1], 8 * pair[1][0] + pair[1][1]
+            return oflat[:, i0 : i1 + 1 : i1 - i0, :]
+
+        def st_transpose(g):
+            for k in range(R * g, R * g + R):
+                h, pair = rounds[k]
+                xt = psum_t.tile([P, 4, P], F32)
+                for s in range(2):
+                    a, c = pair[s]
+                    nc.tensor.transpose(out=xt[:, 2 * s, :], in_=grp(h, a, c), identity=ident[:])
+                    nc.tensor.transpose(out=xt[:, 2 * s + 1, :], in_=grp(h, c, a), identity=perm[:])
+                xts[k] = xt
+
+        def st_exit(g):
+            gt = gpool.tile([P, R, 2, P, 2], F32, align_bytes=64)
+            for i in range(R):
+                nc.scalar.copy(
+                    out=gt[:, i, :, :, :], in_=xts[R * g + i][:].rearrange("p (s w) c -> p s c w", w=2)
+                )
+            gts[g] = gt
+
+        def st_quantise(g):
+            qc = gpool.tile([P, R * 2 * P], U32, align_bytes=64)
+            qs = gpool.tile([P, R * 2 * P], U8, align_bytes=64)
+            nc.vector.quantize_mx(
+                out=qc[:].bitcast(FP8X4),
+                scales=qs[:],
+                in_=gts[g][:].rearrange("p i s c w -> p (i s c w)").bitcast(BF16),
+            )
+            qcs[g] = qc
+            qss[g] = qs
+
+        def st_matmul(g):
+            for i in range(R):
+                h, pair = rounds[R * g + i]
+                ps = psum_o.tile([P, 2 * O], F32)
+                for s in range(2):
+                    c = pair[s][1]
+                    col = (2 * i + s) * P
+                    nc.tensor.matmul_mx(
+                        out=ps[:, s * O : (s + 1) * O],
+                        lhsT=qcs[g][:, col : col + P].bitcast(FP8X4),
+                        lhsT_scale=qss[g][:, col : col + P],
+                        rhs=waq[:].bitcast(FP8X4),
+                        rhs_scale=was[:],
+                        start=True,
+                        stop=False,
+                    )
+                    nc.tensor.matmul_mx(
+                        out=ps[:, s * O : (s + 1) * O],
+                        lhsT=scj[:, h, c, :].bitcast(FP8X4),
+                        lhsT_scale=ssj[:, h, c, :],
+                        rhs=wxq[:, O : 2 * O].bitcast(FP8X4),
+                        rhs_scale=wxs[:, O : 2 * O],
+                        start=False,
+                        stop=True,
+                    )
+                pss[R * g + i] = ps
+
+        def st_add(g):
+            for k in range(R * g, R * g + R):
+                h, pair = rounds[k]
+                a0, a1 = pair[0][0], pair[1][0]
+                nc.vector.tensor_tensor(
+                    out=oslots(pair),
+                    in0=pss[k][:].rearrange("p (s o) -> p s o", s=2),
+                    in1=zall[:, h, a0 : a1 + 1 : a1 - a0, :],
+                    op=ADD,
+                )
+
+        def st_sigmoid(g):
+            for k in range(R * g, R * g + R):
+                h, pair = rounds[k]
+                nc.scalar.activation(out=oslots(pair), in_=oslots(pair), func=SIGMOID)
+                for a, c in pair:
+                    m2 = a - a % 2
+                    if c < m2:
+                        left[(h, m2)] = left.get((h, m2), 0) + 1
+                        if left[(h, m2)] == 2 * m2:
+                            for J in range(4):
+                                nc.sync.dma_start(
+                                    out=oview[h, J, :, m2 : m2 + 2, 0:m2, :],
+                                    in_=obuf[J:P:4, m2 : m2 + 2, 0:m2, :],
+                                )
+                    else:
+                        right[(h, a)] = right.get((h, a), 0) + 1
+                        if right[(h, a)] == 8 - m2:
+                            for J in range(4):
+                                nc.sync.dma_start(
+                                    out=oview[h, J, :, a, m2:8, :], in_=obuf[J:P:4, a, m2:8, :]
+                                )
+
+        unit_start = {0: 0, 1: 1, 8: 2, 9: 3}
+        for n in range(n_groups + 5):
+            if 0 <= n - 5 < n_groups:
+                st_sigmoid(n - 5)
+            if 0 <= n - 4 < n_groups:
+                st_add(n - 4)
+            if n - 2 in unit_start:
+                unit_exit(unit_start[n - 2])
+            if 0 <= n - 3 < n_groups:
+                st_matmul(n - 3)
+            if n - 1 in unit_start:
+                unit_matmul(unit_start[n - 1])
+            if 0 <= n - 2 < n_groups:
+                st_quantise(n - 2)
+            if n in unit_start:
+                unit_quantise(unit_start[n])
+            if 0 <= n - 1 < n_groups:
+                st_exit(n - 1)
+            if n < n_groups:
+                st_transpose(n)

@@ -15,17 +15,13 @@ SIGMOID = mybir.ActivationFunctionType.Sigmoid
 P = 128
 O = 256
 FLOPS = 2 * 16 * 32 * 32 * 1024 * 256
-R = 2
 
 
-def half_rounds():
-    rs = []
-    for u in range(8):
-        if u % 2 == 0:
-            rs.append(((u, u), (u + 1, u + 1)))
-        for v in range(u + 1, 8):
-            rs.append(((u, v), (v, u)))
-    return rs
+def block_groups(A, C):
+    if A == C:
+        a = 2 * A
+        return [[((a, a), (a + 1, a + 1)), ((a, a + 1), (a + 1, a))]]
+    return [[((a, c), (c, a)) for c in (2 * C, 2 * C + 1)] for a in (2 * A, 2 * A + 1)]
 
 
 def tile_differentiablelogicmachine_pa_t_kernel(tc, x1, x2, W2, b2, out):
@@ -70,6 +66,9 @@ def tile_differentiablelogicmachine_pa_t_kernel(tc, x1, x2, W2, b2, out):
         nc.vector.memset(gwx[:], 0.0)
         x1z = const.tile([P, 2, 8, 32, 2], F32, align_bytes=64)
         nc.vector.memset(x1z[:], 0.0)
+        q1c = const.tile([P, 2, 256], U32, align_bytes=64)
+        q1s = const.tile([P, 2, 256], U8, align_bytes=64)
+        nc.vector.memset(q1s[:].bitcast(I32), 0)
         perm = const.tile([P, P], F32)
         nc.vector.tensor_copy(
             out=perm[:].rearrange("p (B I J) -> p B I J", B=8, I=4, J=4),
@@ -77,11 +76,9 @@ def tile_differentiablelogicmachine_pa_t_kernel(tc, x1, x2, W2, b2, out):
         )
 
         gwa = const.tile([P, O, 2, 2], BF16, align_bytes=64)
-        nc.vector.tensor_copy(out=gwa[:], in_=wraw[:, 1:4:2, :, :].rearrange("p s e o -> p o s e"))
+        nc.scalar.copy(out=gwa[:], in_=wraw[:, 1:4:2, :, :].rearrange("p s e o -> p o s e"))
         for x in range(2):
-            nc.vector.tensor_copy(
-                out=gwx[:, x, :, 0, :], in_=wraw[:, 2 * x, :, :].rearrange("p e o -> p o e")
-            )
+            nc.scalar.copy(out=gwx[:, x, :, 0, :], in_=wraw[:, 2 * x, :, :].rearrange("p e o -> p o e"))
         waq = const.tile([P, O], U32, align_bytes=64)
         was = const.tile([P, O], U8, align_bytes=64)
         nc.vector.quantize_mx(
@@ -89,46 +86,39 @@ def tile_differentiablelogicmachine_pa_t_kernel(tc, x1, x2, W2, b2, out):
         )
         wxq = const.tile([P, 2 * O], U32, align_bytes=64)
         wxs = const.tile([P, 2 * O], U8, align_bytes=64)
-        nc.vector.quantize_mx(
-            out=wxq[:].bitcast(FP8X4), scales=wxs[:], in_=gwx[:].rearrange("p x o s e -> p (x o s e)")
-        )
 
         x1t = psum_t.tile([P, 4, P], F32, name="xt")
         for r in range(4):
             nc.tensor.transpose(out=x1t[:, r, :], in_=x1s[:, r, :].bitcast(F32), identity=ident[:])
-        for h in range(2):
-            nc.vector.tensor_copy(
-                out=x1z[:, h, :, :, 0].rearrange("p (t r) m -> p t r m", t=2),
-                in_=x1t[:].rearrange("p r (h m t) -> p h t r m", h=2, m=32, t=2)[:, h, :, :, :],
-            )
         psb = psum_o.tile([P, 2 * O], F32, name="ps")
         nc.tensor.matmul(out=psb[:, 0:O], lhsT=ones[:], rhs=brow[:], start=True, stop=True)
         bias = const.tile([P, O], F32)
-        nc.vector.tensor_copy(out=bias[:], in_=psb[:, 0:O])
 
-        q1c = const.tile([P, 512], U32, align_bytes=64)
-        q1s = const.tile([P, 512], U8, align_bytes=64)
-        nc.vector.memset(q1s[:].bitcast(I32), 0)
-        nc.vector.quantize_mx(
-            out=q1c[:].bitcast(FP8X4),
-            scales=q1s[:],
-            in_=x1z[:].rearrange("p h t m w -> p (h t m w)").bitcast(BF16),
-        )
         scj = const.tile([P, 2, 8, P], U32, align_bytes=64)
         ssj = const.tile([P, 2, 8, P], U8, align_bytes=64)
-        nc.vector.tensor_copy(
-            out=scj[:].rearrange("p h t (B I J) -> p (h t B) I J", B=8, I=4, J=4).bitcast(I32),
-            in_=q1c[:].rearrange("p (g J) -> p g J", J=4).bitcast(I32).unsqueeze(2).to_broadcast([P, P, 4, 4]),
-        )
-        nc.vector.tensor_copy(
-            out=ssj[:].rearrange("p h t c -> p (h t c)").bitcast(I32).rearrange("p (g I) -> p g I", I=4),
-            in_=q1s[:].bitcast(I32).unsqueeze(2).to_broadcast([P, P, 4]),
-        )
-
         sci = const.tile([P, 2, 8, P], U32, align_bytes=64)
         ssi = const.tile([P, 2, 8, P], U8, align_bytes=64)
         zall = const.tile([P, 2, 8, O], F32)
         psz = {}
+
+        def x1_half(h):
+            nc.vector.tensor_copy(
+                out=x1z[:, h, :, :, 0].rearrange("p (t r) m -> p t r m", t=2),
+                in_=x1t[:].rearrange("p r (h m t) -> p h t r m", h=2, m=32, t=2)[:, h, :, :, :],
+            )
+            nc.vector.quantize_mx(
+                out=q1c[:, h, :].bitcast(FP8X4),
+                scales=q1s[:, h, :],
+                in_=x1z[:, h, :, :, :].rearrange("p t m w -> p (t m w)").bitcast(BF16),
+            )
+            nc.vector.tensor_copy(
+                out=scj[:, h, :, :].rearrange("p t (B I J) -> p (t B) I J", B=8, I=4, J=4).bitcast(I32),
+                in_=q1c[:, h, :].rearrange("p (g J) -> p g J", J=4).bitcast(I32).unsqueeze(2).to_broadcast([P, 64, 4, 4]),
+            )
+            nc.vector.tensor_copy(
+                out=ssj[:, h, :, :].rearrange("p t c -> p (t c)").bitcast(I32).rearrange("p (g I) -> p g I", I=4),
+                in_=q1s[:, h, :].bitcast(I32).unsqueeze(2).to_broadcast([P, 64, 4]),
+            )
 
         def unit_quantise(j):
             h, t0 = j // 2, 4 * (j % 2)
@@ -169,11 +159,24 @@ def tile_differentiablelogicmachine_pa_t_kernel(tc, x1, x2, W2, b2, out):
                     op=ADD,
                 )
 
-        rounds = [(h, pair) for h in range(2) for pair in half_rounds()]
-        n_groups = len(rounds) // R
+        x1_half(0)
+        nc.vector.quantize_mx(
+            out=wxq[:].bitcast(FP8X4), scales=wxs[:], in_=gwx[:].rearrange("p x o s e -> p (x o s e)")
+        )
+        nc.vector.tensor_copy(out=bias[:], in_=psb[:, 0:O])
+
+        groups = []
+        for h in range(2):
+            for C in range(4):
+                for A in range(C + 1):
+                    gs = block_groups(A, C)
+                    for i in range(len(gs)):
+                        last = i == len(gs) - 1
+                        groups.append((h, gs[i], sorted(set([(A, C), (C, A)])) if last else []))
+        n_groups = len(groups)
         obuf = const.tile([P, 8, 8, O], F32)
         oflat = obuf[:].rearrange("p a c o -> p (a c) o")
-        xts, gts, qcs, qss, pss, left, right = {}, {}, {}, {}, {}, {}, {}
+        xts, gts, qcs, qss, pss = {}, {}, {}, {}, {}
 
         def grp(h, a, c):
             return xs32[(h, a // 2)][:, a % 2, c * P : (c + 1) * P]
@@ -183,26 +186,26 @@ def tile_differentiablelogicmachine_pa_t_kernel(tc, x1, x2, W2, b2, out):
             return oflat[:, i0 : i1 + 1 : i1 - i0, :]
 
         def st_transpose(g):
-            for k in range(R * g, R * g + R):
-                h, pair = rounds[k]
+            h, rounds, stores = groups[g]
+            for i in range(2):
                 xt = psum_t.tile([P, 4, P], F32)
                 for s in range(2):
-                    a, c = pair[s]
+                    a, c = rounds[i][s]
                     nc.tensor.transpose(out=xt[:, 2 * s, :], in_=grp(h, a, c), identity=ident[:])
                     nc.tensor.transpose(out=xt[:, 2 * s + 1, :], in_=grp(h, c, a), identity=perm[:])
-                xts[k] = xt
+                xts[(g, i)] = xt
 
         def st_exit(g):
-            gt = gpool.tile([P, R, 2, P, 2], F32, align_bytes=64)
-            for i in range(R):
+            gt = gpool.tile([P, 2, 2, P, 2], F32, align_bytes=64)
+            for i in range(2):
                 nc.scalar.copy(
-                    out=gt[:, i, :, :, :], in_=xts[R * g + i][:].rearrange("p (s w) c -> p s c w", w=2)
+                    out=gt[:, i, :, :, :], in_=xts[(g, i)][:].rearrange("p (s w) c -> p s c w", w=2)
                 )
             gts[g] = gt
 
         def st_quantise(g):
-            qc = gpool.tile([P, R * 2 * P], U32, align_bytes=64)
-            qs = gpool.tile([P, R * 2 * P], U8, align_bytes=64)
+            qc = gpool.tile([P, 4 * P], U32, align_bytes=64)
+            qs = gpool.tile([P, 4 * P], U8, align_bytes=64)
             nc.vector.quantize_mx(
                 out=qc[:].bitcast(FP8X4),
                 scales=qs[:],
@@ -212,11 +215,11 @@ def tile_differentiablelogicmachine_pa_t_kernel(tc, x1, x2, W2, b2, out):
             qss[g] = qs
 
         def st_matmul(g):
-            for i in range(R):
-                h, pair = rounds[R * g + i]
+            h, rounds, stores = groups[g]
+            for i in range(2):
                 ps = psum_o.tile([P, 2 * O], F32)
                 for s in range(2):
-                    c = pair[s][1]
+                    c = rounds[i][s][1]
                     col = (2 * i + s) * P
                     nc.tensor.matmul_mx(
                         out=ps[:, s * O : (s + 1) * O],
@@ -236,57 +239,47 @@ def tile_differentiablelogicmachine_pa_t_kernel(tc, x1, x2, W2, b2, out):
                         start=False,
                         stop=True,
                     )
-                pss[R * g + i] = ps
+                pss[(g, i)] = ps
 
         def st_add(g):
-            for k in range(R * g, R * g + R):
-                h, pair = rounds[k]
-                a0, a1 = pair[0][0], pair[1][0]
+            h, rounds, stores = groups[g]
+            for i in range(2):
+                a0, a1 = rounds[i][0][0], rounds[i][1][0]
                 nc.vector.tensor_tensor(
-                    out=oslots(pair),
-                    in0=pss[k][:].rearrange("p (s o) -> p s o", s=2),
+                    out=oslots(rounds[i]),
+                    in0=pss[(g, i)][:].rearrange("p (s o) -> p s o", s=2),
                     in1=zall[:, h, a0 : a1 + 1 : a1 - a0, :],
                     op=ADD,
                 )
 
         def st_sigmoid(g):
-            for k in range(R * g, R * g + R):
-                h, pair = rounds[k]
-                nc.scalar.activation(out=oslots(pair), in_=oslots(pair), func=SIGMOID)
-                for a, c in pair:
-                    m2 = a - a % 2
-                    if c < m2:
-                        left[(h, m2)] = left.get((h, m2), 0) + 1
-                        if left[(h, m2)] == 2 * m2:
-                            for J in range(4):
-                                nc.sync.dma_start(
-                                    out=oview[h, J, :, m2 : m2 + 2, 0:m2, :],
-                                    in_=obuf[J:P:4, m2 : m2 + 2, 0:m2, :],
-                                )
-                    else:
-                        right[(h, a)] = right.get((h, a), 0) + 1
-                        if right[(h, a)] == 8 - m2:
-                            for J in range(4):
-                                nc.sync.dma_start(
-                                    out=oview[h, J, :, a, m2:8, :], in_=obuf[J:P:4, a, m2:8, :]
-                                )
+            h, rounds, stores = groups[g]
+            for i in range(2):
+                nc.scalar.activation(out=oslots(rounds[i]), in_=oslots(rounds[i]), func=SIGMOID)
+            for A, C in stores:
+                for J in range(4):
+                    nc.sync.dma_start(
+                        out=oview[h, J, :, 2 * A : 2 * A + 2, 2 * C : 2 * C + 2, :],
+                        in_=obuf[J:P:4, 2 * A : 2 * A + 2, 2 * C : 2 * C + 2, :],
+                    )
 
-        unit_start = {0: 0, 1: 1, 8: 2, 9: 3}
         for n in range(n_groups + 5):
             if 0 <= n - 5 < n_groups:
                 st_sigmoid(n - 5)
             if 0 <= n - 4 < n_groups:
                 st_add(n - 4)
-            if n - 2 in unit_start:
-                unit_exit(unit_start[n - 2])
+            if 0 <= n - 2 < 4:
+                unit_exit(n - 2)
             if 0 <= n - 3 < n_groups:
                 st_matmul(n - 3)
-            if n - 1 in unit_start:
-                unit_matmul(unit_start[n - 1])
+            if 0 <= n - 1 < 4:
+                unit_matmul(n - 1)
             if 0 <= n - 2 < n_groups:
                 st_quantise(n - 2)
-            if n in unit_start:
-                unit_quantise(unit_start[n])
+            if n == 1:
+                x1_half(1)
+            if n < 4:
+                unit_quantise(n)
             if 0 <= n - 1 < n_groups:
                 st_exit(n - 1)
             if n < n_groups:

@@ -14,6 +14,9 @@ SIGMOID = mybir.ActivationFunctionType.Sigmoid
 
 P = 128
 O = 256
+BG0 = 3
+XG0 = 24
+XM = 2
 FLOPS = 2 * 16 * 32 * 32 * 1024 * 256
 
 
@@ -29,16 +32,16 @@ def tile_differentiablelogicmachine_pa_t_kernel(tc, x1, x2, W2, b2, out):
     with ExitStack() as ctx:
         const = ctx.enter_context(tc.tile_pool(name="const", bufs=1))
         xpool = ctx.enter_context(tc.tile_pool(name="xpool", bufs=8))
-        gpool = ctx.enter_context(tc.tile_pool(name="gpool", bufs=3))
+        gpool = ctx.enter_context(tc.tile_pool(name="gpool", bufs=4))
         upool = ctx.enter_context(tc.tile_pool(name="upool", bufs=2))
         psum_t = ctx.enter_context(tc.psum_pool(name="psum_t", bufs=4))
         psum_o = ctx.enter_context(tc.psum_pool(name="psum_o", bufs=4))
         ctx.enter_context(tc.manual_schedule())
 
-        wraw = const.tile([P, 4, 2, O], BF16)
-        nc.sync.dma_start(out=wraw[:], in_=W2.rearrange("(k p e) o -> p k e o", k=4, p=P, e=2))
         x1s = const.tile([P, 4, O], BF16)
         nc.sync.dma_start(out=x1s[:], in_=x1.rearrange("b (q r) c -> (b q) r c", r=4))
+        wraw = const.tile([P, 4, 2, O], BF16)
+        nc.sync.dma_start(out=wraw[:], in_=W2.rearrange("(k p e) o -> p k e o", k=4, p=P, e=2))
         brow = const.tile([P, O], BF16)
         nc.vector.memset(brow[:], 0.0)
         nc.sync.dma_start(out=brow[0:1, :], in_=b2.rearrange("(a o) -> a o", a=1))
@@ -47,11 +50,17 @@ def tile_differentiablelogicmachine_pa_t_kernel(tc, x1, x2, W2, b2, out):
         )
         xs32 = {}
         for h in range(2):
+            xtiles = []
             for q in range(4):
                 xs = xpool.tile([P, 2, 8 * O], BF16)
-                for J in range(4):
-                    nc.sync.dma_start(out=xs[J:P:4, :, :], in_=xview[h, q, J])
+                xtiles.append(xs)
                 xs32[(h, q)] = xs[:].bitcast(F32)
+            for qh in range(2):
+                for vh in range(2):
+                    for q in (2 * qh, 2 * qh + 1):
+                        cols = slice(vh * 4 * O, (vh + 1) * 4 * O)
+                        for J in range(4):
+                            nc.sync.dma_start(out=xtiles[q][J:P:4, :, cols], in_=xview[h, q, J][:, :, cols])
         oview = out.rearrange("(h B) (I u) (J v) o -> h J (B I) u v o", h=2, B=8, I=4, u=8, J=4, v=8)
 
         ident = const.tile([P, P], F32)
@@ -81,9 +90,6 @@ def tile_differentiablelogicmachine_pa_t_kernel(tc, x1, x2, W2, b2, out):
             nc.scalar.copy(out=gwx[:, x, :, 0, :], in_=wraw[:, 2 * x, :, :].rearrange("p e o -> p o e"))
         waq = const.tile([P, O], U32, align_bytes=64)
         was = const.tile([P, O], U8, align_bytes=64)
-        nc.vector.quantize_mx(
-            out=waq[:].bitcast(FP8X4), scales=was[:], in_=gwa[:].rearrange("p o s e -> p (o s e)")
-        )
         wxq = const.tile([P, 2 * O], U32, align_bytes=64)
         wxs = const.tile([P, 2 * O], U8, align_bytes=64)
 
@@ -101,16 +107,20 @@ def tile_differentiablelogicmachine_pa_t_kernel(tc, x1, x2, W2, b2, out):
         zall = const.tile([P, 2, 8, O], F32)
         psz = {}
 
-        def x1_half(h):
+        for h in range(2):
             nc.vector.tensor_copy(
                 out=x1z[:, h, :, :, 0].rearrange("p (t r) m -> p t r m", t=2),
                 in_=x1t[:].rearrange("p r (h m t) -> p h t r m", h=2, m=32, t=2)[:, h, :, :, :],
             )
+
+        def x1_quantise(h):
             nc.vector.quantize_mx(
                 out=q1c[:, h, :].bitcast(FP8X4),
                 scales=q1s[:, h, :],
                 in_=x1z[:, h, :, :, :].rearrange("p t m w -> p (t m w)").bitcast(BF16),
             )
+
+        def x1_repeat(h):
             nc.vector.tensor_copy(
                 out=scj[:, h, :, :].rearrange("p t (B I J) -> p (t B) I J", B=8, I=4, J=4).bitcast(I32),
                 in_=q1c[:, h, :].rearrange("p (g J) -> p g J", J=4).bitcast(I32).unsqueeze(2).to_broadcast([P, 64, 4, 4]),
@@ -120,46 +130,65 @@ def tile_differentiablelogicmachine_pa_t_kernel(tc, x1, x2, W2, b2, out):
                 in_=q1s[:, h, :].bitcast(I32).unsqueeze(2).to_broadcast([P, 64, 4]),
             )
 
-        def unit_quantise(j):
+        gxs = {}
+
+        def unit_copy(j):
             h, t0 = j // 2, 4 * (j % 2)
             gx = upool.tile([P, 4, 32, 4, 2], F32, align_bytes=64)
             nc.vector.tensor_copy(
                 out=gx[:], in_=x1z[:, h, t0 : t0 + 4, :, :].unsqueeze(3).to_broadcast([P, 4, 32, 4, 2])
             )
+            gxs[j] = gx
+
+        def unit_quantise(j):
+            h, t0 = j // 2, 4 * (j % 2)
             nc.vector.quantize_mx(
                 out=sci[:, h, t0 : t0 + 4, :].rearrange("p t c -> p (t c)").bitcast(FP8X4),
                 scales=ssi[:, h, t0 : t0 + 4, :].rearrange("p t c -> p (t c)"),
-                in_=gx[:].rearrange("p t m J w -> p (t m J w)").bitcast(BF16),
+                in_=gxs[j][:].rearrange("p t m J w -> p (t m J w)").bitcast(BF16),
             )
 
-        def unit_matmul(j):
+        def unit_matmul(j, i):
             h, t0 = j // 2, 4 * (j % 2)
-            for i in range(2):
-                pz = psum_o.tile([P, 2 * O], F32, name="ps")
-                for tt in range(2):
-                    t = t0 + 2 * i + tt
-                    nc.tensor.matmul_mx(
-                        out=pz[:, tt * O : (tt + 1) * O],
-                        lhsT=sci[:, h, t, :].bitcast(FP8X4),
-                        lhsT_scale=ssi[:, h, t, :],
-                        rhs=wxq[:, 0:O].bitcast(FP8X4),
-                        rhs_scale=wxs[:, 0:O],
-                        start=True,
-                        stop=True,
-                    )
-                psz[(j, i)] = pz
-
-        def unit_exit(j):
-            h, t0 = j // 2, 4 * (j % 2)
-            for i in range(2):
-                nc.vector.tensor_tensor(
-                    out=zall[:, h, t0 + 2 * i : t0 + 2 * i + 2, :],
-                    in0=psz[(j, i)][:].rearrange("p (t o) -> p t o", t=2),
-                    in1=bias[:].unsqueeze(1).to_broadcast([P, 2, O]),
-                    op=ADD,
+            pz = psum_o.tile([P, 2 * O], F32, name="ps")
+            for tt in range(2):
+                t = t0 + 2 * i + tt
+                nc.tensor.matmul_mx(
+                    out=pz[:, tt * O : (tt + 1) * O],
+                    lhsT=sci[:, h, t, :].bitcast(FP8X4),
+                    lhsT_scale=ssi[:, h, t, :],
+                    rhs=wxq[:, 0:O].bitcast(FP8X4),
+                    rhs_scale=wxs[:, 0:O],
+                    start=True,
+                    stop=True,
                 )
+            psz[(j, i)] = pz
 
-        x1_half(0)
+        def unit_exit(j, i):
+            h, t0 = j // 2, 4 * (j % 2)
+            nc.vector.tensor_tensor(
+                out=zall[:, h, t0 + 2 * i : t0 + 2 * i + 2, :],
+                in0=psz[(j, i)][:].rearrange("p (t o) -> p t o", t=2),
+                in1=bias[:].unsqueeze(1).to_broadcast([P, 2, O]),
+                op=ADD,
+            )
+
+        def unit_pieces(j):
+            return [
+                lambda: unit_copy(j),
+                lambda: unit_quantise(j),
+                lambda: unit_matmul(j, 0),
+                lambda: (unit_exit(j, 0), unit_matmul(j, 1)),
+                lambda: unit_exit(j, 1),
+            ]
+
+        x1_quantise(0)
+        x1_repeat(0)
+        unit_copy(0)
+        unit_quantise(0)
+        nc.vector.quantize_mx(
+            out=waq[:].bitcast(FP8X4), scales=was[:], in_=gwa[:].rearrange("p o s e -> p (o s e)")
+        )
         nc.vector.quantize_mx(
             out=wxq[:].bitcast(FP8X4), scales=wxs[:], in_=gwx[:].rearrange("p x o s e -> p (x o s e)")
         )
@@ -198,9 +227,11 @@ def tile_differentiablelogicmachine_pa_t_kernel(tc, x1, x2, W2, b2, out):
         def st_exit(g):
             gt = gpool.tile([P, 2, 2, P, 2], F32, align_bytes=64)
             for i in range(2):
-                nc.scalar.copy(
-                    out=gt[:, i, :, :, :], in_=xts[(g, i)][:].rearrange("p (s w) c -> p s c w", w=2)
-                )
+                src = xts[(g, i)][:].rearrange("p (s w) c -> p s c w", w=2)
+                if i == 1 and g >= XG0 and g % XM == 0:
+                    nc.vector.tensor_copy(out=gt[:, i, :, :, :], in_=src)
+                else:
+                    nc.scalar.copy(out=gt[:, i, :, :, :], in_=src)
             gts[g] = gt
 
         def st_quantise(g):
@@ -263,23 +294,24 @@ def tile_differentiablelogicmachine_pa_t_kernel(tc, x1, x2, W2, b2, out):
                         in_=obuf[J:P:4, 2 * A : 2 * A + 2, 2 * C : 2 * C + 2, :],
                     )
 
+        background = unit_pieces(1) + [lambda: x1_quantise(1), lambda: x1_repeat(1)] + unit_pieces(2) + unit_pieces(3)
         for n in range(n_groups + 5):
             if 0 <= n - 5 < n_groups:
                 st_sigmoid(n - 5)
             if 0 <= n - 4 < n_groups:
                 st_add(n - 4)
-            if 0 <= n - 2 < 4:
-                unit_exit(n - 2)
             if 0 <= n - 3 < n_groups:
                 st_matmul(n - 3)
-            if 0 <= n - 1 < 4:
-                unit_matmul(n - 1)
+            if n == 2:
+                unit_matmul(0, 0)
+                unit_matmul(0, 1)
             if 0 <= n - 2 < n_groups:
                 st_quantise(n - 2)
-            if n == 1:
-                x1_half(1)
-            if n < 4:
-                unit_quantise(n)
+            if n == 3:
+                unit_exit(0, 0)
+                unit_exit(0, 1)
+            if 0 <= n - BG0 < len(background):
+                background[n - BG0]()
             if 0 <= n - 1 < n_groups:
                 st_exit(n - 1)
             if n < n_groups:

@@ -14,10 +14,15 @@ SIGMOID = mybir.ActivationFunctionType.Sigmoid
 
 P = 128
 O = 256
-BG0 = 3
-XG0 = 24
-XM = 2
 FLOPS = 2 * 16 * 32 * 32 * 1024 * 256
+
+EXIT = 1
+QUANTISE = 2
+MATMUL = 3
+BIAS_ADD = 4
+SIGMOID_STORE = 5
+FIRST_PIECE = 3
+VECTOR_HELPS_FROM = 24
 
 
 def block_groups(A, C):
@@ -38,281 +43,292 @@ def tile_differentiablelogicmachine_pa_t_kernel(tc, x1, x2, W2, b2, out):
         psum_o = ctx.enter_context(tc.psum_pool(name="psum_o", bufs=4))
         ctx.enter_context(tc.manual_schedule())
 
-        x1s = const.tile([P, 4, O], BF16)
-        nc.sync.dma_start(out=x1s[:], in_=x1.rearrange("b (q r) c -> (b q) r c", r=4))
-        wraw = const.tile([P, 4, 2, O], BF16)
-        nc.sync.dma_start(out=wraw[:], in_=W2.rearrange("(k p e) o -> p k e o", k=4, p=P, e=2))
-        brow = const.tile([P, O], BF16)
-        nc.vector.memset(brow[:], 0.0)
-        nc.sync.dma_start(out=brow[0:1, :], in_=b2.rearrange("(a o) -> a o", a=1))
-        xview = x2.rearrange(
-            "(h B) (I q e) (J v) c -> h q J (B I) e (v c)", h=2, B=8, I=4, q=4, e=2, J=4, v=8
+        x1_rows = const.tile([P, 4, O], BF16)
+        nc.sync.dma_start(out=x1_rows[:], in_=x1.rearrange("b (q r) c -> (b q) r c", r=4))
+        w_rows = const.tile([P, 4, 2, O], BF16)
+        nc.sync.dma_start(out=w_rows[:], in_=W2.rearrange("(k p e) o -> p k e o", k=4, p=P, e=2))
+        bias_row = const.tile([P, O], BF16)
+        nc.vector.memset(bias_row[:], 0.0)
+        nc.sync.dma_start(out=bias_row[0:1, :], in_=b2.rearrange("(a o) -> a o", a=1))
+        x2_view = x2.rearrange(
+            "(h B) (I q e) (J c) k -> h q J (B I) e (c k)", h=2, B=8, I=4, q=4, e=2, J=4, c=8
         )
-        xs32 = {}
+        x2_words = {}
         for h in range(2):
-            xtiles = []
+            x2_tiles = []
             for q in range(4):
-                xs = xpool.tile([P, 2, 8 * O], BF16)
-                xtiles.append(xs)
-                xs32[(h, q)] = xs[:].bitcast(F32)
-            for qh in range(2):
-                for vh in range(2):
-                    for q in (2 * qh, 2 * qh + 1):
-                        cols = slice(vh * 4 * O, (vh + 1) * 4 * O)
+                x2_tile = xpool.tile([P, 2, 8 * O], BF16)
+                x2_tiles.append(x2_tile)
+                x2_words[(h, q)] = x2_tile[:].bitcast(F32)
+            for q_half in range(2):
+                for c_half in range(2):
+                    cut = slice(c_half * 4 * O, (c_half + 1) * 4 * O)
+                    for q in (2 * q_half, 2 * q_half + 1):
                         for J in range(4):
-                            nc.sync.dma_start(out=xtiles[q][J:P:4, :, cols], in_=xview[h, q, J][:, :, cols])
-        oview = out.rearrange("(h B) (I u) (J v) o -> h J (B I) u v o", h=2, B=8, I=4, u=8, J=4, v=8)
+                            nc.sync.dma_start(out=x2_tiles[q][J:P:4, :, cut], in_=x2_view[h, q, J][:, :, cut])
+        out_view = out.rearrange("(h B) (I a) (J c) o -> h J (B I) a c o", h=2, B=8, I=4, a=8, J=4, c=8)
 
         ident = const.tile([P, P], F32)
         make_identity(nc, ident[:])
         ones = const.tile([P, P], BF16)
         nc.vector.memset(ones[:], 1.0)
-        warm = const.tile([P, 1], F32)
-        nc.vector.memset(warm[:], 0.0)
-        warm2 = const.tile([P, 1], F32)
-        nc.scalar.activation(out=warm2[:], in_=warm[:], func=SIGMOID)
-        gwx = const.tile([P, 2, O, 2, 2], BF16, align_bytes=64)
-        nc.vector.memset(gwx[:], 0.0)
-        x1z = const.tile([P, 2, 8, 32, 2], F32, align_bytes=64)
-        nc.vector.memset(x1z[:], 0.0)
-        q1c = const.tile([P, 2, 256], U32, align_bytes=64)
-        q1s = const.tile([P, 2, 256], U8, align_bytes=64)
-        nc.vector.memset(q1s[:].bitcast(I32), 0)
-        perm = const.tile([P, P], F32)
+        warm_in = const.tile([P, 1], F32)
+        nc.vector.memset(warm_in[:], 0.0)
+        warm_out = const.tile([P, 1], F32)
+        nc.scalar.activation(out=warm_out[:], in_=warm_in[:], func=SIGMOID)
+        w1_grouped = const.tile([P, 2, O, 2, 2], BF16, align_bytes=64)
+        nc.vector.memset(w1_grouped[:], 0.0)
+        x1_words = const.tile([P, 2, 8, 32, 2], F32, align_bytes=64)
+        nc.vector.memset(x1_words[:], 0.0)
+        x1_codes = const.tile([P, 2, 256], U32, align_bytes=64)
+        x1_scales = const.tile([P, 2, 256], U8, align_bytes=64)
+        nc.vector.memset(x1_scales[:].bitcast(I32), 0)
+        swap = const.tile([P, P], F32)
         nc.vector.tensor_copy(
-            out=perm[:].rearrange("p (B I J) -> p B I J", B=8, I=4, J=4),
+            out=swap[:].rearrange("p (B I J) -> p B I J", B=8, I=4, J=4),
             in_=ident[:].rearrange("p (B J I) -> p B I J", B=8, J=4, I=4),
         )
 
-        gwa = const.tile([P, O, 2, 2], BF16, align_bytes=64)
-        nc.scalar.copy(out=gwa[:], in_=wraw[:, 1:4:2, :, :].rearrange("p s e o -> p o s e"))
+        w2_grouped = const.tile([P, O, 2, 2], BF16, align_bytes=64)
+        nc.scalar.copy(out=w2_grouped[:], in_=w_rows[:, 1:4:2, :, :].rearrange("p s e o -> p o s e"))
         for x in range(2):
-            nc.scalar.copy(out=gwx[:, x, :, 0, :], in_=wraw[:, 2 * x, :, :].rearrange("p e o -> p o e"))
-        waq = const.tile([P, O], U32, align_bytes=64)
-        was = const.tile([P, O], U8, align_bytes=64)
-        wxq = const.tile([P, 2 * O], U32, align_bytes=64)
-        wxs = const.tile([P, 2 * O], U8, align_bytes=64)
+            nc.scalar.copy(out=w1_grouped[:, x, :, 0, :], in_=w_rows[:, 2 * x, :, :].rearrange("p e o -> p o e"))
+        w2_codes = const.tile([P, O], U32, align_bytes=64)
+        w2_scales = const.tile([P, O], U8, align_bytes=64)
+        w1_codes = const.tile([P, 2 * O], U32, align_bytes=64)
+        w1_scales = const.tile([P, 2 * O], U8, align_bytes=64)
 
-        x1t = psum_t.tile([P, 4, P], F32, name="xt")
+        x1_t = psum_t.tile([P, 4, P], F32, name="xt")
         for r in range(4):
-            nc.tensor.transpose(out=x1t[:, r, :], in_=x1s[:, r, :].bitcast(F32), identity=ident[:])
-        psb = psum_o.tile([P, 2 * O], F32, name="ps")
-        nc.tensor.matmul(out=psb[:, 0:O], lhsT=ones[:], rhs=brow[:], start=True, stop=True)
-        bias = const.tile([P, O], F32)
-
-        scj = const.tile([P, 2, 8, P], U32, align_bytes=64)
-        ssj = const.tile([P, 2, 8, P], U8, align_bytes=64)
-        sci = const.tile([P, 2, 8, P], U32, align_bytes=64)
-        ssi = const.tile([P, 2, 8, P], U8, align_bytes=64)
-        zall = const.tile([P, 2, 8, O], F32)
-        psz = {}
-
+            nc.tensor.transpose(out=x1_t[:, r, :], in_=x1_rows[:, r, :].bitcast(F32), identity=ident[:])
         for h in range(2):
             nc.vector.tensor_copy(
-                out=x1z[:, h, :, :, 0].rearrange("p (t r) m -> p t r m", t=2),
-                in_=x1t[:].rearrange("p r (h m t) -> p h t r m", h=2, m=32, t=2)[:, h, :, :, :],
+                out=x1_words[:, h, :, :, 0].rearrange("p (t r) m -> p t r m", t=2),
+                in_=x1_t[:].rearrange("p r (h m t) -> p h t r m", h=2, m=32, t=2)[:, h, :, :, :],
             )
+        bias_psum = psum_o.tile([P, 2 * O], F32, name="ps")
+        nc.tensor.matmul(out=bias_psum[:, 0:O], lhsT=ones[:], rhs=bias_row[:], start=True, stop=True)
+        bias = const.tile([P, O], F32)
+
+        by_j_codes = const.tile([P, 2, 8, P], U32, align_bytes=64)
+        by_j_scales = const.tile([P, 2, 8, P], U8, align_bytes=64)
+        by_i_codes = const.tile([P, 2, 8, P], U32, align_bytes=64)
+        by_i_scales = const.tile([P, 2, 8, P], U8, align_bytes=64)
+        row_term = const.tile([P, 2, 8, O], F32)
+        by_i_grouped, row_psum = {}, {}
 
         def x1_quantise(h):
             nc.vector.quantize_mx(
-                out=q1c[:, h, :].bitcast(FP8X4),
-                scales=q1s[:, h, :],
-                in_=x1z[:, h, :, :, :].rearrange("p t m w -> p (t m w)").bitcast(BF16),
+                out=x1_codes[:, h, :].bitcast(FP8X4),
+                scales=x1_scales[:, h, :],
+                in_=x1_words[:, h, :, :, :].rearrange("p a m w -> p (a m w)").bitcast(BF16),
             )
 
-        def x1_repeat(h):
+        def x1_repeat_over_i(h):
             nc.vector.tensor_copy(
-                out=scj[:, h, :, :].rearrange("p t (B I J) -> p (t B) I J", B=8, I=4, J=4).bitcast(I32),
-                in_=q1c[:, h, :].rearrange("p (g J) -> p g J", J=4).bitcast(I32).unsqueeze(2).to_broadcast([P, 64, 4, 4]),
+                out=by_j_codes[:, h, :, :].rearrange("p a (B I J) -> p (a B) I J", B=8, I=4, J=4).bitcast(I32),
+                in_=x1_codes[:, h, :]
+                .rearrange("p (g J) -> p g J", J=4)
+                .bitcast(I32)
+                .unsqueeze(2)
+                .to_broadcast([P, 64, 4, 4]),
             )
             nc.vector.tensor_copy(
-                out=ssj[:, h, :, :].rearrange("p t c -> p (t c)").bitcast(I32).rearrange("p (g I) -> p g I", I=4),
-                in_=q1s[:, h, :].bitcast(I32).unsqueeze(2).to_broadcast([P, 64, 4]),
+                out=by_j_scales[:, h, :, :]
+                .rearrange("p a n -> p (a n)")
+                .bitcast(I32)
+                .rearrange("p (g I) -> p g I", I=4),
+                in_=x1_scales[:, h, :].bitcast(I32).unsqueeze(2).to_broadcast([P, 64, 4]),
             )
 
-        gxs = {}
-
-        def unit_copy(j):
-            h, t0 = j // 2, 4 * (j % 2)
-            gx = upool.tile([P, 4, 32, 4, 2], F32, align_bytes=64)
+        def unit_repeat_over_j(u):
+            h, a0 = u // 2, 4 * (u % 2)
+            grouped = upool.tile([P, 4, 32, 4, 2], F32, align_bytes=64)
             nc.vector.tensor_copy(
-                out=gx[:], in_=x1z[:, h, t0 : t0 + 4, :, :].unsqueeze(3).to_broadcast([P, 4, 32, 4, 2])
+                out=grouped[:], in_=x1_words[:, h, a0 : a0 + 4, :, :].unsqueeze(3).to_broadcast([P, 4, 32, 4, 2])
             )
-            gxs[j] = gx
+            by_i_grouped[u] = grouped
 
-        def unit_quantise(j):
-            h, t0 = j // 2, 4 * (j % 2)
+        def unit_quantise(u):
+            h, a0 = u // 2, 4 * (u % 2)
             nc.vector.quantize_mx(
-                out=sci[:, h, t0 : t0 + 4, :].rearrange("p t c -> p (t c)").bitcast(FP8X4),
-                scales=ssi[:, h, t0 : t0 + 4, :].rearrange("p t c -> p (t c)"),
-                in_=gxs[j][:].rearrange("p t m J w -> p (t m J w)").bitcast(BF16),
+                out=by_i_codes[:, h, a0 : a0 + 4, :].rearrange("p a n -> p (a n)").bitcast(FP8X4),
+                scales=by_i_scales[:, h, a0 : a0 + 4, :].rearrange("p a n -> p (a n)"),
+                in_=by_i_grouped[u][:].rearrange("p a m J w -> p (a m J w)").bitcast(BF16),
             )
 
-        def unit_matmul(j, i):
-            h, t0 = j // 2, 4 * (j % 2)
-            pz = psum_o.tile([P, 2 * O], F32, name="ps")
-            for tt in range(2):
-                t = t0 + 2 * i + tt
+        def unit_matmul(u, pair):
+            h, a0 = u // 2, 4 * (u % 2) + 2 * pair
+            ps = psum_o.tile([P, 2 * O], F32)
+            for s in range(2):
                 nc.tensor.matmul_mx(
-                    out=pz[:, tt * O : (tt + 1) * O],
-                    lhsT=sci[:, h, t, :].bitcast(FP8X4),
-                    lhsT_scale=ssi[:, h, t, :],
-                    rhs=wxq[:, 0:O].bitcast(FP8X4),
-                    rhs_scale=wxs[:, 0:O],
+                    out=ps[:, s * O : (s + 1) * O],
+                    lhsT=by_i_codes[:, h, a0 + s, :].bitcast(FP8X4),
+                    lhsT_scale=by_i_scales[:, h, a0 + s, :],
+                    rhs=w1_codes[:, 0:O].bitcast(FP8X4),
+                    rhs_scale=w1_scales[:, 0:O],
                     start=True,
                     stop=True,
                 )
-            psz[(j, i)] = pz
+            row_psum[(u, pair)] = ps
 
-        def unit_exit(j, i):
-            h, t0 = j // 2, 4 * (j % 2)
+        def unit_add_bias(u, pair):
+            h, a0 = u // 2, 4 * (u % 2) + 2 * pair
             nc.vector.tensor_tensor(
-                out=zall[:, h, t0 + 2 * i : t0 + 2 * i + 2, :],
-                in0=psz[(j, i)][:].rearrange("p (t o) -> p t o", t=2),
+                out=row_term[:, h, a0 : a0 + 2, :],
+                in0=row_psum[(u, pair)][:].rearrange("p (s o) -> p s o", s=2),
                 in1=bias[:].unsqueeze(1).to_broadcast([P, 2, O]),
                 op=ADD,
             )
 
-        def unit_pieces(j):
+        def unit_pieces(u):
             return [
-                lambda: unit_copy(j),
-                lambda: unit_quantise(j),
-                lambda: unit_matmul(j, 0),
-                lambda: (unit_exit(j, 0), unit_matmul(j, 1)),
-                lambda: unit_exit(j, 1),
+                lambda: unit_repeat_over_j(u),
+                lambda: unit_quantise(u),
+                lambda: unit_matmul(u, 0),
+                lambda: (unit_add_bias(u, 0), unit_matmul(u, 1)),
+                lambda: unit_add_bias(u, 1),
             ]
 
         x1_quantise(0)
-        x1_repeat(0)
-        unit_copy(0)
+        x1_repeat_over_i(0)
+        unit_repeat_over_j(0)
         unit_quantise(0)
         nc.vector.quantize_mx(
-            out=waq[:].bitcast(FP8X4), scales=was[:], in_=gwa[:].rearrange("p o s e -> p (o s e)")
+            out=w2_codes[:].bitcast(FP8X4),
+            scales=w2_scales[:],
+            in_=w2_grouped[:].rearrange("p o s e -> p (o s e)"),
         )
         nc.vector.quantize_mx(
-            out=wxq[:].bitcast(FP8X4), scales=wxs[:], in_=gwx[:].rearrange("p x o s e -> p (x o s e)")
+            out=w1_codes[:].bitcast(FP8X4),
+            scales=w1_scales[:],
+            in_=w1_grouped[:].rearrange("p x o s e -> p (x o s e)"),
         )
-        nc.vector.tensor_copy(out=bias[:], in_=psb[:, 0:O])
+        nc.vector.tensor_copy(out=bias[:], in_=bias_psum[:, 0:O])
+        pieces = (
+            unit_pieces(1) + [lambda: x1_quantise(1), lambda: x1_repeat_over_i(1)] + unit_pieces(2) + unit_pieces(3)
+        )
 
         groups = []
         for h in range(2):
-            for C in range(4):
-                for A in range(C + 1):
-                    gs = block_groups(A, C)
-                    for i in range(len(gs)):
-                        last = i == len(gs) - 1
-                        groups.append((h, gs[i], sorted(set([(A, C), (C, A)])) if last else []))
+            blocks = [(A, C) for C in range(4) for A in range(C + 1)]
+            if h == 1:
+                blocks = [b for b in blocks if b[0] != b[1]] + [b for b in blocks if b[0] == b[1]]
+            for A, C in blocks:
+                of_block = block_groups(A, C)
+                for rounds in of_block[:-1]:
+                    groups.append((h, rounds, []))
+                groups.append((h, of_block[-1], sorted(set([(A, C), (C, A)]))))
         n_groups = len(groups)
-        obuf = const.tile([P, 8, 8, O], F32)
-        oflat = obuf[:].rearrange("p a c o -> p (a c) o")
-        xts, gts, qcs, qss, pss = {}, {}, {}, {}, {}
+        result = const.tile([P, 8, 8, O], F32)
+        result_slots = result[:].rearrange("p a c o -> p (a c) o")
+        transposed, grouped_of, codes_of, scales_of, sums = {}, {}, {}, {}, {}
 
-        def grp(h, a, c):
-            return xs32[(h, a // 2)][:, a % 2, c * P : (c + 1) * P]
+        def x2_slot(h, a, c):
+            return x2_words[(h, a // 2)][:, a % 2, c * P : (c + 1) * P]
 
-        def oslots(pair):
-            i0, i1 = 8 * pair[0][0] + pair[0][1], 8 * pair[1][0] + pair[1][1]
-            return oflat[:, i0 : i1 + 1 : i1 - i0, :]
+        def slots_of(one_round):
+            first, second = 8 * one_round[0][0] + one_round[0][1], 8 * one_round[1][0] + one_round[1][1]
+            return result_slots[:, first : second + 1 : second - first, :]
 
-        def st_transpose(g):
-            h, rounds, stores = groups[g]
+        def transposes(g):
+            h, rounds, complete = groups[g]
             for i in range(2):
                 xt = psum_t.tile([P, 4, P], F32)
                 for s in range(2):
                     a, c = rounds[i][s]
-                    nc.tensor.transpose(out=xt[:, 2 * s, :], in_=grp(h, a, c), identity=ident[:])
-                    nc.tensor.transpose(out=xt[:, 2 * s + 1, :], in_=grp(h, c, a), identity=perm[:])
-                xts[(g, i)] = xt
+                    nc.tensor.transpose(out=xt[:, 2 * s, :], in_=x2_slot(h, a, c), identity=ident[:])
+                    nc.tensor.transpose(out=xt[:, 2 * s + 1, :], in_=x2_slot(h, c, a), identity=swap[:])
+                transposed[(g, i)] = xt
 
-        def st_exit(g):
-            gt = gpool.tile([P, 2, 2, P, 2], F32, align_bytes=64)
+        def exits(g):
+            grouped = gpool.tile([P, 2, 2, P, 2], F32, align_bytes=64)
             for i in range(2):
-                src = xts[(g, i)][:].rearrange("p (s w) c -> p s c w", w=2)
-                if i == 1 and g >= XG0 and g % XM == 0:
-                    nc.vector.tensor_copy(out=gt[:, i, :, :, :], in_=src)
+                words = transposed[(g, i)][:].rearrange("p (s w) n -> p s n w", w=2)
+                if i == 1 and g >= VECTOR_HELPS_FROM and g % 2 == 0:
+                    nc.vector.tensor_copy(out=grouped[:, i, :, :, :], in_=words)
                 else:
-                    nc.scalar.copy(out=gt[:, i, :, :, :], in_=src)
-            gts[g] = gt
+                    nc.scalar.copy(out=grouped[:, i, :, :, :], in_=words)
+            grouped_of[g] = grouped
 
-        def st_quantise(g):
-            qc = gpool.tile([P, 4 * P], U32, align_bytes=64)
-            qs = gpool.tile([P, 4 * P], U8, align_bytes=64)
+        def quantise(g):
+            codes = gpool.tile([P, 4 * P], U32, align_bytes=64)
+            scales = gpool.tile([P, 4 * P], U8, align_bytes=64)
             nc.vector.quantize_mx(
-                out=qc[:].bitcast(FP8X4),
-                scales=qs[:],
-                in_=gts[g][:].rearrange("p i s c w -> p (i s c w)").bitcast(BF16),
+                out=codes[:].bitcast(FP8X4),
+                scales=scales[:],
+                in_=grouped_of[g][:].rearrange("p i s n w -> p (i s n w)").bitcast(BF16),
             )
-            qcs[g] = qc
-            qss[g] = qs
+            codes_of[g] = codes
+            scales_of[g] = scales
 
-        def st_matmul(g):
-            h, rounds, stores = groups[g]
+        def matmuls(g):
+            h, rounds, complete = groups[g]
             for i in range(2):
                 ps = psum_o.tile([P, 2 * O], F32)
                 for s in range(2):
                     c = rounds[i][s][1]
-                    col = (2 * i + s) * P
+                    columns = slice((2 * i + s) * P, (2 * i + s + 1) * P)
                     nc.tensor.matmul_mx(
                         out=ps[:, s * O : (s + 1) * O],
-                        lhsT=qcs[g][:, col : col + P].bitcast(FP8X4),
-                        lhsT_scale=qss[g][:, col : col + P],
-                        rhs=waq[:].bitcast(FP8X4),
-                        rhs_scale=was[:],
+                        lhsT=codes_of[g][:, columns].bitcast(FP8X4),
+                        lhsT_scale=scales_of[g][:, columns],
+                        rhs=w2_codes[:].bitcast(FP8X4),
+                        rhs_scale=w2_scales[:],
                         start=True,
                         stop=False,
                     )
                     nc.tensor.matmul_mx(
                         out=ps[:, s * O : (s + 1) * O],
-                        lhsT=scj[:, h, c, :].bitcast(FP8X4),
-                        lhsT_scale=ssj[:, h, c, :],
-                        rhs=wxq[:, O : 2 * O].bitcast(FP8X4),
-                        rhs_scale=wxs[:, O : 2 * O],
+                        lhsT=by_j_codes[:, h, c, :].bitcast(FP8X4),
+                        lhsT_scale=by_j_scales[:, h, c, :],
+                        rhs=w1_codes[:, O : 2 * O].bitcast(FP8X4),
+                        rhs_scale=w1_scales[:, O : 2 * O],
                         start=False,
                         stop=True,
                     )
-                pss[(g, i)] = ps
+                sums[(g, i)] = ps
 
-        def st_add(g):
-            h, rounds, stores = groups[g]
+        def add_row_terms(g):
+            h, rounds, complete = groups[g]
             for i in range(2):
-                a0, a1 = rounds[i][0][0], rounds[i][1][0]
+                first, second = rounds[i][0][0], rounds[i][1][0]
                 nc.vector.tensor_tensor(
-                    out=oslots(rounds[i]),
-                    in0=pss[(g, i)][:].rearrange("p (s o) -> p s o", s=2),
-                    in1=zall[:, h, a0 : a1 + 1 : a1 - a0, :],
+                    out=slots_of(rounds[i]),
+                    in0=sums[(g, i)][:].rearrange("p (s o) -> p s o", s=2),
+                    in1=row_term[:, h, first : second + 1 : second - first, :],
                     op=ADD,
                 )
 
-        def st_sigmoid(g):
-            h, rounds, stores = groups[g]
+        def sigmoids_and_stores(g):
+            h, rounds, complete = groups[g]
             for i in range(2):
-                nc.scalar.activation(out=oslots(rounds[i]), in_=oslots(rounds[i]), func=SIGMOID)
-            for A, C in stores:
+                nc.scalar.activation(out=slots_of(rounds[i]), in_=slots_of(rounds[i]), func=SIGMOID)
+            for A, C in complete:
                 for J in range(4):
                     nc.sync.dma_start(
-                        out=oview[h, J, :, 2 * A : 2 * A + 2, 2 * C : 2 * C + 2, :],
-                        in_=obuf[J:P:4, 2 * A : 2 * A + 2, 2 * C : 2 * C + 2, :],
+                        out=out_view[h, J, :, 2 * A : 2 * A + 2, 2 * C : 2 * C + 2, :],
+                        in_=result[J:P:4, 2 * A : 2 * A + 2, 2 * C : 2 * C + 2, :],
                     )
 
-        background = unit_pieces(1) + [lambda: x1_quantise(1), lambda: x1_repeat(1)] + unit_pieces(2) + unit_pieces(3)
-        for n in range(n_groups + 5):
-            if 0 <= n - 5 < n_groups:
-                st_sigmoid(n - 5)
-            if 0 <= n - 4 < n_groups:
-                st_add(n - 4)
-            if 0 <= n - 3 < n_groups:
-                st_matmul(n - 3)
-            if n == 2:
+        for n in range(n_groups + SIGMOID_STORE):
+            if 0 <= n - SIGMOID_STORE < n_groups:
+                sigmoids_and_stores(n - SIGMOID_STORE)
+            if 0 <= n - BIAS_ADD < n_groups:
+                add_row_terms(n - BIAS_ADD)
+            if 0 <= n - MATMUL < n_groups:
+                matmuls(n - MATMUL)
+            if n == MATMUL - 1:
                 unit_matmul(0, 0)
                 unit_matmul(0, 1)
-            if 0 <= n - 2 < n_groups:
-                st_quantise(n - 2)
-            if n == 3:
-                unit_exit(0, 0)
-                unit_exit(0, 1)
-            if 0 <= n - BG0 < len(background):
-                background[n - BG0]()
-            if 0 <= n - 1 < n_groups:
-                st_exit(n - 1)
+            if 0 <= n - QUANTISE < n_groups:
+                quantise(n - QUANTISE)
+            if n == BIAS_ADD - 1:
+                unit_add_bias(0, 0)
+                unit_add_bias(0, 1)
+            if 0 <= n - FIRST_PIECE < len(pieces):
+                pieces[n - FIRST_PIECE]()
+            if 0 <= n - EXIT < n_groups:
+                exits(n - EXIT)
             if n < n_groups:
-                st_transpose(n)
+                transposes(n)

@@ -66,7 +66,7 @@ def tile_differentiablelogicmachine_pa_t_kernel(tc, x1, x2, W2, b2, out):
                     for q in (2 * q_half, 2 * q_half + 1):
                         for J in range(4):
                             nc.sync.dma_start(out=x2_tiles[q][J:P:4, :, cut], in_=x2_view[h, q, J][:, :, cut])
-        out_view = out.rearrange("(h B) (I a) (J c) o -> h J (B I) a c o", h=2, B=8, I=4, a=8, J=4, c=8)
+        out_rows = out.rearrange("(h B) (I a) (J c) o -> h a (B I) J (c o)", h=2, B=8, I=4, a=8, J=4, c=8)
 
         ident = const.tile([P, P], F32)
         make_identity(nc, ident[:])
@@ -305,10 +305,10 @@ def tile_differentiablelogicmachine_pa_t_kernel(tc, x1, x2, W2, b2, out):
             for i in range(2):
                 nc.scalar.activation(out=slots_of(rounds[i]), in_=slots_of(rounds[i]), func=SIGMOID)
             for A, C in complete:
-                for J in range(4):
+                for a in (2 * A, 2 * A + 1):
                     nc.sync.dma_start(
-                        out=out_view[h, J, :, 2 * A : 2 * A + 2, 2 * C : 2 * C + 2, :],
-                        in_=result[J:P:4, 2 * A : 2 * A + 2, 2 * C : 2 * C + 2, :],
+                        out=out_rows[h, a, :, :, 2 * C * O : (2 * C + 2) * O],
+                        in_=result[:, a, 2 * C : 2 * C + 2, :].rearrange("p c o -> p (c o)"),
                     )
 
         for n in range(n_groups + SIGMOID_STORE):

@@ -21,314 +21,384 @@ QUANTISE = 2
 MATMUL = 3
 BIAS_ADD = 4
 SIGMOID_STORE = 5
-FIRST_PIECE = 3
-VECTOR_HELPS_FROM = 24
+VECTOR_HELPS_FROM = 18
+VECTOR_HELPS_EVERY = 4
+RESULT_SLOTS = 16
 
 
-def block_groups(A, C):
-    if A == C:
-        a = 2 * A
-        return [[((a, a), (a + 1, a + 1)), ((a, a + 1), (a + 1, a))]]
-    return [[((a, c), (c, a)) for c in (2 * C, 2 * C + 1)] for a in (2 * A, 2 * A + 1)]
+def make_groups():
+    groups = []
+    for C in (3, 2, 1, 0):
+        for gamma in range(2):
+            c0 = 8 * gamma + 2 * C
+            c1 = c0 + 1
+            split = C if C >= 2 else 0
+            for a_lo, a_hi, last in ((0, split, False), (split, 2 * C, True)):
+                n = a_hi - a_lo
+                if n == 0 and not last:
+                    continue
+                base = 2 * n + (3 if last else 0)
+                chunk = []
+                for t in range(n):
+                    a = a_lo + t
+                    chunk.append(
+                        dict(
+                            first=False,
+                            stationaries=[(a, c0), (a, c1)],
+                            banks=[
+                                dict(wide=True, parts=[(0, c0)], a=a, slots=slice(2 * t, base + t + 1, base - t)),
+                                dict(
+                                    wide=True,
+                                    parts=[(1, c1)],
+                                    a=a,
+                                    slots=slice(2 * t + 1, base + n + t + 1, base + n - t - 1),
+                                ),
+                            ],
+                            sigmoids=[slice(2 * t, 2 * t + 2, 1), slice(base + t, base + n + t + 1, n)],
+                            stores=[("n", a, c0, c1 + 1, 2 * t)],
+                        )
+                    )
+                if last:
+                    d0 = 2 * C
+                    d1 = d0 + 1
+                    chunk.append(
+                        dict(
+                            first=False,
+                            stationaries=[(d0, c0), (d1, c1), (d0, c1)],
+                            banks=[
+                                dict(
+                                    wide=True,
+                                    parts=[(2, c1)],
+                                    a=d0,
+                                    slots=slice(2 * n + 1, base + 2 * n + 1, base - 1),
+                                ),
+                                dict(wide=False, parts=[(0, c0), (1, c1)], a=d0, slots=slice(2 * n, 2 * n + 3, 2)),
+                            ],
+                            sigmoids=[slice(2 * n, 2 * n + 3, 1), slice(base + 2 * n, base + 2 * n + 1, 1)],
+                            stores=[("n", d0, c0, c1 + 1, 2 * n), ("n", d1, c1, c1 + 1, 2 * n + 2)],
+                        )
+                    )
+                if n > 0:
+                    chunk[-1]["stores"].append(("p", c0, a_lo, a_hi, base))
+                chunk[-1]["stores"].append(("p", c1, a_lo, a_hi + (1 if last else 0), base + n))
+                chunk[0]["first"] = True
+                groups.extend(chunk)
+    return groups
 
 
 def tile_differentiablelogicmachine_pa_t_kernel(tc, x1, x2, W2, b2, out):
     nc = tc.nc
     with ExitStack() as ctx:
         const = ctx.enter_context(tc.tile_pool(name="const", bufs=1))
-        xpool = ctx.enter_context(tc.tile_pool(name="xpool", bufs=8))
-        gpool = ctx.enter_context(tc.tile_pool(name="gpool", bufs=4))
+        gpool = ctx.enter_context(tc.tile_pool(name="gpool", bufs=6))
         upool = ctx.enter_context(tc.tile_pool(name="upool", bufs=2))
-        psum_t = ctx.enter_context(tc.psum_pool(name="psum_t", bufs=4))
+        rpool = ctx.enter_context(tc.tile_pool(name="rpool", bufs=4))
+        psum_t = ctx.enter_context(tc.psum_pool(name="psum_t", bufs=3))
         psum_o = ctx.enter_context(tc.psum_pool(name="psum_o", bufs=4))
+        psum_r = ctx.enter_context(tc.psum_pool(name="psum_r", bufs=1))
         ctx.enter_context(tc.manual_schedule())
 
         x1_rows = const.tile([P, 4, O], BF16)
         nc.sync.dma_start(out=x1_rows[:], in_=x1.rearrange("b (q r) c -> (b q) r c", r=4))
-        w_rows = const.tile([P, 4, 2, O], BF16)
-        nc.sync.dma_start(out=w_rows[:], in_=W2.rearrange("(k p e) o -> p k e o", k=4, p=P, e=2))
+        w_rows = const.tile([P, 5, 2, O], BF16)
+        w_view = W2.rearrange("(k p e) o -> p k e o", k=4, p=P, e=2)
+        nc.sync.dma_start(out=w_rows[:, 0:4, :, :], in_=w_view)
+        nc.sync.dma_start(out=w_rows[:, 4:5, :, :], in_=w_view[:, 1:2, :, :])
         bias_row = const.tile([P, O], BF16)
-        nc.vector.memset(bias_row[:], 0.0)
+        nc.gpsimd.memset(bias_row[:], 0.0)
         nc.sync.dma_start(out=bias_row[0:1, :], in_=b2.rearrange("(a o) -> a o", a=1))
-        x2_view = x2.rearrange(
-            "(h B) (I q e) (J c) k -> h q J (B I) e (c k)", h=2, B=8, I=4, q=4, e=2, J=4, c=8
-        )
-        x2_words = {}
-        for h in range(2):
-            x2_tiles = []
-            for q in range(4):
-                x2_tile = xpool.tile([P, 2, 8 * O], BF16)
-                x2_tiles.append(x2_tile)
-                x2_words[(h, q)] = x2_tile[:].bitcast(F32)
-            for q_half in range(2):
-                for c_half in range(2):
-                    cut = slice(c_half * 4 * O, (c_half + 1) * 4 * O)
-                    for q in (2 * q_half, 2 * q_half + 1):
-                        for J in range(4):
-                            nc.sync.dma_start(out=x2_tiles[q][J:P:4, :, cut], in_=x2_view[h, q, J][:, :, cut])
-        out_rows = out.rearrange("(h B) (I a) (J c) o -> h a (B I) J (c o)", h=2, B=8, I=4, a=8, J=4, c=8)
+
+        xn_words, xp_words = {}, {}
+        xn_view = x2.rearrange("b (I a) (J c) k -> a (b I) J (c k)", I=4, a=8, J=2, c=16)
+        xp_view = x2.rearrange("b (J c) (I a) k -> c J b I (a k)", J=2, c=16, I=4, a=8)
+        out_n = out.rearrange("b (I a) (J c) o -> a (b I) J (c o)", I=4, a=8, J=2, c=16)
+        out_p = out.rearrange("b (J c) (I a) o -> c J b I (a o)", J=2, c=16, I=4, a=8)
+
+        def load_xn(a, c_lo, c_hi):
+            xn = const.tile([P, (c_hi - c_lo) * O], BF16, name="xn_%d_%d" % (a, c_lo))
+            nc.sync.dma_start(out=xn[:], in_=xn_view[a, :, :, c_lo * O : c_hi * O])
+            for c in range(c_lo, c_hi):
+                xn_words[(a, c)] = xn[:, (c - c_lo) * O : (c - c_lo + 1) * O].bitcast(F32)
+
+        def load_xp(c, a_lo, a_hi):
+            xp = const.tile([P, (a_hi - a_lo) * O], BF16, name="xp_%d_%d" % (c, a_lo))
+            for J in range(2):
+                nc.sync.dma_start(out=xp[J:P:2, :], in_=xp_view[c, J, :, :, a_lo * O : a_hi * O])
+            for a in range(a_lo, a_hi):
+                xp_words[(a, c)] = xp[:, (a - a_lo) * O : (a - a_lo + 1) * O].bitcast(F32)
+
+        load_xp(6, 0, 3)
+        load_xp(7, 0, 3)
+        for a in range(3):
+            load_xn(a, 6, 8)
+        load_xp(6, 3, 7)
+        load_xp(7, 3, 8)
+        for a in range(3, 8):
+            load_xn(a, max(a, 6), 8)
+        load_xp(14, 0, 7)
+        load_xp(15, 0, 8)
+        for a in range(8):
+            load_xn(a, 8 + a, 16)
+        load_xp(4, 0, 5)
+        load_xp(5, 0, 6)
+        for a in range(6):
+            load_xn(a, a, 6)
+        for c in (12, 13, 2, 3, 10, 11, 0, 1, 8, 9):
+            load_xp(c, 0, c % 8 + 1)
 
         ident = const.tile([P, P], F32)
         make_identity(nc, ident[:])
         ones = const.tile([P, P], BF16)
-        nc.vector.memset(ones[:], 1.0)
+        nc.gpsimd.memset(ones[:], 1.0)
         warm_in = const.tile([P, 1], F32)
-        nc.vector.memset(warm_in[:], 0.0)
+        nc.gpsimd.memset(warm_in[:], 0.0)
         warm_out = const.tile([P, 1], F32)
         nc.scalar.activation(out=warm_out[:], in_=warm_in[:], func=SIGMOID)
         w1_grouped = const.tile([P, 2, O, 2, 2], BF16, align_bytes=64)
-        nc.vector.memset(w1_grouped[:], 0.0)
-        x1_words = const.tile([P, 2, 8, 32, 2], F32, align_bytes=64)
-        nc.vector.memset(x1_words[:], 0.0)
-        x1_codes = const.tile([P, 2, 256], U32, align_bytes=64)
-        x1_scales = const.tile([P, 2, 256], U8, align_bytes=64)
-        nc.vector.memset(x1_scales[:].bitcast(I32), 0)
-        swap = const.tile([P, P], F32)
-        nc.vector.tensor_copy(
-            out=swap[:].rearrange("p (B I J) -> p B I J", B=8, I=4, J=4),
-            in_=ident[:].rearrange("p (B J I) -> p B I J", B=8, J=4, I=4),
-        )
+        nc.gpsimd.memset(w1_grouped[:], 0.0)
+        x1_words = const.tile([P, 2, 4, 16, 8], F32)
+        nc.gpsimd.memset(x1_words[:, 1, :, :, :], 0.0)
 
-        w2_grouped = const.tile([P, O, 2, 2], BF16, align_bytes=64)
-        nc.scalar.copy(out=w2_grouped[:], in_=w_rows[:, 1:4:2, :, :].rearrange("p s e o -> p o s e"))
-        for x in range(2):
-            nc.scalar.copy(out=w1_grouped[:, x, :, 0, :], in_=w_rows[:, 2 * x, :, :].rearrange("p e o -> p o e"))
-        w2_codes = const.tile([P, O], U32, align_bytes=64)
-        w2_scales = const.tile([P, O], U8, align_bytes=64)
+        w2_grouped = const.tile([P, 2, O, 2, 2], BF16, align_bytes=64)
+        nc.scalar.copy(out=w2_grouped[:, 0, :, :, :], in_=w_rows[:, 1:4:2, :, :].rearrange("p s e o -> p o s e"))
+        nc.scalar.copy(out=w2_grouped[:, 1, :, :, :], in_=w_rows[:, 3:5, :, :].rearrange("p s e o -> p o s e"))
+        w2_codes = const.tile([P, 2 * O], U32, align_bytes=64)
+        w2_scales = const.tile([P, 2 * O], U8, align_bytes=64)
         w1_codes = const.tile([P, 2 * O], U32, align_bytes=64)
         w1_scales = const.tile([P, 2 * O], U8, align_bytes=64)
 
         x1_t = psum_t.tile([P, 4, P], F32, name="xt")
         for r in range(4):
             nc.tensor.transpose(out=x1_t[:, r, :], in_=x1_rows[:, r, :].bitcast(F32), identity=ident[:])
-        for h in range(2):
-            nc.vector.tensor_copy(
-                out=x1_words[:, h, :, :, 0].rearrange("p (t r) m -> p t r m", t=2),
-                in_=x1_t[:].rearrange("p r (h m t) -> p h t r m", h=2, m=32, t=2)[:, h, :, :, :],
-            )
-        bias_psum = psum_o.tile([P, 2 * O], F32, name="ps")
+        nc.vector.tensor_copy(
+            out=x1_words[:, 0, :, :, :].rearrange("p r b q -> p (r b q)"), in_=x1_t[:].rearrange("p r n -> p (r n)")
+        )
+        bias_psum = psum_r.tile([P, 2 * O], F32, name="rp")
         nc.tensor.matmul(out=bias_psum[:, 0:O], lhsT=ones[:], rhs=bias_row[:], start=True, stop=True)
         bias = const.tile([P, O], F32)
 
-        by_j_codes = const.tile([P, 2, 8, P], U32, align_bytes=64)
-        by_j_scales = const.tile([P, 2, 8, P], U8, align_bytes=64)
-        by_i_codes = const.tile([P, 2, 8, P], U32, align_bytes=64)
-        by_i_scales = const.tile([P, 2, 8, P], U8, align_bytes=64)
-        row_term = const.tile([P, 2, 8, O], F32)
-        by_i_grouped, row_psum = {}, {}
+        by_j_codes = const.tile([P, 16, P], U32, align_bytes=64)
+        by_j_scales = const.tile([P, 16, P], U8, align_bytes=64)
+        by_i_codes = const.tile([P, 8, P], U32, align_bytes=64)
+        by_i_scales = const.tile([P, 8, P], U8, align_bytes=64)
+        row_term = const.tile([P, 8, 2, O], F32)
+        repeated, row_psum = {}, {}
 
-        def x1_quantise(h):
-            nc.vector.quantize_mx(
-                out=x1_codes[:, h, :].bitcast(FP8X4),
-                scales=x1_scales[:, h, :],
-                in_=x1_words[:, h, :, :, :].rearrange("p a m w -> p (a m w)").bitcast(BF16),
-            )
+        def copy_on(engine, target, source):
+            if engine == "vector":
+                nc.vector.tensor_copy(out=target, in_=source)
+            else:
+                nc.scalar.copy(out=target, in_=source)
 
-        def x1_repeat_over_i(h):
-            nc.vector.tensor_copy(
-                out=by_j_codes[:, h, :, :].rearrange("p a (B I J) -> p (a B) I J", B=8, I=4, J=4).bitcast(I32),
-                in_=x1_codes[:, h, :]
-                .rearrange("p (g J) -> p g J", J=4)
-                .bitcast(I32)
+        def repeat_by_j(u, engine):
+            rep = upool.tile([P, 1024], F32, align_bytes=64)
+            copy_on(
+                engine,
+                rep[:].rearrange("p (m I J w) -> p m I J w", m=64, I=4, J=2, w=2),
+                x1_words[:, :, :, :, u : u + 5 : 4]
+                .rearrange("p w r b J -> p (r b) J w")
                 .unsqueeze(2)
-                .to_broadcast([P, 64, 4, 4]),
+                .to_broadcast([P, 64, 4, 2, 2]),
             )
-            nc.vector.tensor_copy(
-                out=by_j_scales[:, h, :, :]
-                .rearrange("p a n -> p (a n)")
-                .bitcast(I32)
-                .rearrange("p (g I) -> p g I", I=4),
-                in_=x1_scales[:, h, :].bitcast(I32).unsqueeze(2).to_broadcast([P, 64, 4]),
-            )
+            repeated[("j", u)] = rep
 
-        def unit_repeat_over_j(u):
-            h, a0 = u // 2, 4 * (u % 2)
-            grouped = upool.tile([P, 4, 32, 4, 2], F32, align_bytes=64)
-            nc.vector.tensor_copy(
-                out=grouped[:], in_=x1_words[:, h, a0 : a0 + 4, :, :].unsqueeze(3).to_broadcast([P, 4, 32, 4, 2])
-            )
-            by_i_grouped[u] = grouped
-
-        def unit_quantise(u):
-            h, a0 = u // 2, 4 * (u % 2)
+        def quantise_by_j(u):
             nc.vector.quantize_mx(
-                out=by_i_codes[:, h, a0 : a0 + 4, :].rearrange("p a n -> p (a n)").bitcast(FP8X4),
-                scales=by_i_scales[:, h, a0 : a0 + 4, :].rearrange("p a n -> p (a n)"),
-                in_=by_i_grouped[u][:].rearrange("p a m J w -> p (a m J w)").bitcast(BF16),
+                out=by_j_codes[:, 4 * u : 4 * u + 4, :].rearrange("p c n -> p (c n)").bitcast(FP8X4),
+                scales=by_j_scales[:, 4 * u : 4 * u + 4, :].rearrange("p c n -> p (c n)"),
+                in_=repeated[("j", u)][:].bitcast(BF16),
             )
 
-        def unit_matmul(u, pair):
-            h, a0 = u // 2, 4 * (u % 2) + 2 * pair
-            ps = psum_o.tile([P, 2 * O], F32)
+        def repeat_by_i(u, engine):
+            rep = upool.tile([P, 1024], F32, align_bytes=64)
+            copy_on(
+                engine,
+                rep[:].rearrange("p (m J w) -> p m J w", m=256, J=2, w=2),
+                x1_words[:, :, :, :, u : u + 7 : 2]
+                .rearrange("p w r b I -> p (r b I) w")
+                .unsqueeze(2)
+                .to_broadcast([P, 256, 2, 2]),
+            )
+            repeated[("i", u)] = rep
+
+        def quantise_by_i(u):
+            nc.vector.quantize_mx(
+                out=by_i_codes[:, 4 * u : 4 * u + 4, :].rearrange("p a n -> p (a n)").bitcast(FP8X4),
+                scales=by_i_scales[:, 4 * u : 4 * u + 4, :].rearrange("p a n -> p (a n)"),
+                in_=repeated[("i", u)][:].bitcast(BF16),
+            )
+
+        def row_matmul(a):
+            rp = psum_r.tile([P, 2 * O], F32)
             for s in range(2):
                 nc.tensor.matmul_mx(
-                    out=ps[:, s * O : (s + 1) * O],
-                    lhsT=by_i_codes[:, h, a0 + s, :].bitcast(FP8X4),
-                    lhsT_scale=by_i_scales[:, h, a0 + s, :],
-                    rhs=w1_codes[:, 0:O].bitcast(FP8X4),
-                    rhs_scale=w1_scales[:, 0:O],
+                    out=rp[:, s * O : (s + 1) * O],
+                    lhsT=by_i_codes[:, a, :].bitcast(FP8X4),
+                    lhsT_scale=by_i_scales[:, a, :],
+                    rhs=w1_codes[:, (1 - s) * O : (2 - s) * O].bitcast(FP8X4),
+                    rhs_scale=w1_scales[:, (1 - s) * O : (2 - s) * O],
                     start=True,
                     stop=True,
                 )
-            row_psum[(u, pair)] = ps
+            row_psum[a] = rp
 
-        def unit_add_bias(u, pair):
-            h, a0 = u // 2, 4 * (u % 2) + 2 * pair
+        def row_add_bias(a):
             nc.vector.tensor_tensor(
-                out=row_term[:, h, a0 : a0 + 2, :],
-                in0=row_psum[(u, pair)][:].rearrange("p (s o) -> p s o", s=2),
+                out=row_term[:, a, :, :],
+                in0=row_psum[a][:].rearrange("p (s o) -> p s o", s=2),
                 in1=bias[:].unsqueeze(1).to_broadcast([P, 2, O]),
                 op=ADD,
             )
 
-        def unit_pieces(u):
-            return [
-                lambda: unit_repeat_over_j(u),
-                lambda: unit_quantise(u),
-                lambda: unit_matmul(u, 0),
-                lambda: (unit_add_bias(u, 0), unit_matmul(u, 1)),
-                lambda: unit_add_bias(u, 1),
-            ]
-
-        x1_quantise(0)
-        x1_repeat_over_i(0)
-        unit_repeat_over_j(0)
-        unit_quantise(0)
+        repeat_by_j(1, "vector")
+        repeat_by_i(0, "vector")
+        quantise_by_j(1)
+        quantise_by_i(0)
+        for x in range(2):
+            nc.vector.tensor_copy(
+                out=w1_grouped[:, x, :, 0, :], in_=w_rows[:, 2 - 2 * x, :, :].rearrange("p e o -> p o e")
+            )
         nc.vector.quantize_mx(
             out=w2_codes[:].bitcast(FP8X4),
             scales=w2_scales[:],
-            in_=w2_grouped[:].rearrange("p o s e -> p (o s e)"),
+            in_=w2_grouped[:].rearrange("p x o s e -> p (x o s e)"),
         )
+        nc.vector.tensor_copy(out=bias[:], in_=bias_psum[:, 0:O])
         nc.vector.quantize_mx(
             out=w1_codes[:].bitcast(FP8X4),
             scales=w1_scales[:],
             in_=w1_grouped[:].rearrange("p x o s e -> p (x o s e)"),
         )
-        nc.vector.tensor_copy(out=bias[:], in_=bias_psum[:, 0:O])
-        pieces = (
-            unit_pieces(1) + [lambda: x1_quantise(1), lambda: x1_repeat_over_i(1)] + unit_pieces(2) + unit_pieces(3)
+
+        early, late = {}, {}
+        for a in range(8):
+            late.setdefault(a + 2, []).append(("row_matmul", a))
+            early.setdefault(a + 3, []).append(("row_add_bias", a))
+        late.setdefault(3, []).append(("repeat_by_i", 1))
+        late.setdefault(4, []).append(("quantise_by_i", 1))
+        late.setdefault(6, []).append(("repeat_by_j", 3))
+        late.setdefault(7, []).append(("quantise_by_j", 3))
+        late.setdefault(12, []).append(("repeat_by_j", 0))
+        late.setdefault(13, []).append(("quantise_by_j", 0))
+        late.setdefault(14, []).append(("repeat_by_j", 2))
+        late.setdefault(15, []).append(("quantise_by_j", 2))
+        pieces = dict(
+            row_matmul=row_matmul,
+            row_add_bias=row_add_bias,
+            repeat_by_i=lambda u: repeat_by_i(u, "scalar"),
+            quantise_by_i=quantise_by_i,
+            repeat_by_j=lambda u: repeat_by_j(u, "scalar"),
+            quantise_by_j=quantise_by_j,
         )
 
-        groups = []
-        for h in range(2):
-            blocks = [(A, C) for C in range(4) for A in range(C + 1)]
-            if h == 1:
-                blocks = [b for b in blocks if b[0] != b[1]] + [b for b in blocks if b[0] == b[1]]
-            for A, C in blocks:
-                of_block = block_groups(A, C)
-                for rounds in of_block[:-1]:
-                    groups.append((h, rounds, []))
-                groups.append((h, of_block[-1], sorted(set([(A, C), (C, A)]))))
+        groups = make_groups()
         n_groups = len(groups)
-        result = const.tile([P, 8, 8, O], F32)
-        result_slots = result[:].rearrange("p a c o -> p (a c) o")
-        transposed, grouped_of, codes_of, scales_of, sums = {}, {}, {}, {}, {}
-
-        def x2_slot(h, a, c):
-            return x2_words[(h, a // 2)][:, a % 2, c * P : (c + 1) * P]
-
-        def slots_of(one_round):
-            first, second = 8 * one_round[0][0] + one_round[0][1], 8 * one_round[1][0] + one_round[1][1]
-            return result_slots[:, first : second + 1 : second - first, :]
+        transposed, grouped_of, codes_of, scales_of, sums, result_of = {}, {}, {}, {}, {}, {}
 
         def transposes(g):
-            h, rounds, complete = groups[g]
-            for i in range(2):
+            stationaries = groups[g]["stationaries"]
+            for k in range(0, len(stationaries), 2):
                 xt = psum_t.tile([P, 4, P], F32)
-                for s in range(2):
-                    a, c = rounds[i][s]
-                    nc.tensor.transpose(out=xt[:, 2 * s, :], in_=x2_slot(h, a, c), identity=ident[:])
-                    nc.tensor.transpose(out=xt[:, 2 * s + 1, :], in_=x2_slot(h, c, a), identity=swap[:])
-                transposed[(g, i)] = xt
+                for s, (a, c) in enumerate(stationaries[k : k + 2]):
+                    nc.tensor.transpose(out=xt[:, 2 * s, :], in_=xn_words[(a, c)], identity=ident[:])
+                    nc.tensor.transpose(out=xt[:, 2 * s + 1, :], in_=xp_words[(a, c)], identity=ident[:])
+                transposed[(g, k // 2)] = xt
 
         def exits(g):
-            grouped = gpool.tile([P, 2, 2, P, 2], F32, align_bytes=64)
-            for i in range(2):
-                words = transposed[(g, i)][:].rearrange("p (s w) n -> p s n w", w=2)
-                if i == 1 and g >= VECTOR_HELPS_FROM and g % 2 == 0:
-                    nc.vector.tensor_copy(out=grouped[:, i, :, :, :], in_=words)
+            stationaries = groups[g]["stationaries"]
+            for k in range(0, len(stationaries), 2):
+                count = len(stationaries[k : k + 2])
+                grouped = gpool.tile([P, 2, P, 2], F32, align_bytes=64)
+                words = transposed[(g, k // 2)][:, 0 : 2 * count, :].rearrange("p (s w) n -> p s n w", w=2)
+                if g >= VECTOR_HELPS_FROM and g % VECTOR_HELPS_EVERY == 0:
+                    nc.vector.tensor_copy(out=grouped[:, 0:count, :, :], in_=words)
                 else:
-                    nc.scalar.copy(out=grouped[:, i, :, :, :], in_=words)
-            grouped_of[g] = grouped
+                    nc.scalar.copy(out=grouped[:, 0:count, :, :], in_=words)
+                grouped_of[(g, k // 2)] = grouped
 
         def quantise(g):
-            codes = gpool.tile([P, 4 * P], U32, align_bytes=64)
-            scales = gpool.tile([P, 4 * P], U8, align_bytes=64)
-            nc.vector.quantize_mx(
-                out=codes[:].bitcast(FP8X4),
-                scales=scales[:],
-                in_=grouped_of[g][:].rearrange("p i s n w -> p (i s n w)").bitcast(BF16),
-            )
-            codes_of[g] = codes
-            scales_of[g] = scales
+            stationaries = groups[g]["stationaries"]
+            for k in range(0, len(stationaries), 2):
+                count = len(stationaries[k : k + 2])
+                codes = gpool.tile([P, 2 * P], U32, align_bytes=64)
+                scales = gpool.tile([P, 2 * P], U8, align_bytes=64)
+                nc.vector.quantize_mx(
+                    out=codes[:, 0 : count * P].bitcast(FP8X4),
+                    scales=scales[:, 0 : count * P],
+                    in_=grouped_of[(g, k // 2)][:, 0:count, :, :].rearrange("p s n w -> p (s n w)").bitcast(BF16),
+                )
+                codes_of[(g, k // 2)] = codes
+                scales_of[(g, k // 2)] = scales
 
         def matmuls(g):
-            h, rounds, complete = groups[g]
-            for i in range(2):
+            for i, bank in enumerate(groups[g]["banks"]):
                 ps = psum_o.tile([P, 2 * O], F32)
-                for s in range(2):
-                    c = rounds[i][s][1]
-                    columns = slice((2 * i + s) * P, (2 * i + s + 1) * P)
+                width = 2 * O if bank["wide"] else O
+                for q, (s, c) in enumerate(bank["parts"]):
+                    columns = slice((s % 2) * P, (s % 2 + 1) * P)
                     nc.tensor.matmul_mx(
-                        out=ps[:, s * O : (s + 1) * O],
-                        lhsT=codes_of[g][:, columns].bitcast(FP8X4),
-                        lhsT_scale=scales_of[g][:, columns],
-                        rhs=w2_codes[:].bitcast(FP8X4),
-                        rhs_scale=w2_scales[:],
+                        out=ps[:, q * width : (q + 1) * width],
+                        lhsT=codes_of[(g, s // 2)][:, columns].bitcast(FP8X4),
+                        lhsT_scale=scales_of[(g, s // 2)][:, columns],
+                        rhs=w2_codes[:, 0:width].bitcast(FP8X4),
+                        rhs_scale=w2_scales[:, 0:width],
                         start=True,
                         stop=False,
                     )
                     nc.tensor.matmul_mx(
-                        out=ps[:, s * O : (s + 1) * O],
-                        lhsT=by_j_codes[:, h, c, :].bitcast(FP8X4),
-                        lhsT_scale=by_j_scales[:, h, c, :],
-                        rhs=w1_codes[:, O : 2 * O].bitcast(FP8X4),
-                        rhs_scale=w1_scales[:, O : 2 * O],
+                        out=ps[:, q * width : (q + 1) * width],
+                        lhsT=by_j_codes[:, c, :].bitcast(FP8X4),
+                        lhsT_scale=by_j_scales[:, c, :],
+                        rhs=w1_codes[:, 0:width].bitcast(FP8X4),
+                        rhs_scale=w1_scales[:, 0:width],
                         start=False,
                         stop=True,
                     )
                 sums[(g, i)] = ps
 
         def add_row_terms(g):
-            h, rounds, complete = groups[g]
-            for i in range(2):
-                first, second = rounds[i][0][0], rounds[i][1][0]
+            if groups[g]["first"]:
+                result = rpool.tile([P, RESULT_SLOTS, O], F32)
+                result_of["now"] = result
+            result_of[g] = result_of["now"]
+            for i, bank in enumerate(groups[g]["banks"]):
+                a = bank["a"]
                 nc.vector.tensor_tensor(
-                    out=slots_of(rounds[i]),
+                    out=result_of[g][:, bank["slots"], :],
                     in0=sums[(g, i)][:].rearrange("p (s o) -> p s o", s=2),
-                    in1=row_term[:, h, first : second + 1 : second - first, :],
+                    in1=row_term[:, a, :, :] if bank["wide"] else row_term[:, a : a + 2, 0, :],
                     op=ADD,
                 )
 
         def sigmoids_and_stores(g):
-            h, rounds, complete = groups[g]
-            for i in range(2):
-                nc.scalar.activation(out=slots_of(rounds[i]), in_=slots_of(rounds[i]), func=SIGMOID)
-            for A, C in complete:
-                for a in (2 * A, 2 * A + 1):
-                    nc.sync.dma_start(
-                        out=out_rows[h, a, :, :, 2 * C * O : (2 * C + 2) * O],
-                        in_=result[:, a, 2 * C : 2 * C + 2, :].rearrange("p c o -> p (c o)"),
-                    )
+            result = result_of[g]
+            for slots in groups[g]["sigmoids"]:
+                nc.scalar.activation(out=result[:, slots, :], in_=result[:, slots, :], func=SIGMOID)
+            for kind, major, lo, hi, s in groups[g]["stores"]:
+                rows = result[:, s : s + hi - lo, :].rearrange("p s o -> p (s o)")
+                if kind == "n":
+                    nc.sync.dma_start(out=out_n[major, :, :, lo * O : hi * O], in_=rows)
+                else:
+                    for J in range(2):
+                        nc.sync.dma_start(
+                            out=out_p[major, J, :, :, lo * O : hi * O],
+                            in_=result[J:P:2, s : s + hi - lo, :].rearrange("p s o -> p (s o)"),
+                        )
 
         for n in range(n_groups + SIGMOID_STORE):
+            for name, arg in early.get(n, []):
+                pieces[name](arg)
             if 0 <= n - SIGMOID_STORE < n_groups:
                 sigmoids_and_stores(n - SIGMOID_STORE)
             if 0 <= n - BIAS_ADD < n_groups:
                 add_row_terms(n - BIAS_ADD)
             if 0 <= n - MATMUL < n_groups:
                 matmuls(n - MATMUL)
-            if n == MATMUL - 1:
-                unit_matmul(0, 0)
-                unit_matmul(0, 1)
             if 0 <= n - QUANTISE < n_groups:
                 quantise(n - QUANTISE)
-            if n == BIAS_ADD - 1:
-                unit_add_bias(0, 0)
-                unit_add_bias(0, 1)
-            if 0 <= n - FIRST_PIECE < len(pieces):
-                pieces[n - FIRST_PIECE]()
             if 0 <= n - EXIT < n_groups:
                 exits(n - EXIT)
             if n < n_groups:
                 transposes(n)
+            for name, arg in late.get(n, []):
+                pieces[name](arg)

@@ -105,12 +105,12 @@ def tile_differentiablelogicmachine_pa_t_kernel(tc, x1, x2, W2, b2, out):
         nc.sync.dma_start(out=w_rows[:, 0:4, :, :], in_=w_view)
         nc.sync.dma_start(out=w_rows[:, 4:5, :, :], in_=w_view[:, 1:2, :, :])
         bias_row = const.tile([P, O], BF16)
-        nc.gpsimd.memset(bias_row[:], 0.0)
+        nc.vector.memset(bias_row[:], 0.0)
         nc.sync.dma_start(out=bias_row[0:1, :], in_=b2.rearrange("(a o) -> a o", a=1))
 
         xn_words, xp_words = {}, {}
         xn_view = x2.rearrange("b (I a) (J c) k -> a (b I) J (c k)", I=4, a=8, J=2, c=16)
-        xp_view = x2.rearrange("b (J c) (I a) k -> c J b I (a k)", J=2, c=16, I=4, a=8)
+        xp_view = x2.rearrange("b (J c) (I a) k -> c (b J) I (a k)", J=2, c=16, I=4, a=8)
         out_n = out.rearrange("b (I a) (J c) o -> a (b I) J (c o)", I=4, a=8, J=2, c=16)
         out_p = out.rearrange("b (J c) (I a) o -> c J b I (a o)", J=2, c=16, I=4, a=8)
 
@@ -122,8 +122,7 @@ def tile_differentiablelogicmachine_pa_t_kernel(tc, x1, x2, W2, b2, out):
 
         def load_xp(c, a_lo, a_hi):
             xp = const.tile([P, (a_hi - a_lo) * O], BF16, name="xp_%d_%d" % (c, a_lo))
-            for J in range(2):
-                nc.sync.dma_start(out=xp[J:P:2, :], in_=xp_view[c, J, :, :, a_lo * O : a_hi * O])
+            nc.sync.dma_start(out=xp[:], in_=xp_view[c, :, :, a_lo * O : a_hi * O])
             for a in range(a_lo, a_hi):
                 xp_words[(a, c)] = xp[:, (a - a_lo) * O : (a - a_lo + 1) * O].bitcast(F32)
 
@@ -148,16 +147,21 @@ def tile_differentiablelogicmachine_pa_t_kernel(tc, x1, x2, W2, b2, out):
 
         ident = const.tile([P, P], F32)
         make_identity(nc, ident[:])
+        turn = const.tile([P, P], F32)
+        nc.vector.tensor_copy(
+            out=turn[:].rearrange("p (b I J) -> p b I J", b=16, I=4, J=2),
+            in_=ident[:].rearrange("p (b J I) -> p b I J", b=16, J=2, I=4),
+        )
         ones = const.tile([P, P], BF16)
-        nc.gpsimd.memset(ones[:], 1.0)
+        nc.vector.memset(ones[:], 1.0)
         warm_in = const.tile([P, 1], F32)
-        nc.gpsimd.memset(warm_in[:], 0.0)
+        nc.vector.memset(warm_in[:], 0.0)
         warm_out = const.tile([P, 1], F32)
         nc.scalar.activation(out=warm_out[:], in_=warm_in[:], func=SIGMOID)
         w1_grouped = const.tile([P, 2, O, 2, 2], BF16, align_bytes=64)
-        nc.gpsimd.memset(w1_grouped[:], 0.0)
+        nc.vector.memset(w1_grouped[:], 0.0)
         x1_words = const.tile([P, 2, 4, 16, 8], F32)
-        nc.gpsimd.memset(x1_words[:, 1, :, :, :], 0.0)
+        nc.vector.memset(x1_words[:, 1, :, :, :], 0.0)
 
         w2_grouped = const.tile([P, 2, O, 2, 2], BF16, align_bytes=64)
         nc.scalar.copy(out=w2_grouped[:, 0, :, :, :], in_=w_rows[:, 1:4:2, :, :].rearrange("p s e o -> p o s e"))
@@ -301,7 +305,7 @@ def tile_differentiablelogicmachine_pa_t_kernel(tc, x1, x2, W2, b2, out):
                 xt = psum_t.tile([P, 4, P], F32)
                 for s, (a, c) in enumerate(stationaries[k : k + 2]):
                     nc.tensor.transpose(out=xt[:, 2 * s, :], in_=xn_words[(a, c)], identity=ident[:])
-                    nc.tensor.transpose(out=xt[:, 2 * s + 1, :], in_=xp_words[(a, c)], identity=ident[:])
+                    nc.tensor.transpose(out=xt[:, 2 * s + 1, :], in_=xp_words[(a, c)], identity=turn[:])
                 transposed[(g, k // 2)] = xt
 
         def exits(g):

@@ -23,66 +23,91 @@ BIAS_ADD = 4
 SIGMOID_STORE = 5
 VECTOR_HELPS_FROM = 18
 VECTOR_HELPS_EVERY = 4
-RESULT_SLOTS = 16
+RESULT_SLOTS = 32
+
+
+def by_j_block(c):
+    return (c % 8 // 2) * 4 + (c // 8) * 2 + c % 2
+
+
+def shifted(slots, off):
+    return slice(slots.start + off, slots.stop + off, slots.step)
+
+
+def chunk_groups(C, gamma, a_lo, a_hi, last, off):
+    c0 = 8 * gamma + 2 * C
+    c1 = c0 + 1
+    n = a_hi - a_lo
+    base = 2 * n + (3 if last else 0)
+    chunk = []
+    for t in range(n):
+        a = a_lo + t
+        chunk.append(
+            dict(
+                first=False,
+                stationaries=[(a, c0), (a, c1)],
+                banks=[
+                    dict(wide=True, parts=[(0, c0)], a=a, slots=shifted(slice(2 * t, base + t + 1, base - t), off)),
+                    dict(
+                        wide=True,
+                        parts=[(1, c1)],
+                        a=a,
+                        slots=shifted(slice(2 * t + 1, base + n + t + 1, base + n - t - 1), off),
+                    ),
+                ],
+                sigmoids=[shifted(slice(2 * t, 2 * t + 2, 1), off), shifted(slice(base + t, base + n + t + 1, n), off)],
+                stores=[("n", a, 2 * C, 2 * C + 2, 2 * t)] if gamma == 1 else [],
+            )
+        )
+    if last:
+        d0 = 2 * C
+        d1 = d0 + 1
+        chunk.append(
+            dict(
+                first=False,
+                stationaries=[(d0, c0), (d1, c1), (d0, c1)],
+                banks=[
+                    dict(
+                        wide=True,
+                        parts=[(2, c1)],
+                        a=d0,
+                        slots=shifted(slice(2 * n + 1, base + 2 * n + 1, base - 1), off),
+                    ),
+                    dict(wide=False, parts=[(0, c0), (1, c1)], a=d0, slots=shifted(slice(2 * n, 2 * n + 3, 2), off)),
+                ],
+                sigmoids=[
+                    shifted(slice(2 * n, 2 * n + 3, 1), off),
+                    shifted(slice(base + 2 * n, base + 2 * n + 1, 1), off),
+                ],
+                stores=[("n", d0, d0, d1 + 1, 2 * n), ("n", d1, d1, d1 + 1, 2 * n + 2)] if gamma == 1 else [],
+            )
+        )
+    partner = []
+    if n > 0:
+        partner.append(("p", c0, a_lo, a_hi, off + base))
+    partner.append(("p", c1, a_lo, a_hi + (1 if last else 0), off + base + n))
+    return chunk, partner
 
 
 def make_groups():
     groups = []
     for C in (3, 2, 1, 0):
-        for gamma in range(2):
-            c0 = 8 * gamma + 2 * C
-            c1 = c0 + 1
-            split = C if C >= 2 else 0
-            for a_lo, a_hi, last in ((0, split, False), (split, 2 * C, True)):
-                n = a_hi - a_lo
-                if n == 0 and not last:
-                    continue
-                base = 2 * n + (3 if last else 0)
-                chunk = []
-                for t in range(n):
-                    a = a_lo + t
-                    chunk.append(
-                        dict(
-                            first=False,
-                            stationaries=[(a, c0), (a, c1)],
-                            banks=[
-                                dict(wide=True, parts=[(0, c0)], a=a, slots=slice(2 * t, base + t + 1, base - t)),
-                                dict(
-                                    wide=True,
-                                    parts=[(1, c1)],
-                                    a=a,
-                                    slots=slice(2 * t + 1, base + n + t + 1, base + n - t - 1),
-                                ),
-                            ],
-                            sigmoids=[slice(2 * t, 2 * t + 2, 1), slice(base + t, base + n + t + 1, n)],
-                            stores=[("n", a, c0, c1 + 1, 2 * t)],
-                        )
-                    )
-                if last:
-                    d0 = 2 * C
-                    d1 = d0 + 1
-                    chunk.append(
-                        dict(
-                            first=False,
-                            stationaries=[(d0, c0), (d1, c1), (d0, c1)],
-                            banks=[
-                                dict(
-                                    wide=True,
-                                    parts=[(2, c1)],
-                                    a=d0,
-                                    slots=slice(2 * n + 1, base + 2 * n + 1, base - 1),
-                                ),
-                                dict(wide=False, parts=[(0, c0), (1, c1)], a=d0, slots=slice(2 * n, 2 * n + 3, 2)),
-                            ],
-                            sigmoids=[slice(2 * n, 2 * n + 3, 1), slice(base + 2 * n, base + 2 * n + 1, 1)],
-                            stores=[("n", d0, c0, c1 + 1, 2 * n), ("n", d1, c1, c1 + 1, 2 * n + 2)],
-                        )
-                    )
-                if n > 0:
-                    chunk[-1]["stores"].append(("p", c0, a_lo, a_hi, base))
-                chunk[-1]["stores"].append(("p", c1, a_lo, a_hi + (1 if last else 0), base + n))
-                chunk[0]["first"] = True
-                groups.extend(chunk)
+        split = C if C >= 2 else 0
+        for a_lo, a_hi, last in ((0, split, False), (split, 2 * C, True)):
+            if a_hi == a_lo and not last:
+                continue
+            size = 4 * (a_hi - a_lo) + (4 if last else 0)
+            first, first_partner = chunk_groups(C, 0, a_lo, a_hi, last, 0)
+            second, second_partner = chunk_groups(C, 1, a_lo, a_hi, last, size)
+            chunk = []
+            for one, other in zip(first, second):
+                one["size"] = size
+                other["size"] = size
+                chunk.extend([one, other])
+            chunk[-2]["stores"].extend(first_partner)
+            chunk[-1]["stores"].extend(second_partner)
+            chunk[0]["first"] = True
+            groups.extend(chunk)
     return groups
 
 
@@ -92,7 +117,7 @@ def tile_differentiablelogicmachine_pa_t_kernel(tc, x1, x2, W2, b2, out):
         const = ctx.enter_context(tc.tile_pool(name="const", bufs=1))
         gpool = ctx.enter_context(tc.tile_pool(name="gpool", bufs=6))
         upool = ctx.enter_context(tc.tile_pool(name="upool", bufs=2))
-        rpool = ctx.enter_context(tc.tile_pool(name="rpool", bufs=4))
+        rpool = ctx.enter_context(tc.tile_pool(name="rpool", bufs=2))
         psum_t = ctx.enter_context(tc.psum_pool(name="psum_t", bufs=3))
         psum_o = ctx.enter_context(tc.psum_pool(name="psum_o", bufs=4))
         psum_r = ctx.enter_context(tc.psum_pool(name="psum_r", bufs=1))
@@ -109,16 +134,19 @@ def tile_differentiablelogicmachine_pa_t_kernel(tc, x1, x2, W2, b2, out):
         nc.sync.dma_start(out=bias_row[0:1, :], in_=b2.rearrange("(a o) -> a o", a=1))
 
         xn_words, xp_words = {}, {}
-        xn_view = x2.rearrange("b (I a) (J c) k -> a (b I) J (c k)", I=4, a=8, J=2, c=16)
+        xn_view = x2.rearrange("b (I a) (G c) k -> a (b I) G (c k)", I=4, a=8, G=4, c=8)
         xp_view = x2.rearrange("b (J c) (I a) k -> c (b J) I (a k)", J=2, c=16, I=4, a=8)
-        out_n = out.rearrange("b (I a) (J c) o -> a (b I) J (c o)", I=4, a=8, J=2, c=16)
+        out_n = out.rearrange("b (I a) (G c) o -> a (b I) G (c o)", I=4, a=8, G=4, c=8)
         out_p = out.rearrange("b (J c) (I a) o -> c J b I (a o)", J=2, c=16, I=4, a=8)
 
-        def load_xn(a, c_lo, c_hi):
-            xn = const.tile([P, (c_hi - c_lo) * O], BF16, name="xn_%d_%d" % (a, c_lo))
-            nc.sync.dma_start(out=xn[:], in_=xn_view[a, :, :, c_lo * O : c_hi * O])
-            for c in range(c_lo, c_hi):
-                xn_words[(a, c)] = xn[:, (c - c_lo) * O : (c - c_lo + 1) * O].bitcast(F32)
+        def load_xn(a, cl_lo, cl_hi):
+            xn = const.tile([P, 2, cl_hi - cl_lo, O], BF16, name="xn_%d_%d" % (a, cl_lo))
+            nc.sync.dma_start(
+                out=xn[:].rearrange("p g c k -> p g (c k)"), in_=xn_view[a, :, :, cl_lo * O : cl_hi * O]
+            )
+            for gamma in range(2):
+                for cl in range(cl_lo, cl_hi):
+                    xn_words[(a, 8 * gamma + cl)] = xn[:, gamma, cl - cl_lo, :].bitcast(F32)
 
         def load_xp(c, a_lo, a_hi):
             xp = const.tile([P, (a_hi - a_lo) * O], BF16, name="xp_%d_%d" % (c, a_lo))
@@ -126,23 +154,19 @@ def tile_differentiablelogicmachine_pa_t_kernel(tc, x1, x2, W2, b2, out):
             for a in range(a_lo, a_hi):
                 xp_words[(a, c)] = xp[:, (a - a_lo) * O : (a - a_lo + 1) * O].bitcast(F32)
 
-        load_xp(6, 0, 3)
-        load_xp(7, 0, 3)
+        for c in (6, 7, 14, 15):
+            load_xp(c, 0, 3)
         for a in range(3):
             load_xn(a, 6, 8)
-        load_xp(6, 3, 7)
-        load_xp(7, 3, 8)
+        for c in (6, 7, 14, 15):
+            load_xp(c, 3, c % 8 + 1)
         for a in range(3, 8):
             load_xn(a, max(a, 6), 8)
-        load_xp(14, 0, 7)
-        load_xp(15, 0, 8)
-        for a in range(8):
-            load_xn(a, 8 + a, 16)
-        load_xp(4, 0, 5)
-        load_xp(5, 0, 6)
+        for c in (4, 5, 12, 13):
+            load_xp(c, 0, c % 8 + 1)
         for a in range(6):
             load_xn(a, a, 6)
-        for c in (12, 13, 2, 3, 10, 11, 0, 1, 8, 9):
+        for c in (2, 3, 10, 11, 0, 1, 8, 9):
             load_xp(c, 0, c % 8 + 1)
 
         ident = const.tile([P, P], F32)
@@ -196,14 +220,17 @@ def tile_differentiablelogicmachine_pa_t_kernel(tc, x1, x2, W2, b2, out):
 
         def repeat_by_j(u, engine):
             rep = upool.tile([P, 1024], F32, align_bytes=64)
-            copy_on(
-                engine,
-                rep[:].rearrange("p (m I J w) -> p m I J w", m=64, I=4, J=2, w=2),
-                x1_words[:, :, :, :, u : u + 5 : 4]
-                .rearrange("p w r b J -> p (r b) J w")
-                .unsqueeze(2)
-                .to_broadcast([P, 64, 4, 2, 2]),
-            )
+            for gamma in range(2):
+                q0 = 2 * gamma + u // 2
+                r0 = 2 * (u % 2)
+                copy_on(
+                    engine,
+                    rep[:, gamma * 512 : (gamma + 1) * 512].rearrange("p (m I J w) -> p m I J w", m=32, I=4, J=2, w=2),
+                    x1_words[:, :, r0 : r0 + 2, :, q0 : q0 + 5 : 4]
+                    .rearrange("p w r b J -> p (r b) J w")
+                    .unsqueeze(2)
+                    .to_broadcast([P, 32, 4, 2, 2]),
+                )
             repeated[("j", u)] = rep
 
         def quantise_by_j(u):
@@ -254,19 +281,17 @@ def tile_differentiablelogicmachine_pa_t_kernel(tc, x1, x2, W2, b2, out):
                 op=ADD,
             )
 
-        repeat_by_j(1, "vector")
-        repeat_by_i(0, "vector")
-        quantise_by_j(1)
-        quantise_by_i(0)
         for x in range(2):
-            nc.vector.tensor_copy(
-                out=w1_grouped[:, x, :, 0, :], in_=w_rows[:, 2 - 2 * x, :, :].rearrange("p e o -> p o e")
-            )
+            nc.scalar.copy(out=w1_grouped[:, x, :, 0, :], in_=w_rows[:, 2 - 2 * x, :, :].rearrange("p e o -> p o e"))
+        repeat_by_j(3, "vector")
+        repeat_by_i(0, "vector")
         nc.vector.quantize_mx(
             out=w2_codes[:].bitcast(FP8X4),
             scales=w2_scales[:],
             in_=w2_grouped[:].rearrange("p x o s e -> p (x o s e)"),
         )
+        quantise_by_j(3)
+        quantise_by_i(0)
         nc.vector.tensor_copy(out=bias[:], in_=bias_psum[:, 0:O])
         nc.vector.quantize_mx(
             out=w1_codes[:].bitcast(FP8X4),
@@ -276,16 +301,13 @@ def tile_differentiablelogicmachine_pa_t_kernel(tc, x1, x2, W2, b2, out):
 
         early, late = {}, {}
         for a in range(8):
-            late.setdefault(a + 2, []).append(("row_matmul", a))
-            early.setdefault(a + 3, []).append(("row_add_bias", a))
-        late.setdefault(3, []).append(("repeat_by_i", 1))
-        late.setdefault(4, []).append(("quantise_by_i", 1))
-        late.setdefault(6, []).append(("repeat_by_j", 3))
-        late.setdefault(7, []).append(("quantise_by_j", 3))
-        late.setdefault(12, []).append(("repeat_by_j", 0))
-        late.setdefault(13, []).append(("quantise_by_j", 0))
-        late.setdefault(14, []).append(("repeat_by_j", 2))
-        late.setdefault(15, []).append(("quantise_by_j", 2))
+            late.setdefault(min(2 * a + 2, a + 7), []).append(("row_matmul", a))
+            early.setdefault(min(2 * a + 3, a + 8), []).append(("row_add_bias", a))
+        late.setdefault(5, []).append(("repeat_by_i", 1))
+        late.setdefault(6, []).append(("quantise_by_i", 1))
+        for u, n in ((2, 11), (1, 19), (0, 23)):
+            late.setdefault(n, []).append(("repeat_by_j", u))
+            late.setdefault(n + 1, []).append(("quantise_by_j", u))
         pieces = dict(
             row_matmul=row_matmul,
             row_add_bias=row_add_bias,
@@ -351,8 +373,8 @@ def tile_differentiablelogicmachine_pa_t_kernel(tc, x1, x2, W2, b2, out):
                     )
                     nc.tensor.matmul_mx(
                         out=ps[:, q * width : (q + 1) * width],
-                        lhsT=by_j_codes[:, c, :].bitcast(FP8X4),
-                        lhsT_scale=by_j_scales[:, c, :],
+                        lhsT=by_j_codes[:, by_j_block(c), :].bitcast(FP8X4),
+                        lhsT_scale=by_j_scales[:, by_j_block(c), :],
                         rhs=w1_codes[:, 0:width].bitcast(FP8X4),
                         rhs_scale=w1_scales[:, 0:width],
                         start=False,
@@ -378,10 +400,15 @@ def tile_differentiablelogicmachine_pa_t_kernel(tc, x1, x2, W2, b2, out):
             result = result_of[g]
             for slots in groups[g]["sigmoids"]:
                 nc.scalar.activation(out=result[:, slots, :], in_=result[:, slots, :], func=SIGMOID)
+            size = groups[g]["size"]
             for kind, major, lo, hi, s in groups[g]["stores"]:
-                rows = result[:, s : s + hi - lo, :].rearrange("p s o -> p (s o)")
                 if kind == "n":
-                    nc.sync.dma_start(out=out_n[major, :, :, lo * O : hi * O], in_=rows)
+                    nc.sync.dma_start(
+                        out=out_n[major, :, :, lo * O : hi * O],
+                        in_=result[:, 0 : 2 * size, :]
+                        .rearrange("p (g s) o -> p g s o", g=2)[:, :, s : s + hi - lo, :]
+                        .rearrange("p g s o -> p g (s o)"),
+                    )
                 else:
                     for J in range(2):
                         nc.sync.dma_start(
@@ -390,8 +417,6 @@ def tile_differentiablelogicmachine_pa_t_kernel(tc, x1, x2, W2, b2, out):
                         )
 
         for n in range(n_groups + SIGMOID_STORE):
-            for name, arg in early.get(n, []):
-                pieces[name](arg)
             if 0 <= n - SIGMOID_STORE < n_groups:
                 sigmoids_and_stores(n - SIGMOID_STORE)
             if 0 <= n - BIAS_ADD < n_groups:
@@ -400,6 +425,8 @@ def tile_differentiablelogicmachine_pa_t_kernel(tc, x1, x2, W2, b2, out):
                 matmuls(n - MATMUL)
             if 0 <= n - QUANTISE < n_groups:
                 quantise(n - QUANTISE)
+            for name, arg in early.get(n, []):
+                pieces[name](arg)
             if 0 <= n - EXIT < n_groups:
                 exits(n - EXIT)
             if n < n_groups:

@@ -23,90 +23,55 @@ BIAS_ADD = 4
 SIGMOID_STORE = 5
 VECTOR_HELPS_FROM = 18
 VECTOR_HELPS_EVERY = 4
-RESULT_SLOTS = 32
+RESULT_TAGS = ("result_a", "result_b", "result_c")
+RESULT_SLOTS = dict(result_a=24, result_b=32, result_c=16)
 
 
 def by_j_block(c):
     return (c % 8 // 2) * 4 + (c // 8) * 2 + c % 2
 
 
-def shifted(slots, off):
-    return slice(slots.start + off, slots.stop + off, slots.step)
-
-
-def chunk_groups(C, gamma, a_lo, a_hi, last, off):
-    c0 = 8 * gamma + 2 * C
-    c1 = c0 + 1
-    n = a_hi - a_lo
-    base = 2 * n + (3 if last else 0)
-    chunk = []
-    for t in range(n):
-        a = a_lo + t
-        chunk.append(
-            dict(
-                first=False,
-                stationaries=[(a, c0), (a, c1)],
-                banks=[
-                    dict(wide=True, parts=[(0, c0)], a=a, slots=shifted(slice(2 * t, base + t + 1, base - t), off)),
-                    dict(
-                        wide=True,
-                        parts=[(1, c1)],
-                        a=a,
-                        slots=shifted(slice(2 * t + 1, base + n + t + 1, base + n - t - 1), off),
-                    ),
-                ],
-                sigmoids=[shifted(slice(2 * t, 2 * t + 2, 1), off), shifted(slice(base + t, base + n + t + 1, n), off)],
-                stores=[("n", a, 2 * C, 2 * C + 2, 2 * t)] if gamma == 1 else [],
-            )
-        )
-    if last:
-        d0 = 2 * C
-        d1 = d0 + 1
-        chunk.append(
-            dict(
-                first=False,
-                stationaries=[(d0, c0), (d1, c1), (d0, c1)],
-                banks=[
-                    dict(
-                        wide=True,
-                        parts=[(2, c1)],
-                        a=d0,
-                        slots=shifted(slice(2 * n + 1, base + 2 * n + 1, base - 1), off),
-                    ),
-                    dict(wide=False, parts=[(0, c0), (1, c1)], a=d0, slots=shifted(slice(2 * n, 2 * n + 3, 2), off)),
-                ],
-                sigmoids=[
-                    shifted(slice(2 * n, 2 * n + 3, 1), off),
-                    shifted(slice(base + 2 * n, base + 2 * n + 1, 1), off),
-                ],
-                stores=[("n", d0, d0, d1 + 1, 2 * n), ("n", d1, d1, d1 + 1, 2 * n + 2)] if gamma == 1 else [],
-            )
-        )
-    partner = []
-    if n > 0:
-        partner.append(("p", c0, a_lo, a_hi, off + base))
-    partner.append(("p", c1, a_lo, a_hi + (1 if last else 0), off + base + n))
-    return chunk, partner
-
-
 def make_groups():
     groups = []
+    n_chunks = 0
     for C in (3, 2, 1, 0):
         split = C if C >= 2 else 0
         for a_lo, a_hi, last in ((0, split, False), (split, 2 * C, True)):
             if a_hi == a_lo and not last:
                 continue
-            size = 4 * (a_hi - a_lo) + (4 if last else 0)
-            first, first_partner = chunk_groups(C, 0, a_lo, a_hi, last, 0)
-            second, second_partner = chunk_groups(C, 1, a_lo, a_hi, last, size)
+            n = a_hi - a_lo
+            base = 2 * n + (3 if last else 0)
+            size = 4 * n + (4 if last else 0)
+            cl0 = 2 * C
+            cl1 = cl0 + 1
             chunk = []
-            for one, other in zip(first, second):
-                one["size"] = size
-                other["size"] = size
-                chunk.extend([one, other])
-            chunk[-2]["stores"].extend(first_partner)
-            chunk[-1]["stores"].extend(second_partner)
-            chunk[0]["first"] = True
+            for a in range(a_lo, a_hi):
+                t = a - a_lo
+                chunk.append(dict(a=a, cl=cl0, direct=2 * t, mirrored=base + t, stores=[]))
+                chunk.append(
+                    dict(a=a, cl=cl1, direct=2 * t + 1, mirrored=base + n + t, stores=[("n", a, cl0, cl1 + 1, 2 * t)])
+                )
+            if n > 0:
+                chunk[-2]["stores"].append(("p", cl0, a_lo, a_hi, base))
+            if last:
+                chunk.append(dict(a=cl0, cl=cl0, direct=2 * n, mirrored=None, stores=[]))
+                chunk.append(
+                    dict(
+                        a=cl0,
+                        cl=cl1,
+                        direct=2 * n + 1,
+                        mirrored=base + 2 * n,
+                        stores=[("n", cl0, cl0, cl1 + 1, 2 * n), ("p", cl1, a_lo, cl0 + 1, base + n)],
+                    )
+                )
+                chunk.append(dict(a=cl1, cl=cl1, direct=2 * n + 2, mirrored=None, stores=[("n", cl1, cl1, cl1 + 1, 2 * n + 2)]))
+            else:
+                chunk[-1]["stores"].append(("p", cl1, a_lo, a_hi, base + n))
+            for k, group in enumerate(chunk):
+                group["size"] = size
+                group["first"] = k == 0
+                group["chunk"] = n_chunks
+            n_chunks += 1
             groups.extend(chunk)
     return groups
 
@@ -117,7 +82,7 @@ def tile_differentiablelogicmachine_pa_t_kernel(tc, x1, x2, W2, b2, out):
         const = ctx.enter_context(tc.tile_pool(name="const", bufs=1))
         gpool = ctx.enter_context(tc.tile_pool(name="gpool", bufs=6))
         upool = ctx.enter_context(tc.tile_pool(name="upool", bufs=2))
-        rpool = ctx.enter_context(tc.tile_pool(name="rpool", bufs=2))
+        rpool = ctx.enter_context(tc.tile_pool(name="rpool", bufs=1))
         psum_t = ctx.enter_context(tc.psum_pool(name="psum_t", bufs=3))
         psum_o = ctx.enter_context(tc.psum_pool(name="psum_o", bufs=4))
         psum_r = ctx.enter_context(tc.psum_pool(name="psum_r", bufs=1))
@@ -133,48 +98,36 @@ def tile_differentiablelogicmachine_pa_t_kernel(tc, x1, x2, W2, b2, out):
         nc.vector.memset(bias_row[:], 0.0)
         nc.sync.dma_start(out=bias_row[0:1, :], in_=b2.rearrange("(a o) -> a o", a=1))
 
-        xn_words, xp_words = {}, {}
-        xn_view = x2.rearrange("b (I a) (G c) k -> a (b I) G (c k)", I=4, a=8, G=4, c=8)
-        xp_view = x2.rearrange("b (J c) (I a) k -> c (b J) I (a k)", J=2, c=16, I=4, a=8)
+        x2_words = {}
+        x2_view = x2.rearrange("b (I a) (G c) k -> a (b I) G (c k)", I=4, a=8, G=4, c=8)
         out_n = out.rearrange("b (I a) (G c) o -> a (b I) G (c o)", I=4, a=8, G=4, c=8)
         out_p = out.rearrange("b (J c) (I a) o -> c J b I (a o)", J=2, c=16, I=4, a=8)
 
-        def load_xn(a, cl_lo, cl_hi):
-            xn = const.tile([P, 2, cl_hi - cl_lo, O], BF16, name="xn_%d_%d" % (a, cl_lo))
+        def load_x2(a, half):
+            rows = const.tile([P, 2, 4, O], BF16, name="x2_%d_%d" % (a, half))
             nc.sync.dma_start(
-                out=xn[:].rearrange("p g c k -> p g (c k)"), in_=xn_view[a, :, :, cl_lo * O : cl_hi * O]
+                out=rows[:].rearrange("p g c k -> p g (c k)"), in_=x2_view[a, :, :, half * 4 * O : (half + 1) * 4 * O]
             )
             for gamma in range(2):
-                for cl in range(cl_lo, cl_hi):
-                    xn_words[(a, 8 * gamma + cl)] = xn[:, gamma, cl - cl_lo, :].bitcast(F32)
+                for c in range(4):
+                    x2_words[(a, gamma, 4 * half + c)] = rows[:, gamma, c, :].bitcast(F32)
 
-        def load_xp(c, a_lo, a_hi):
-            xp = const.tile([P, (a_hi - a_lo) * O], BF16, name="xp_%d_%d" % (c, a_lo))
-            nc.sync.dma_start(out=xp[:], in_=xp_view[c, :, :, a_lo * O : a_hi * O])
-            for a in range(a_lo, a_hi):
-                xp_words[(a, c)] = xp[:, (a - a_lo) * O : (a - a_lo + 1) * O].bitcast(F32)
-
-        for c in (6, 7, 14, 15):
-            load_xp(c, 0, 3)
-        for a in range(3):
-            load_xn(a, 6, 8)
-        for c in (6, 7, 14, 15):
-            load_xp(c, 3, c % 8 + 1)
-        for a in range(3, 8):
-            load_xn(a, max(a, 6), 8)
-        for c in (4, 5, 12, 13):
-            load_xp(c, 0, c % 8 + 1)
-        for a in range(6):
-            load_xn(a, a, 6)
-        for c in (2, 3, 10, 11, 0, 1, 8, 9):
-            load_xp(c, 0, c % 8 + 1)
+        for a, half in (
+            (6, 0), (0, 1), (7, 0), (1, 1), (2, 1), (3, 1), (6, 1), (4, 1), (7, 1), (5, 1),
+            (4, 0), (5, 0), (2, 0), (3, 0), (0, 0), (1, 0),
+        ):
+            load_x2(a, half)
 
         ident = const.tile([P, P], F32)
         make_identity(nc, ident[:])
-        turn = const.tile([P, P], F32)
+        by_q = const.tile([P, P], F32)
         nc.vector.tensor_copy(
-            out=turn[:].rearrange("p (b I J) -> p b I J", b=16, I=4, J=2),
-            in_=ident[:].rearrange("p (b J I) -> p b I J", b=16, J=2, I=4),
+            out=by_q[:].rearrange("p (q m) -> p q m", q=4), in_=ident[:].rearrange("p (m q) -> p q m", q=4)
+        )
+        by_partner = const.tile([P, P], F32)
+        nc.vector.tensor_copy(
+            out=by_partner[:].rearrange("p (j b x) -> p j b x", j=4, b=16, x=2),
+            in_=ident[:].rearrange("p (b j x) -> p j b x", b=16, j=4, x=2),
         )
         ones = const.tile([P, P], BF16)
         nc.vector.memset(ones[:], 1.0)
@@ -322,86 +275,104 @@ def tile_differentiablelogicmachine_pa_t_kernel(tc, x1, x2, W2, b2, out):
         transposed, grouped_of, codes_of, scales_of, sums, result_of = {}, {}, {}, {}, {}, {}
 
         def transposes(g):
-            stationaries = groups[g]["stationaries"]
-            for k in range(0, len(stationaries), 2):
-                xt = psum_t.tile([P, 4, P], F32)
-                for s, (a, c) in enumerate(stationaries[k : k + 2]):
-                    nc.tensor.transpose(out=xt[:, 2 * s, :], in_=xn_words[(a, c)], identity=ident[:])
-                    nc.tensor.transpose(out=xt[:, 2 * s + 1, :], in_=xp_words[(a, c)], identity=turn[:])
-                transposed[(g, k // 2)] = xt
+            a, cl = groups[g]["a"], groups[g]["cl"]
+            xt = psum_t.tile([P, 4, 2, 64], F32)
+            for gamma in range(2):
+                nc.tensor.transpose(
+                    out=xt[:, :, 0, 32 * gamma : 32 * gamma + 32], in_=x2_words[(a, gamma, cl)], identity=by_q[:]
+                )
+            for y in range(2):
+                nc.tensor.transpose(
+                    out=xt[:, 2 * y : 2 * y + 2, 1, :], in_=x2_words[(cl, y, a)], identity=by_partner[:]
+                )
+            transposed[g] = xt
 
         def exits(g):
-            stationaries = groups[g]["stationaries"]
-            for k in range(0, len(stationaries), 2):
-                count = len(stationaries[k : k + 2])
-                grouped = gpool.tile([P, 2, P, 2], F32, align_bytes=64)
-                words = transposed[(g, k // 2)][:, 0 : 2 * count, :].rearrange("p (s w) n -> p s n w", w=2)
-                if g >= VECTOR_HELPS_FROM and g % VECTOR_HELPS_EVERY == 0:
-                    nc.vector.tensor_copy(out=grouped[:, 0:count, :, :], in_=words)
-                else:
-                    nc.scalar.copy(out=grouped[:, 0:count, :, :], in_=words)
-                grouped_of[(g, k // 2)] = grouped
+            grouped = gpool.tile([P, 64, 4, 2], F32, align_bytes=64)
+            words = transposed[g][:].rearrange("p q w m -> p m q w")
+            if g >= VECTOR_HELPS_FROM and g % VECTOR_HELPS_EVERY == 0:
+                nc.vector.tensor_copy(out=grouped[:], in_=words)
+            else:
+                nc.scalar.copy(out=grouped[:], in_=words)
+            grouped_of[g] = grouped
 
         def quantise(g):
-            stationaries = groups[g]["stationaries"]
-            for k in range(0, len(stationaries), 2):
-                count = len(stationaries[k : k + 2])
-                codes = gpool.tile([P, 2 * P], U32, align_bytes=64)
-                scales = gpool.tile([P, 2 * P], U8, align_bytes=64)
-                nc.vector.quantize_mx(
-                    out=codes[:, 0 : count * P].bitcast(FP8X4),
-                    scales=scales[:, 0 : count * P],
-                    in_=grouped_of[(g, k // 2)][:, 0:count, :, :].rearrange("p s n w -> p (s n w)").bitcast(BF16),
-                )
-                codes_of[(g, k // 2)] = codes
-                scales_of[(g, k // 2)] = scales
+            codes = gpool.tile([P, 2 * P], U32, align_bytes=64)
+            scales = gpool.tile([P, 2 * P], U8, align_bytes=64)
+            nc.vector.quantize_mx(
+                out=codes[:].bitcast(FP8X4),
+                scales=scales[:],
+                in_=grouped_of[g][:].rearrange("p m q w -> p (m q w)").bitcast(BF16),
+            )
+            codes_of[g] = codes
+            scales_of[g] = scales
 
         def matmuls(g):
-            for i, bank in enumerate(groups[g]["banks"]):
-                ps = psum_o.tile([P, 2 * O], F32)
-                width = 2 * O if bank["wide"] else O
-                for q, (s, c) in enumerate(bank["parts"]):
-                    columns = slice((s % 2) * P, (s % 2 + 1) * P)
-                    nc.tensor.matmul_mx(
-                        out=ps[:, q * width : (q + 1) * width],
-                        lhsT=codes_of[(g, s // 2)][:, columns].bitcast(FP8X4),
-                        lhsT_scale=scales_of[(g, s // 2)][:, columns],
-                        rhs=w2_codes[:, 0:width].bitcast(FP8X4),
-                        rhs_scale=w2_scales[:, 0:width],
-                        start=True,
-                        stop=False,
-                    )
-                    nc.tensor.matmul_mx(
-                        out=ps[:, q * width : (q + 1) * width],
-                        lhsT=by_j_codes[:, by_j_block(c), :].bitcast(FP8X4),
-                        lhsT_scale=by_j_scales[:, by_j_block(c), :],
-                        rhs=w1_codes[:, 0:width].bitcast(FP8X4),
-                        rhs_scale=w1_scales[:, 0:width],
-                        start=False,
-                        stop=True,
-                    )
-                sums[(g, i)] = ps
+            wide = groups[g]["mirrored"] is not None
+            width = 2 * O if wide else O
+            for gamma in range(2):
+                if wide or gamma == 0:
+                    ps = psum_o.tile([P, 2 * O], F32)
+                    lo = 0
+                else:
+                    lo = O
+                c = by_j_block(8 * gamma + groups[g]["cl"])
+                nc.tensor.matmul_mx(
+                    out=ps[:, lo : lo + width],
+                    lhsT=codes_of[g][:, gamma * P : (gamma + 1) * P].bitcast(FP8X4),
+                    lhsT_scale=scales_of[g][:, gamma * P : (gamma + 1) * P],
+                    rhs=w2_codes[:, 0:width].bitcast(FP8X4),
+                    rhs_scale=w2_scales[:, 0:width],
+                    start=True,
+                    stop=False,
+                )
+                nc.tensor.matmul_mx(
+                    out=ps[:, lo : lo + width],
+                    lhsT=by_j_codes[:, c, :].bitcast(FP8X4),
+                    lhsT_scale=by_j_scales[:, c, :],
+                    rhs=w1_codes[:, 0:width].bitcast(FP8X4),
+                    rhs_scale=w1_scales[:, 0:width],
+                    start=False,
+                    stop=True,
+                )
+                sums[(g, gamma)] = ps
+
+        def result_slots(g):
+            group = groups[g]
+            view = result_of[g][:, 0 : 2 * group["size"], :].rearrange("p (g s) o -> p g s o", g=2)
+            if group["mirrored"] is None:
+                return view[:, :, group["direct"], :]
+            return view[:, :, group["direct"] : group["mirrored"] + 1 : group["mirrored"] - group["direct"], :]
 
         def add_row_terms(g):
-            if groups[g]["first"]:
-                result = rpool.tile([P, RESULT_SLOTS, O], F32)
-                result_of["now"] = result
+            group = groups[g]
+            if group["first"]:
+                tag = RESULT_TAGS[group["chunk"] % 3]
+                result_of["now"] = rpool.tile([P, RESULT_SLOTS[tag], O], F32, name=tag)
             result_of[g] = result_of["now"]
-            for i, bank in enumerate(groups[g]["banks"]):
-                a = bank["a"]
+            a = group["a"]
+            if group["mirrored"] is None:
                 nc.vector.tensor_tensor(
-                    out=result_of[g][:, bank["slots"], :],
-                    in0=sums[(g, i)][:].rearrange("p (s o) -> p s o", s=2),
-                    in1=row_term[:, a, :, :] if bank["wide"] else row_term[:, a : a + 2, 0, :],
+                    out=result_slots(g),
+                    in0=sums[(g, 0)][:].rearrange("p (s o) -> p s o", s=2),
+                    in1=row_term[:, a, 0, :].unsqueeze(1).to_broadcast([P, 2, O]),
+                    op=ADD,
+                )
+                return
+            for gamma in range(2):
+                nc.vector.tensor_tensor(
+                    out=result_slots(g)[:, gamma, :, :],
+                    in0=sums[(g, gamma)][:].rearrange("p (s o) -> p s o", s=2),
+                    in1=row_term[:, a, :, :],
                     op=ADD,
                 )
 
         def sigmoids_and_stores(g):
+            group = groups[g]
+            nc.scalar.activation(out=result_slots(g), in_=result_slots(g), func=SIGMOID)
             result = result_of[g]
-            for slots in groups[g]["sigmoids"]:
-                nc.scalar.activation(out=result[:, slots, :], in_=result[:, slots, :], func=SIGMOID)
-            size = groups[g]["size"]
-            for kind, major, lo, hi, s in groups[g]["stores"]:
+            size = group["size"]
+            for kind, major, lo, hi, s in group["stores"]:
                 if kind == "n":
                     nc.sync.dma_start(
                         out=out_n[major, :, :, lo * O : hi * O],
@@ -410,11 +381,14 @@ def tile_differentiablelogicmachine_pa_t_kernel(tc, x1, x2, W2, b2, out):
                         .rearrange("p g s o -> p g (s o)"),
                     )
                 else:
-                    for J in range(2):
-                        nc.sync.dma_start(
-                            out=out_p[major, J, :, :, lo * O : hi * O],
-                            in_=result[J:P:2, s : s + hi - lo, :].rearrange("p s o -> p (s o)"),
-                        )
+                    for gamma in range(2):
+                        for J in range(2):
+                            nc.sync.dma_start(
+                                out=out_p[8 * gamma + major, J, :, :, lo * O : hi * O],
+                                in_=result[J:P:2, gamma * size + s : gamma * size + s + hi - lo, :].rearrange(
+                                    "p s o -> p (s o)"
+                                ),
+                            )
 
         for n in range(n_groups + SIGMOID_STORE):
             if 0 <= n - SIGMOID_STORE < n_groups:

@@ -120,15 +120,12 @@ def tile_differentiablelogicmachine_pa_t_kernel(tc, x1, x2, W2, b2, out):
 
         ident = const.tile([P, P], F32)
         make_identity(nc, ident[:])
-        by_q = const.tile([P, P], F32)
-        nc.vector.tensor_copy(
-            out=by_q[:].rearrange("p (q m) -> p q m", q=4), in_=ident[:].rearrange("p (m q) -> p q m", q=4)
-        )
         by_partner = const.tile([P, P], F32)
-        nc.vector.tensor_copy(
-            out=by_partner[:].rearrange("p (j b x) -> p j b x", j=4, b=16, x=2),
-            in_=ident[:].rearrange("p (b j x) -> p j b x", b=16, j=4, x=2),
-        )
+        for gamma in range(2):
+            nc.vector.tensor_copy(
+                out=by_partner[:, 64 * gamma : 64 * gamma + 64].rearrange("p (b x J) -> p b x J", b=16, x=2, J=2),
+                in_=ident[:].rearrange("p (b J g x) -> p g b x J", b=16, J=2, g=2, x=2)[:, gamma, :, :, :],
+            )
         ones = const.tile([P, P], BF16)
         nc.vector.memset(ones[:], 1.0)
         warm_in = const.tile([P, 1], F32)
@@ -276,20 +273,20 @@ def tile_differentiablelogicmachine_pa_t_kernel(tc, x1, x2, W2, b2, out):
 
         def transposes(g):
             a, cl = groups[g]["a"], groups[g]["cl"]
-            xt = psum_t.tile([P, 4, 2, 64], F32)
+            xt = psum_t.tile([P, 2, 2, 32, 2, 2], F32)
             for gamma in range(2):
                 nc.tensor.transpose(
-                    out=xt[:, :, 0, 32 * gamma : 32 * gamma + 32], in_=x2_words[(a, gamma, cl)], identity=by_q[:]
+                    out=xt[:, gamma, 0, :, :, :].rearrange("p m y J -> p (m y J)"),
+                    in_=x2_words[(a, gamma, cl)],
+                    identity=ident[:],
                 )
             for y in range(2):
-                nc.tensor.transpose(
-                    out=xt[:, 2 * y : 2 * y + 2, 1, :], in_=x2_words[(cl, y, a)], identity=by_partner[:]
-                )
+                nc.tensor.transpose(out=xt[:, :, 1, :, y, :], in_=x2_words[(cl, y, a)], identity=by_partner[:])
             transposed[g] = xt
 
         def exits(g):
-            grouped = gpool.tile([P, 64, 4, 2], F32, align_bytes=64)
-            words = transposed[g][:].rearrange("p q w m -> p m q w")
+            grouped = gpool.tile([P, 2, P, 2], F32, align_bytes=64)
+            words = transposed[g][:].rearrange("p g w m y J -> p g (m y J) w")
             if g >= VECTOR_HELPS_FROM and g % VECTOR_HELPS_EVERY == 0:
                 nc.vector.tensor_copy(out=grouped[:], in_=words)
             else:
@@ -302,7 +299,7 @@ def tile_differentiablelogicmachine_pa_t_kernel(tc, x1, x2, W2, b2, out):
             nc.vector.quantize_mx(
                 out=codes[:].bitcast(FP8X4),
                 scales=scales[:],
-                in_=grouped_of[g][:].rearrange("p m q w -> p (m q w)").bitcast(BF16),
+                in_=grouped_of[g][:].rearrange("p g n w -> p (g n w)").bitcast(BF16),
             )
             codes_of[g] = codes
             scales_of[g] = scales

@@ -5,7 +5,6 @@ from concourse.masks import make_identity
 
 F32 = mybir.dt.float32
 BF16 = mybir.dt.bfloat16
-I32 = mybir.dt.int32
 U32 = mybir.dt.uint32
 U8 = mybir.dt.uint8
 FP8X4 = mybir.dt.float8_e4m3fn_x4
@@ -18,69 +17,63 @@ FLOPS = 2 * 16 * 32 * 32 * 1024 * 256
 
 EXIT = 1
 QUANTISE = 2
-MATMUL = 3
-BIAS_ADD = 4
-SIGMOID_STORE = 5
-VECTOR_HELPS_FROM = 18
-VECTOR_HELPS_EVERY = 4
-RESULT_TAGS = ("result_a", "result_b", "result_c")
-RESULT_SLOTS = dict(result_a=24, result_b=32, result_c=16)
+MATMUL = 6
+BIAS_ADD = 7
+SIGMOID_STORE = 8
+SLOTS = 16
 
 
 def by_j_block(c):
     return (c % 8 // 2) * 4 + (c // 8) * 2 + c % 2
 
 
-def make_groups():
-    groups = []
-    n_chunks = 0
-    for C in (3, 2, 1, 0):
-        split = C if C >= 2 else 0
-        for a_lo, a_hi, last in ((0, split, False), (split, 2 * C, True)):
-            if a_hi == a_lo and not last:
-                continue
-            n = a_hi - a_lo
-            base = 2 * n + (3 if last else 0)
-            size = 4 * n + (4 if last else 0)
-            cl0 = 2 * C
-            cl1 = cl0 + 1
-            chunk = []
-            for a in range(a_lo, a_hi):
-                t = a - a_lo
-                chunk.append(dict(a=a, cl=cl0, direct=2 * t, mirrored=base + t, stores=[]))
-                chunk.append(
-                    dict(a=a, cl=cl1, direct=2 * t + 1, mirrored=base + n + t, stores=[("n", a, cl0, cl1 + 1, 2 * t)])
-                )
-            if n > 0:
-                chunk[-2]["stores"].append(("p", cl0, a_lo, a_hi, base))
-            if last:
-                chunk.append(dict(a=cl0, cl=cl0, direct=2 * n, mirrored=None, stores=[]))
-                chunk.append(
-                    dict(
-                        a=cl0,
-                        cl=cl1,
-                        direct=2 * n + 1,
-                        mirrored=base + 2 * n,
-                        stores=[("n", cl0, cl0, cl1 + 1, 2 * n), ("p", cl1, a_lo, cl0 + 1, base + n)],
-                    )
-                )
-                chunk.append(dict(a=cl1, cl=cl1, direct=2 * n + 2, mirrored=None, stores=[("n", cl1, cl1, cl1 + 1, 2 * n + 2)]))
-            else:
-                chunk[-1]["stores"].append(("p", cl1, a_lo, a_hi, base + n))
-            for k, group in enumerate(chunk):
-                group["size"] = size
-                group["first"] = k == 0
-                group["chunk"] = n_chunks
-            n_chunks += 1
-            groups.extend(chunk)
+def chunk_of(order, direct, mirrored, pieces, tag):
+    groups = [dict(a=a, cl=cl, tag=tag, direct=direct[(a, cl)], mirrored=mirrored.get((a, cl)), stores=[]) for a, cl in order]
+    groups[0]["first"] = True
+    for kind, members in pieces:
+        last = max(order.index(pair) for pair in members)
+        groups[last]["stores"].append((kind, members, (direct if kind == "n" else mirrored)[members[0]]))
     return groups
+
+
+def triangle(lo, descending, tag):
+    rows = {r: [(lo + r, lo + c) for c in range(r, 4)] for r in range(4)}
+    columns = {c: [(lo + r, lo + c) for r in range(c)] for c in range(4)}
+    direct = {pair: k for k, pair in enumerate(rows[0] + rows[1] + rows[2] + rows[3])}
+    mirrored = {pair: len(direct) + k for k, pair in enumerate(columns[1] + columns[2] + columns[3])}
+    pieces = [("p", columns[c]) for c in (1, 2, 3)]
+    pieces += [("n", rows[0][0:2]), ("n", rows[0][2:4]), ("n", rows[1][0:1]), ("n", rows[1][1:3]), ("n", rows[2]), ("n", rows[3])]
+    if descending:
+        order = columns[3] + columns[2] + rows[2][0:1] + rows[3] + columns[1] + rows[0][0:1] + rows[1][0:1]
+    else:
+        order = [pair for c in range(4) for pair in columns[c] + rows[c][0:1]]
+    return chunk_of(order, direct, mirrored, pieces, tag)
+
+
+def rectangle(cl_lo, tag):
+    rows = [[(a, cl_lo), (a, cl_lo + 1)] for a in range(4)]
+    columns = [[(a, cl) for a in range(4)] for cl in (cl_lo, cl_lo + 1)]
+    direct = {pair: k for k, pair in enumerate(rows[0] + rows[1] + rows[2] + rows[3])}
+    mirrored = {pair: len(direct) + k for k, pair in enumerate(columns[0] + columns[1])}
+    pieces = [("n", row) for row in rows] + [("p", column) for column in columns]
+    return chunk_of(columns[0] + columns[1], direct, mirrored, pieces, tag)
+
+
+def make_groups():
+    return (
+        triangle(0, False, "result_a")
+        + rectangle(4, "result_b")
+        + rectangle(6, "result_c")
+        + triangle(4, True, "result_a")
+    )
 
 
 def tile_differentiablelogicmachine_pa_t_kernel(tc, x1, x2, W2, b2, out):
     nc = tc.nc
     with ExitStack() as ctx:
         const = ctx.enter_context(tc.tile_pool(name="const", bufs=1))
-        gpool = ctx.enter_context(tc.tile_pool(name="gpool", bufs=6))
+        gpool = ctx.enter_context(tc.tile_pool(name="gpool", bufs=4))
+        cpool = ctx.enter_context(tc.tile_pool(name="cpool", bufs=7))
         upool = ctx.enter_context(tc.tile_pool(name="upool", bufs=2))
         rpool = ctx.enter_context(tc.tile_pool(name="rpool", bufs=1))
         psum_t = ctx.enter_context(tc.psum_pool(name="psum_t", bufs=3))
@@ -90,10 +83,12 @@ def tile_differentiablelogicmachine_pa_t_kernel(tc, x1, x2, W2, b2, out):
 
         x1_rows = const.tile([P, 4, O], BF16)
         nc.sync.dma_start(out=x1_rows[:], in_=x1.rearrange("b (q r) c -> (b q) r c", r=4))
-        w_rows = const.tile([P, 5, 2, O], BF16)
         w_view = W2.rearrange("(k p e) o -> p k e o", k=4, p=P, e=2)
-        nc.sync.dma_start(out=w_rows[:, 0:4, :, :], in_=w_view)
-        nc.sync.dma_start(out=w_rows[:, 4:5, :, :], in_=w_view[:, 1:2, :, :])
+        w_rows_x2 = const.tile([P, 3, 2, O], BF16)
+        w_rows_x1 = const.tile([P, 2, 2, O], BF16)
+        nc.sync.dma_start(out=w_rows_x2[:, 0:2, :, :], in_=w_view[:, 1:4:2, :, :])
+        nc.sync.dma_start(out=w_rows_x2[:, 2:3, :, :], in_=w_view[:, 1:2, :, :])
+        nc.sync.dma_start(out=w_rows_x1[:], in_=w_view[:, 0:3:2, :, :])
         bias_row = const.tile([P, O], BF16)
         nc.vector.memset(bias_row[:], 0.0)
         nc.sync.dma_start(out=bias_row[0:1, :], in_=b2.rearrange("(a o) -> a o", a=1))
@@ -112,54 +107,41 @@ def tile_differentiablelogicmachine_pa_t_kernel(tc, x1, x2, W2, b2, out):
                 for c in range(4):
                     x2_words[(a, gamma, 4 * half + c)] = rows[:, gamma, c, :].bitcast(F32)
 
-        for a, half in (
-            (6, 0), (0, 1), (7, 0), (1, 1), (2, 1), (3, 1), (6, 1), (4, 1), (7, 1), (5, 1),
-            (4, 0), (5, 0), (2, 0), (3, 0), (0, 0), (1, 0),
-        ):
+        for a, half in ((0, 0), (1, 0), (2, 0), (3, 0), (4, 0), (0, 1), (1, 1), (2, 1), (3, 1), (5, 0)):
             load_x2(a, half)
+        later_loads = {3: (6, 0), 5: (7, 0), 9: (7, 1), 10: (4, 1), 11: (5, 1), 12: (6, 1)}
 
         ident = const.tile([P, P], F32)
         make_identity(nc, ident[:])
+        warm_in = const.tile([P, 1], F32)
+        nc.vector.memset(warm_in[:], 0.0)
+        warm_out = const.tile([P, 1], F32)
+        nc.scalar.activation(out=warm_out[:], in_=warm_in[:], func=SIGMOID)
+        x1_words = const.tile([P, 2, 4, 16, 8], F32)
+        nc.vector.memset(x1_words[:, 1, :, :, :], 0.0)
+        w2_grouped = const.tile([P, 2, O, 2, 2], BF16, align_bytes=64, name="w2_grouped")
+        w1_grouped = const.tile([P, 2, O, 2, 2], BF16, align_bytes=64, name="w1_grouped")
+        nc.vector.memset(w1_grouped[:], 0.0)
+        ones = const.tile([P, P], BF16)
+        nc.vector.memset(ones[:], 1.0)
         by_partner = const.tile([P, P], F32)
         for gamma in range(2):
             nc.vector.tensor_copy(
                 out=by_partner[:, 64 * gamma : 64 * gamma + 64].rearrange("p (b x J) -> p b x J", b=16, x=2, J=2),
                 in_=ident[:].rearrange("p (b J g x) -> p g b x J", b=16, J=2, g=2, x=2)[:, gamma, :, :, :],
             )
-        ones = const.tile([P, P], BF16)
-        nc.vector.memset(ones[:], 1.0)
-        warm_in = const.tile([P, 1], F32)
-        nc.vector.memset(warm_in[:], 0.0)
-        warm_out = const.tile([P, 1], F32)
-        nc.scalar.activation(out=warm_out[:], in_=warm_in[:], func=SIGMOID)
-        w1_grouped = const.tile([P, 2, O, 2, 2], BF16, align_bytes=64)
-        nc.vector.memset(w1_grouped[:], 0.0)
-        x1_words = const.tile([P, 2, 4, 16, 8], F32)
-        nc.vector.memset(x1_words[:, 1, :, :, :], 0.0)
 
-        w2_grouped = const.tile([P, 2, O, 2, 2], BF16, align_bytes=64)
-        nc.scalar.copy(out=w2_grouped[:, 0, :, :, :], in_=w_rows[:, 1:4:2, :, :].rearrange("p s e o -> p o s e"))
-        nc.scalar.copy(out=w2_grouped[:, 1, :, :, :], in_=w_rows[:, 3:5, :, :].rearrange("p s e o -> p o s e"))
         w2_codes = const.tile([P, 2 * O], U32, align_bytes=64)
         w2_scales = const.tile([P, 2 * O], U8, align_bytes=64)
         w1_codes = const.tile([P, 2 * O], U32, align_bytes=64)
         w1_scales = const.tile([P, 2 * O], U8, align_bytes=64)
-
-        x1_t = psum_t.tile([P, 4, P], F32, name="xt")
-        for r in range(4):
-            nc.tensor.transpose(out=x1_t[:, r, :], in_=x1_rows[:, r, :].bitcast(F32), identity=ident[:])
-        nc.vector.tensor_copy(
-            out=x1_words[:, 0, :, :, :].rearrange("p r b q -> p (r b q)"), in_=x1_t[:].rearrange("p r n -> p (r n)")
-        )
-        bias_psum = psum_r.tile([P, 2 * O], F32, name="rp")
-        nc.tensor.matmul(out=bias_psum[:, 0:O], lhsT=ones[:], rhs=bias_row[:], start=True, stop=True)
-        bias = const.tile([P, O], F32)
-
         by_j_codes = const.tile([P, 16, P], U32, align_bytes=64)
         by_j_scales = const.tile([P, 16, P], U8, align_bytes=64)
         by_i_codes = const.tile([P, 8, P], U32, align_bytes=64)
         by_i_scales = const.tile([P, 8, P], U8, align_bytes=64)
-        row_term = const.tile([P, 8, 2, O], F32)
+        bias = const.tile([P, O], F32)
+        row_low = const.tile([P, 4, 2, O], F32)
+        row_terms = {a: row_low[:, a, :, :] for a in range(4)}
         repeated, row_psum = {}, {}
 
         def copy_on(engine, target, source):
@@ -224,46 +206,68 @@ def tile_differentiablelogicmachine_pa_t_kernel(tc, x1, x2, W2, b2, out):
             row_psum[a] = rp
 
         def row_add_bias(a):
+            if a == 4:
+                row_high = const.tile([P, 2, 2, O], F32, align_bytes=64, name="w2_grouped")
+                row_terms[4] = row_high[:, 0, :, :]
+                row_terms[5] = row_high[:, 1, :, :]
+            if a == 6:
+                row_high = const.tile([P, 2, 2, O], F32, align_bytes=64, name="w1_grouped")
+                row_terms[6] = row_high[:, 0, :, :]
+                row_terms[7] = row_high[:, 1, :, :]
             nc.vector.tensor_tensor(
-                out=row_term[:, a, :, :],
+                out=row_terms[a],
                 in0=row_psum[a][:].rearrange("p (s o) -> p s o", s=2),
                 in1=bias[:].unsqueeze(1).to_broadcast([P, 2, O]),
                 op=ADD,
             )
 
+        x1_t = psum_t.tile([P, 4, P], F32, name="xt")
+        for r in range(4):
+            nc.tensor.transpose(out=x1_t[:, r, :], in_=x1_rows[:, r, :].bitcast(F32), identity=ident[:])
+        nc.scalar.copy(
+            out=x1_words[:, 0, :, :, :].rearrange("p r b q -> p (r b q)"), in_=x1_t[:].rearrange("p r n -> p (r n)")
+        )
+        repeat_by_j(0, "scalar")
+        repeat_by_i(0, "scalar")
         for x in range(2):
-            nc.scalar.copy(out=w1_grouped[:, x, :, 0, :], in_=w_rows[:, 2 - 2 * x, :, :].rearrange("p e o -> p o e"))
-        repeat_by_j(3, "vector")
-        repeat_by_i(0, "vector")
+            nc.vector.tensor_copy(
+                out=w2_grouped[:, x, :, :, :], in_=w_rows_x2[:, x : x + 2, :, :].rearrange("p s e o -> p o s e")
+            )
+        for x in range(2):
+            nc.vector.tensor_copy(
+                out=w1_grouped[:, x, :, 0, :], in_=w_rows_x1[:, 1 - x, :, :].rearrange("p e o -> p o e")
+            )
         nc.vector.quantize_mx(
             out=w2_codes[:].bitcast(FP8X4),
             scales=w2_scales[:],
             in_=w2_grouped[:].rearrange("p x o s e -> p (x o s e)"),
         )
-        quantise_by_j(3)
-        quantise_by_i(0)
-        nc.vector.tensor_copy(out=bias[:], in_=bias_psum[:, 0:O])
+        quantise_by_j(0)
         nc.vector.quantize_mx(
             out=w1_codes[:].bitcast(FP8X4),
             scales=w1_scales[:],
             in_=w1_grouped[:].rearrange("p x o s e -> p (x o s e)"),
         )
+        quantise_by_i(0)
+        bias_psum = psum_r.tile([P, 2 * O], F32, name="rp")
+        nc.tensor.matmul(out=bias_psum[:, 0:O], lhsT=ones[:], rhs=bias_row[:], start=True, stop=True)
+        nc.scalar.copy(out=bias[:], in_=bias_psum[:, 0:O])
 
         early, late = {}, {}
-        for a in range(8):
-            late.setdefault(min(2 * a + 2, a + 7), []).append(("row_matmul", a))
-            early.setdefault(min(2 * a + 3, a + 8), []).append(("row_add_bias", a))
-        late.setdefault(5, []).append(("repeat_by_i", 1))
-        late.setdefault(6, []).append(("quantise_by_i", 1))
-        for u, n in ((2, 11), (1, 19), (0, 23)):
+        for a, n in enumerate((5, 7, 9, 12, 22, 25, 28, 31)):
+            late.setdefault(n, []).append(("row_matmul", a))
+            early.setdefault(n + 1, []).append(("row_add_bias", a))
+        for u, n in ((1, 4), (2, 10), (3, 17)):
             late.setdefault(n, []).append(("repeat_by_j", u))
             late.setdefault(n + 1, []).append(("quantise_by_j", u))
+        late.setdefault(20, []).append(("repeat_by_i", 1))
+        late.setdefault(21, []).append(("quantise_by_i", 1))
         pieces = dict(
             row_matmul=row_matmul,
             row_add_bias=row_add_bias,
-            repeat_by_i=lambda u: repeat_by_i(u, "scalar"),
+            repeat_by_i=lambda u: repeat_by_i(u, "vector"),
             quantise_by_i=quantise_by_i,
-            repeat_by_j=lambda u: repeat_by_j(u, "scalar"),
+            repeat_by_j=lambda u: repeat_by_j(u, "vector"),
             quantise_by_j=quantise_by_j,
         )
 
@@ -286,16 +290,12 @@ def tile_differentiablelogicmachine_pa_t_kernel(tc, x1, x2, W2, b2, out):
 
         def exits(g):
             grouped = gpool.tile([P, 2, P, 2], F32, align_bytes=64)
-            words = transposed[g][:].rearrange("p g w m y J -> p g (m y J) w")
-            if g >= VECTOR_HELPS_FROM and g % VECTOR_HELPS_EVERY == 0:
-                nc.vector.tensor_copy(out=grouped[:], in_=words)
-            else:
-                nc.scalar.copy(out=grouped[:], in_=words)
+            nc.scalar.copy(out=grouped[:], in_=transposed[g][:].rearrange("p g w m y J -> p g (m y J) w"))
             grouped_of[g] = grouped
 
         def quantise(g):
-            codes = gpool.tile([P, 2 * P], U32, align_bytes=64)
-            scales = gpool.tile([P, 2 * P], U8, align_bytes=64)
+            codes = cpool.tile([P, 2 * P], U32, align_bytes=64)
+            scales = cpool.tile([P, 2 * P], U8, align_bytes=64)
             nc.vector.quantize_mx(
                 out=codes[:].bitcast(FP8X4),
                 scales=scales[:],
@@ -335,24 +335,23 @@ def tile_differentiablelogicmachine_pa_t_kernel(tc, x1, x2, W2, b2, out):
                 sums[(g, gamma)] = ps
 
         def result_slots(g):
-            group = groups[g]
-            view = result_of[g][:, 0 : 2 * group["size"], :].rearrange("p (g s) o -> p g s o", g=2)
-            if group["mirrored"] is None:
-                return view[:, :, group["direct"], :]
-            return view[:, :, group["direct"] : group["mirrored"] + 1 : group["mirrored"] - group["direct"], :]
+            direct, mirrored = groups[g]["direct"], groups[g]["mirrored"]
+            view = result_of[g][:].rearrange("p (g s) o -> p g s o", g=2)
+            if mirrored is None:
+                return view[:, :, direct, :]
+            return view[:, :, direct : mirrored + 1 : mirrored - direct, :]
 
         def add_row_terms(g):
             group = groups[g]
-            if group["first"]:
-                tag = RESULT_TAGS[group["chunk"] % 3]
-                result_of["now"] = rpool.tile([P, RESULT_SLOTS[tag], O], F32, name=tag)
+            if group.get("first"):
+                result_of["now"] = rpool.tile([P, 2 * SLOTS, O], F32, name=group["tag"])
             result_of[g] = result_of["now"]
             a = group["a"]
             if group["mirrored"] is None:
                 nc.vector.tensor_tensor(
                     out=result_slots(g),
                     in0=sums[(g, 0)][:].rearrange("p (s o) -> p s o", s=2),
-                    in1=row_term[:, a, 0, :].unsqueeze(1).to_broadcast([P, 2, O]),
+                    in1=row_terms[a][:, 0, :].unsqueeze(1).to_broadcast([P, 2, O]),
                     op=ADD,
                 )
                 return
@@ -360,36 +359,37 @@ def tile_differentiablelogicmachine_pa_t_kernel(tc, x1, x2, W2, b2, out):
                 nc.vector.tensor_tensor(
                     out=result_slots(g)[:, gamma, :, :],
                     in0=sums[(g, gamma)][:].rearrange("p (s o) -> p s o", s=2),
-                    in1=row_term[:, a, :, :],
+                    in1=row_terms[a],
                     op=ADD,
                 )
 
         def sigmoids_and_stores(g):
-            group = groups[g]
             nc.scalar.activation(out=result_slots(g), in_=result_slots(g), func=SIGMOID)
             result = result_of[g]
-            size = group["size"]
-            for kind, major, lo, hi, s in group["stores"]:
+            for kind, members, s in groups[g]["stores"]:
                 if kind == "n":
+                    major, lo, hi = members[0][0], members[0][1], members[-1][1] + 1
                     nc.sync.dma_start(
                         out=out_n[major, :, :, lo * O : hi * O],
-                        in_=result[:, 0 : 2 * size, :]
+                        in_=result[:]
                         .rearrange("p (g s) o -> p g s o", g=2)[:, :, s : s + hi - lo, :]
                         .rearrange("p g s o -> p g (s o)"),
                     )
                 else:
+                    major, lo, hi = members[0][1], members[0][0], members[-1][0] + 1
                     for gamma in range(2):
+                        first = gamma * SLOTS + s
                         for J in range(2):
                             nc.sync.dma_start(
                                 out=out_p[8 * gamma + major, J, :, :, lo * O : hi * O],
-                                in_=result[J:P:2, gamma * size + s : gamma * size + s + hi - lo, :].rearrange(
-                                    "p s o -> p (s o)"
-                                ),
+                                in_=result[J:P:2, first : first + hi - lo, :].rearrange("p s o -> p (s o)"),
                             )
 
         for n in range(n_groups + SIGMOID_STORE):
             if 0 <= n - SIGMOID_STORE < n_groups:
                 sigmoids_and_stores(n - SIGMOID_STORE)
+                if n - SIGMOID_STORE in later_loads:
+                    load_x2(later_loads[n - SIGMOID_STORE][0], later_loads[n - SIGMOID_STORE][1])
             if 0 <= n - BIAS_ADD < n_groups:
                 add_row_terms(n - BIAS_ADD)
             if 0 <= n - MATMUL < n_groups:

@@ -17,9 +17,9 @@ FLOPS = 2 * 16 * 32 * 32 * 1024 * 256
 
 EXIT = 1
 QUANTISE = 2
-MATMUL = 6
-BIAS_ADD = 7
-SIGMOID_STORE = 8
+MATMUL = 3
+BIAS_ADD = 4
+SIGMOID_STORE = 5
 SLOTS = 16
 
 
@@ -76,9 +76,8 @@ def tile_differentiablelogicmachine_pa_t_kernel(tc, x1, x2, W2, b2, out):
         cpool = ctx.enter_context(tc.tile_pool(name="cpool", bufs=7))
         upool = ctx.enter_context(tc.tile_pool(name="upool", bufs=2))
         rpool = ctx.enter_context(tc.tile_pool(name="rpool", bufs=1))
-        psum_t = ctx.enter_context(tc.psum_pool(name="psum_t", bufs=3))
+        psum_t = ctx.enter_context(tc.psum_pool(name="psum_t", bufs=4))
         psum_o = ctx.enter_context(tc.psum_pool(name="psum_o", bufs=4))
-        psum_r = ctx.enter_context(tc.psum_pool(name="psum_r", bufs=1))
         ctx.enter_context(tc.manual_schedule())
 
         x1_rows = const.tile([P, 4, O], BF16)
@@ -192,7 +191,7 @@ def tile_differentiablelogicmachine_pa_t_kernel(tc, x1, x2, W2, b2, out):
             )
 
         def row_matmul(a):
-            rp = psum_r.tile([P, 2 * O], F32)
+            rp = psum_o.tile([P, 2 * O], F32, name="ps")
             for s in range(2):
                 nc.tensor.matmul_mx(
                     out=rp[:, s * O : (s + 1) * O],
@@ -249,27 +248,13 @@ def tile_differentiablelogicmachine_pa_t_kernel(tc, x1, x2, W2, b2, out):
             in_=w1_grouped[:].rearrange("p x o s e -> p (x o s e)"),
         )
         quantise_by_i(0)
-        bias_psum = psum_r.tile([P, 2 * O], F32, name="rp")
+        bias_psum = psum_o.tile([P, 2 * O], F32, name="ps")
         nc.tensor.matmul(out=bias_psum[:, 0:O], lhsT=ones[:], rhs=bias_row[:], start=True, stop=True)
         nc.scalar.copy(out=bias[:], in_=bias_psum[:, 0:O])
 
-        early, late = {}, {}
-        for a, n in enumerate((5, 7, 9, 12, 22, 25, 28, 31)):
-            late.setdefault(n, []).append(("row_matmul", a))
-            early.setdefault(n + 1, []).append(("row_add_bias", a))
-        for u, n in ((1, 4), (2, 10), (3, 17)):
-            late.setdefault(n, []).append(("repeat_by_j", u))
-            late.setdefault(n + 1, []).append(("quantise_by_j", u))
-        late.setdefault(20, []).append(("repeat_by_i", 1))
-        late.setdefault(21, []).append(("quantise_by_i", 1))
-        pieces = dict(
-            row_matmul=row_matmul,
-            row_add_bias=row_add_bias,
-            repeat_by_i=lambda u: repeat_by_i(u, "vector"),
-            quantise_by_i=quantise_by_i,
-            repeat_by_j=lambda u: repeat_by_j(u, "vector"),
-            quantise_by_j=quantise_by_j,
-        )
+        row_terms_in = {3: 0, 4: 1, 5: 2, 6: 3, 11: 4, 13: 5, 14: 6, 16: 7}
+        repeats_in = {1: 1, 4: 2, 8: 3}
+        quantises_in = {2: 1, 5: 2, 9: 3}
 
         groups = make_groups()
         n_groups = len(groups)
@@ -385,22 +370,35 @@ def tile_differentiablelogicmachine_pa_t_kernel(tc, x1, x2, W2, b2, out):
                                 in_=result[J:P:2, first : first + hi - lo, :].rearrange("p s o -> p (s o)"),
                             )
 
-        for n in range(n_groups + SIGMOID_STORE):
-            if 0 <= n - SIGMOID_STORE < n_groups:
-                sigmoids_and_stores(n - SIGMOID_STORE)
-                if n - SIGMOID_STORE in later_loads:
-                    load_x2(later_loads[n - SIGMOID_STORE][0], later_loads[n - SIGMOID_STORE][1])
-            if 0 <= n - BIAS_ADD < n_groups:
-                add_row_terms(n - BIAS_ADD)
-            if 0 <= n - MATMUL < n_groups:
-                matmuls(n - MATMUL)
-            if 0 <= n - QUANTISE < n_groups:
-                quantise(n - QUANTISE)
-            for name, arg in early.get(n, []):
-                pieces[name](arg)
-            if 0 <= n - EXIT < n_groups:
-                exits(n - EXIT)
-            if n < n_groups:
-                transposes(n)
-            for name, arg in late.get(n, []):
-                pieces[name](arg)
+        def in_range(p):
+            return [g for g in (2 * p, 2 * p + 1) if 0 <= g < n_groups]
+
+        for p in range(n_groups // 2 + SIGMOID_STORE):
+            for g in in_range(p):
+                transposes(g)
+            for e in range(2):
+                for g in in_range(p - SIGMOID_STORE)[e : e + 1]:
+                    sigmoids_and_stores(g)
+                    if g in later_loads:
+                        load_x2(later_loads[g][0], later_loads[g][1])
+                for g in in_range(p - BIAS_ADD)[e : e + 1]:
+                    add_row_terms(g)
+                for g in in_range(p - QUANTISE)[e : e + 1]:
+                    quantise(g)
+                if p in row_terms_in:
+                    if e == 0:
+                        row_matmul(row_terms_in[p])
+                    else:
+                        row_add_bias(row_terms_in[p])
+                for g in in_range(p - EXIT)[e : e + 1]:
+                    exits(g)
+            for g in in_range(p - MATMUL):
+                matmuls(g)
+            if p in repeats_in:
+                repeat_by_j(repeats_in[p], "vector")
+            if p in quantises_in:
+                quantise_by_j(quantises_in[p])
+            if p == 9:
+                repeat_by_i(1, "vector")
+            if p == 10:
+                quantise_by_i(1)

@@ -42,10 +42,11 @@ def triangle(lo, descending, tag):
     direct = {pair: k for k, pair in enumerate(rows[0] + rows[1] + rows[2] + rows[3])}
     mirrored = {pair: len(direct) + k for k, pair in enumerate(columns[1] + columns[2] + columns[3])}
     pieces = [("p", columns[c]) for c in (1, 2, 3)]
-    pieces += [("n", rows[0][0:2]), ("n", rows[0][2:4]), ("n", rows[1][0:1]), ("n", rows[1][1:3]), ("n", rows[2]), ("n", rows[3])]
     if descending:
+        pieces += [("n", rows[0][0:2]), ("n", rows[0][2:4]), ("n", rows[1][0:1]), ("n", rows[1][1:3]), ("n", rows[2]), ("n", rows[3])]
         order = columns[3] + columns[2] + rows[2][0:1] + rows[3] + columns[1] + rows[0][0:1] + rows[1][0:1]
     else:
+        pieces += [("n", rows[r]) for r in range(4)]
         order = [pair for c in range(4) for pair in columns[c] + rows[c][0:1]]
     return chunk_of(order, direct, mirrored, pieces, tag)
 
@@ -83,10 +84,9 @@ def tile_differentiablelogicmachine_pa_t_kernel(tc, x1, x2, W2, b2, out):
         x1_rows = const.tile([P, 4, O], BF16)
         nc.sync.dma_start(out=x1_rows[:], in_=x1.rearrange("b (q r) c -> (b q) r c", r=4))
         w_view = W2.rearrange("(k p e) o -> p k e o", k=4, p=P, e=2)
-        w_rows_x2 = const.tile([P, 3, 2, O], BF16)
+        w_rows_x2 = const.tile([P, 2, 2, O], BF16)
         w_rows_x1 = const.tile([P, 2, 2, O], BF16)
-        nc.sync.dma_start(out=w_rows_x2[:, 0:2, :, :], in_=w_view[:, 1:4:2, :, :])
-        nc.sync.dma_start(out=w_rows_x2[:, 2:3, :, :], in_=w_view[:, 1:2, :, :])
+        nc.sync.dma_start(out=w_rows_x2[:], in_=w_view[:, 1:4:2, :, :])
         nc.sync.dma_start(out=w_rows_x1[:], in_=w_view[:, 0:3:2, :, :])
         bias_row = const.tile([P, O], BF16)
         nc.vector.memset(bias_row[:], 0.0)
@@ -94,21 +94,27 @@ def tile_differentiablelogicmachine_pa_t_kernel(tc, x1, x2, W2, b2, out):
 
         x2_words = {}
         x2_view = x2.rearrange("b (I a) (G c) k -> a (b I) G (c k)", I=4, a=8, G=4, c=8)
+        x2_whole = x2.rearrange("b (I a) (J m) k -> a (b I) J (m k)", I=4, a=8, J=2, m=16)
         out_n = out.rearrange("b (I a) (G c) o -> a (b I) G (c o)", I=4, a=8, G=4, c=8)
         out_p = out.rearrange("b (J c) (I a) o -> c J b I (a o)", J=2, c=16, I=4, a=8)
 
-        def load_x2(a, half):
-            rows = const.tile([P, 2, 4, O], BF16, name="x2_%d_%d" % (a, half))
-            nc.sync.dma_start(
-                out=rows[:].rearrange("p g c k -> p g (c k)"), in_=x2_view[a, :, :, half * 4 * O : (half + 1) * 4 * O]
-            )
+        def load_x2(a, lo, hi):
+            rows = const.tile([P, 2, hi - lo, O], BF16, name="x2_%d_%d" % (a, lo))
+            if hi - lo == 8:
+                nc.sync.dma_start(out=rows[:].rearrange("p g c k -> p (g c k)"), in_=x2_whole[a])
+            else:
+                nc.sync.dma_start(out=rows[:].rearrange("p g c k -> p g (c k)"), in_=x2_view[a, :, :, lo * O : hi * O])
             for gamma in range(2):
-                for c in range(4):
-                    x2_words[(a, gamma, 4 * half + c)] = rows[:, gamma, c, :].bitcast(F32)
+                for cl in range(lo, hi):
+                    x2_words[(a, gamma, cl)] = rows[:, gamma, cl - lo, :].bitcast(F32)
 
-        for a, half in ((0, 0), (1, 0), (2, 0), (3, 0), (4, 0), (0, 1), (1, 1), (2, 1), (3, 1), (5, 0)):
-            load_x2(a, half)
-        later_loads = {3: (6, 0), 5: (7, 0), 9: (7, 1), 10: (4, 1), 11: (5, 1), 12: (6, 1)}
+        for a in range(4):
+            load_x2(a, 0, 4)
+        load_x2(4, 0, 8)
+        for a in range(4):
+            load_x2(a, 4, 8)
+        for a in (5, 6, 7):
+            load_x2(a, 0, 8)
 
         ident = const.tile([P, P], F32)
         make_identity(nc, ident[:])
@@ -230,7 +236,8 @@ def tile_differentiablelogicmachine_pa_t_kernel(tc, x1, x2, W2, b2, out):
         repeat_by_i(0, "scalar")
         for x in range(2):
             nc.vector.tensor_copy(
-                out=w2_grouped[:, x, :, :, :], in_=w_rows_x2[:, x : x + 2, :, :].rearrange("p s e o -> p o s e")
+                out=w2_grouped[:, x, :, :, :],
+                in_=(w_rows_x2[:, ::-1, :, :] if x == 1 else w_rows_x2[:]).rearrange("p s e o -> p o s e"),
             )
         for x in range(2):
             nc.vector.tensor_copy(
@@ -379,8 +386,6 @@ def tile_differentiablelogicmachine_pa_t_kernel(tc, x1, x2, W2, b2, out):
             for e in range(2):
                 for g in in_range(p - SIGMOID_STORE)[e : e + 1]:
                     sigmoids_and_stores(g)
-                    if g in later_loads:
-                        load_x2(later_loads[g][0], later_loads[g][1])
                 for g in in_range(p - BIAS_ADD)[e : e + 1]:
                     add_row_terms(g)
                 for g in in_range(p - QUANTISE)[e : e + 1]:

@@ -44,7 +44,7 @@ def triangle(lo, descending, tag):
     pieces = [("p", columns[c]) for c in (1, 2, 3)]
     if descending:
         pieces += [("n", rows[0][0:2]), ("n", rows[0][2:4]), ("n", rows[1][0:1]), ("n", rows[1][1:3]), ("n", rows[2]), ("n", rows[3])]
-        order = columns[3] + columns[2] + rows[2][0:1] + rows[3] + columns[1] + rows[0][0:1] + rows[1][0:1]
+        order = rows[0][2:4] + rows[1][1:3] + rows[2][1:2] + rows[2][0:1] + rows[3] + columns[1] + rows[0][0:1] + rows[1][0:1]
     else:
         pieces += [("n", rows[r]) for r in range(4)]
         order = [pair for c in range(4) for pair in columns[c] + rows[c][0:1]]
@@ -198,16 +198,15 @@ def tile_differentiablelogicmachine_pa_t_kernel(tc, x1, x2, W2, b2, out):
 
         def row_matmul(a):
             rp = psum_o.tile([P, 2 * O], F32, name="ps")
-            for s in range(2):
-                nc.tensor.matmul_mx(
-                    out=rp[:, s * O : (s + 1) * O],
-                    lhsT=by_i_codes[:, a, :].bitcast(FP8X4),
-                    lhsT_scale=by_i_scales[:, a, :],
-                    rhs=w1_codes[:, (1 - s) * O : (2 - s) * O].bitcast(FP8X4),
-                    rhs_scale=w1_scales[:, (1 - s) * O : (2 - s) * O],
-                    start=True,
-                    stop=True,
-                )
+            nc.tensor.matmul_mx(
+                out=rp[:],
+                lhsT=by_i_codes[:, a, :].bitcast(FP8X4),
+                lhsT_scale=by_i_scales[:, a, :],
+                rhs=w1_codes[:].bitcast(FP8X4),
+                rhs_scale=w1_scales[:],
+                start=True,
+                stop=True,
+            )
             row_psum[a] = rp
 
         def row_add_bias(a):
@@ -221,7 +220,7 @@ def tile_differentiablelogicmachine_pa_t_kernel(tc, x1, x2, W2, b2, out):
                 row_terms[7] = row_high[:, 1, :, :]
             nc.vector.tensor_tensor(
                 out=row_terms[a],
-                in0=row_psum[a][:].rearrange("p (s o) -> p s o", s=2),
+                in0=row_psum[a][:].rearrange("p (s o) -> p s o", s=2)[:, ::-1, :],
                 in1=bias[:].unsqueeze(1).to_broadcast([P, 2, O]),
                 op=ADD,
             )
@@ -259,7 +258,7 @@ def tile_differentiablelogicmachine_pa_t_kernel(tc, x1, x2, W2, b2, out):
         nc.tensor.matmul(out=bias_psum[:, 0:O], lhsT=ones[:], rhs=bias_row[:], start=True, stop=True)
         nc.scalar.copy(out=bias[:], in_=bias_psum[:, 0:O])
 
-        row_terms_in = {3: 0, 4: 1, 5: 2, 6: 3, 11: 4, 13: 5, 14: 6, 16: 7}
+        row_terms_in = {3: 0, 4: 1, 5: 2, 7: 3, 12: 4, 14: 5, 16: 6, 19: 7}
         repeats_in = {1: 1, 4: 2, 8: 3}
         quantises_in = {2: 1, 5: 2, 9: 3}
 

@@ -51,20 +51,25 @@ def triangle(lo, descending, tag):
     return chunk_of(order, direct, mirrored, pieces, tag)
 
 
-def rectangle(cl_lo, tag):
+def rectangle(cl_lo, by_rows, tag):
     rows = [[(a, cl_lo), (a, cl_lo + 1)] for a in range(4)]
     columns = [[(a, cl) for a in range(4)] for cl in (cl_lo, cl_lo + 1)]
     direct = {pair: k for k, pair in enumerate(rows[0] + rows[1] + rows[2] + rows[3])}
     mirrored = {pair: len(direct) + k for k, pair in enumerate(columns[0] + columns[1])}
-    pieces = [("n", row) for row in rows] + [("p", column) for column in columns]
-    return chunk_of(columns[0] + columns[1], direct, mirrored, pieces, tag)
+    if by_rows:
+        order = rows[0] + rows[1] + rows[2] + rows[3]
+        pieces = [("n", row) for row in rows] + [("p", column[k : k + 2]) for column in columns for k in (0, 2)]
+    else:
+        order = columns[0] + columns[1]
+        pieces = [("n", row) for row in rows] + [("p", column) for column in columns]
+    return chunk_of(order, direct, mirrored, pieces, tag)
 
 
 def make_groups():
     return (
         triangle(0, False, "result_a")
-        + rectangle(4, "result_b")
-        + rectangle(6, "result_c")
+        + rectangle(4, False, "result_b")
+        + rectangle(6, True, "result_c")
         + triangle(4, True, "result_a")
     )
 
@@ -73,8 +78,8 @@ def tile_differentiablelogicmachine_pa_t_kernel(tc, x1, x2, W2, b2, out):
     nc = tc.nc
     with ExitStack() as ctx:
         const = ctx.enter_context(tc.tile_pool(name="const", bufs=1))
-        gpool = ctx.enter_context(tc.tile_pool(name="gpool", bufs=4))
-        cpool = ctx.enter_context(tc.tile_pool(name="cpool", bufs=7))
+        gpool = ctx.enter_context(tc.tile_pool(name="gpool", bufs=2))
+        cpool = ctx.enter_context(tc.tile_pool(name="cpool", bufs=4))
         upool = ctx.enter_context(tc.tile_pool(name="upool", bufs=2))
         rpool = ctx.enter_context(tc.tile_pool(name="rpool", bufs=1))
         psum_t = ctx.enter_context(tc.psum_pool(name="psum_t", bufs=4))
@@ -155,9 +160,11 @@ def tile_differentiablelogicmachine_pa_t_kernel(tc, x1, x2, W2, b2, out):
             else:
                 nc.scalar.copy(out=target, in_=source)
 
-        def repeat_by_j(u, engine):
-            rep = upool.tile([P, 1024], F32, align_bytes=64)
-            for gamma in range(2):
+        def repeat_by_j(u, engine, gammas=(0, 1)):
+            if 0 in gammas:
+                repeated[("j", u)] = upool.tile([P, 1024], F32, align_bytes=64, name="rep")
+            rep = repeated[("j", u)]
+            for gamma in gammas:
                 q0 = 2 * gamma + u // 2
                 r0 = 2 * (u % 2)
                 copy_on(
@@ -168,7 +175,6 @@ def tile_differentiablelogicmachine_pa_t_kernel(tc, x1, x2, W2, b2, out):
                     .unsqueeze(2)
                     .to_broadcast([P, 32, 4, 2, 2]),
                 )
-            repeated[("j", u)] = rep
 
         def quantise_by_j(u):
             nc.vector.quantize_mx(
@@ -178,7 +184,7 @@ def tile_differentiablelogicmachine_pa_t_kernel(tc, x1, x2, W2, b2, out):
             )
 
         def repeat_by_i(u, engine):
-            rep = upool.tile([P, 1024], F32, align_bytes=64)
+            rep = upool.tile([P, 1024], F32, align_bytes=64, name="rep")
             copy_on(
                 engine,
                 rep[:].rearrange("p (m J w) -> p m J w", m=256, J=2, w=2),
@@ -259,7 +265,7 @@ def tile_differentiablelogicmachine_pa_t_kernel(tc, x1, x2, W2, b2, out):
         nc.scalar.copy(out=bias[:], in_=bias_psum[:, 0:O])
 
         row_terms_in = {3: 0, 4: 1, 5: 2, 7: 3, 12: 4, 14: 5, 16: 6, 19: 7}
-        repeats_in = {1: 1, 4: 2, 8: 3}
+        repeats_in = {1: 1, 8: 3}
         quantises_in = {2: 1, 5: 2, 9: 3}
 
         groups = make_groups()
@@ -280,20 +286,23 @@ def tile_differentiablelogicmachine_pa_t_kernel(tc, x1, x2, W2, b2, out):
             transposed[g] = xt
 
         def exits(g):
-            grouped = gpool.tile([P, 2, P, 2], F32, align_bytes=64)
-            nc.scalar.copy(out=grouped[:], in_=transposed[g][:].rearrange("p g w m y J -> p g (m y J) w"))
-            grouped_of[g] = grouped
-
-        def quantise(g):
-            codes = cpool.tile([P, 2 * P], U32, align_bytes=64)
-            scales = cpool.tile([P, 2 * P], U8, align_bytes=64)
-            nc.vector.quantize_mx(
-                out=codes[:].bitcast(FP8X4),
-                scales=scales[:],
-                in_=grouped_of[g][:].rearrange("p g n w -> p (g n w)").bitcast(BF16),
+            if g % 2 == 0:
+                grouped_of[g // 2] = gpool.tile([P, 2, 2, P, 2], F32, align_bytes=64, name="grouped")
+            nc.scalar.copy(
+                out=grouped_of[g // 2][:, g % 2, :, :, :], in_=transposed[g][:].rearrange("p g w m y J -> p g (m y J) w")
             )
-            codes_of[g] = codes
-            scales_of[g] = scales
+
+        def quantise(p):
+            codes = cpool.tile([P, 2, 2 * P], U32, align_bytes=64)
+            scales = cpool.tile([P, 2, 2 * P], U8, align_bytes=64)
+            nc.vector.quantize_mx(
+                out=codes[:].rearrange("p h n -> p (h n)").bitcast(FP8X4),
+                scales=scales[:].rearrange("p h n -> p (h n)"),
+                in_=grouped_of[p][:].rearrange("p h g n w -> p (h g n w)").bitcast(BF16),
+            )
+            for h in range(2):
+                codes_of[2 * p + h] = codes[:, h, :]
+                scales_of[2 * p + h] = scales[:, h, :]
 
         def matmuls(g):
             wide = groups[g]["mirrored"] is not None
@@ -387,8 +396,8 @@ def tile_differentiablelogicmachine_pa_t_kernel(tc, x1, x2, W2, b2, out):
                     sigmoids_and_stores(g)
                 for g in in_range(p - BIAS_ADD)[e : e + 1]:
                     add_row_terms(g)
-                for g in in_range(p - QUANTISE)[e : e + 1]:
-                    quantise(g)
+                if e == 0 and in_range(p - QUANTISE):
+                    quantise(p - QUANTISE)
                 if p in row_terms_in:
                     if e == 0:
                         row_matmul(row_terms_in[p])
@@ -400,6 +409,8 @@ def tile_differentiablelogicmachine_pa_t_kernel(tc, x1, x2, W2, b2, out):
                 matmuls(g)
             if p in repeats_in:
                 repeat_by_j(repeats_in[p], "vector")
+            if p in (2, 3):
+                repeat_by_j(2, "scalar", gammas=(p - 2,))
             if p in quantises_in:
                 quantise_by_j(quantises_in[p])
             if p == 9:

@@ -241,12 +241,13 @@ def tile_differentiablelogicmachine_pa_t_kernel(tc, x1, x2, W2, b2, out):
         repeat_by_i(0, "scalar")
         for x in range(2):
             nc.vector.tensor_copy(
-                out=w2_grouped[:, x, :, :, :],
-                in_=(w_rows_x2[:, ::-1, :, :] if x == 1 else w_rows_x2[:]).rearrange("p s e o -> p o s e"),
+                out=w2_grouped[:, x, :, :, :].rearrange("p (c i) s e -> p c s e i", i=4),
+                in_=(w_rows_x2[:, ::-1, :, :] if x == 1 else w_rows_x2[:]).rearrange("p s e (c i) -> p c s e i", i=4),
             )
         for x in range(2):
             nc.vector.tensor_copy(
-                out=w1_grouped[:, x, :, 0, :], in_=w_rows_x1[:, 1 - x, :, :].rearrange("p e o -> p o e")
+                out=w1_grouped[:, x, :, 0, :].rearrange("p (c i) e -> p c e i", i=4),
+                in_=w_rows_x1[:, 1 - x, :, :].rearrange("p e (c i) -> p c e i", i=4),
             )
         nc.vector.quantize_mx(
             out=w2_codes[:].bitcast(FP8X4),
@@ -266,7 +267,7 @@ def tile_differentiablelogicmachine_pa_t_kernel(tc, x1, x2, W2, b2, out):
 
         row_terms_in = {3: 0, 4: 1, 5: 2, 7: 3, 12: 4, 14: 5, 16: 6, 19: 7}
         repeats_in = {1: 1, 8: 3}
-        quantises_in = {2: 1, 5: 2, 9: 3}
+        quantises_in = {2: 1, 4: 2, 9: 3}
 
         groups = make_groups()
         n_groups = len(groups)

from contextlib import ExitStack

import concourse.mybir as mybir
from concourse.masks import make_identity

F32 = mybir.dt.float32
BF16 = mybir.dt.bfloat16
U32 = mybir.dt.uint32
U8 = mybir.dt.uint8
FP8X4 = mybir.dt.float8_e4m3fn_x4
ADD = mybir.AluOpType.add
SIGMOID = mybir.ActivationFunctionType.Sigmoid

P = 128
O = 256
FLOPS = 2 * 16 * 32 * 32 * 1024 * 256

EXIT = 1
QUANTISE = 2
MATMUL = 3
BIAS_ADD = 4
SIGMOID_STORE = 5
SLOTS = 16


def by_j_block(c):
    return (c % 8 // 2) * 4 + (c // 8) * 2 + c % 2


def chunk_of(order, direct, mirrored, pieces, tag):
    groups = [dict(a=a, cl=cl, tag=tag, direct=direct[(a, cl)], mirrored=mirrored.get((a, cl)), stores=[]) for a, cl in order]
    groups[0]["first"] = True
    for kind, members in pieces:
        last = max(order.index(pair) for pair in members)
        groups[last]["stores"].append((kind, members, (direct if kind == "n" else mirrored)[members[0]]))
    return groups


def triangle(lo, descending, tag):
    rows = {r: [(lo + r, lo + c) for c in range(r, 4)] for r in range(4)}
    columns = {c: [(lo + r, lo + c) for r in range(c)] for c in range(4)}
    direct = {pair: k for k, pair in enumerate(rows[0] + rows[1] + rows[2] + rows[3])}
    mirrored = {pair: len(direct) + k for k, pair in enumerate(columns[1] + columns[2] + columns[3])}
    pieces = [("p", columns[c]) for c in (1, 2, 3)]
    if descending:
        pieces += [("n", rows[0][0:2]), ("n", rows[0][2:4]), ("n", rows[1][0:1]), ("n", rows[1][1:3]), ("n", rows[2]), ("n", rows[3])]
        order = rows[0][2:4] + rows[1][1:3] + rows[2][1:2] + rows[2][0:1] + rows[3] + columns[1] + rows[0][0:1] + rows[1][0:1]
    else:
        pieces += [("n", rows[r]) for r in range(4)]
        order = [pair for c in range(4) for pair in columns[c] + rows[c][0:1]]
    return chunk_of(order, direct, mirrored, pieces, tag)


def rectangle(cl_lo, by_rows, tag):
    rows = [[(a, cl_lo), (a, cl_lo + 1)] for a in range(4)]
    columns = [[(a, cl) for a in range(4)] for cl in (cl_lo, cl_lo + 1)]
    direct = {pair: k for k, pair in enumerate(rows[0] + rows[1] + rows[2] + rows[3])}
    mirrored = {pair: len(direct) + k for k, pair in enumerate(columns[0] + columns[1])}
    if by_rows:
        order = rows[0] + rows[1] + rows[2] + rows[3]
        pieces = [("n", row) for row in rows] + [("p", column[k : k + 2]) for column in columns for k in (0, 2)]
    else:
        order = columns[0] + columns[1]
        pieces = [("n", row) for row in rows] + [("p", column) for column in columns]
    return chunk_of(order, direct, mirrored, pieces, tag)


def make_groups():
    return (
        triangle(0, False, "result_a")
        + rectangle(4, False, "result_b")
        + rectangle(6, True, "result_c")
        + triangle(4, True, "result_a")
    )


def tile_differentiablelogicmachine_pa_t_kernel(tc, x1, x2, W2, b2, out):
    nc = tc.nc
    with ExitStack() as ctx:
        const = ctx.enter_context(tc.tile_pool(name="const", bufs=1))
        gpool = ctx.enter_context(tc.tile_pool(name="gpool", bufs=2))
        cpool = ctx.enter_context(tc.tile_pool(name="cpool", bufs=4))
        upool = ctx.enter_context(tc.tile_pool(name="upool", bufs=2))
        rpool = ctx.enter_context(tc.tile_pool(name="rpool", bufs=1))
        psum_t = ctx.enter_context(tc.psum_pool(name="psum_t", bufs=4))
        psum_o = ctx.enter_context(tc.psum_pool(name="psum_o", bufs=4))
        ctx.enter_context(tc.manual_schedule())

        x1_rows = const.tile([P, 4, O], BF16)
        nc.sync.dma_start(out=x1_rows[:], in_=x1.rearrange("b (q r) c -> (b q) r c", r=4))
        w_view = W2.rearrange("(k p e) o -> p k e o", k=4, p=P, e=2)
        w_rows_x2 = const.tile([P, 2, 2, O], BF16)
        w_rows_x1 = const.tile([P, 2, 2, O], BF16)
        nc.sync.dma_start(out=w_rows_x2[:], in_=w_view[:, 1:4:2, :, :])
        nc.sync.dma_start(out=w_rows_x1[:], in_=w_view[:, 0:3:2, :, :])
        bias_row = const.tile([P, O], BF16)
        nc.vector.memset(bias_row[:], 0.0)
        nc.sync.dma_start(out=bias_row[0:1, :], in_=b2.rearrange("(a o) -> a o", a=1))

        x2_words = {}
        x2_view = x2.rearrange("b (I a) (G c) k -> a (b I) G (c k)", I=4, a=8, G=4, c=8)
        x2_whole = x2.rearrange("b (I a) (J m) k -> a (b I) J (m k)", I=4, a=8, J=2, m=16)
        out_n = out.rearrange("b (I a) (G c) o -> a (b I) G (c o)", I=4, a=8, G=4, c=8)
        out_p = out.rearrange("b (J c) (I a) o -> c J b I (a o)", J=2, c=16, I=4, a=8)

        def load_x2(a, lo, hi):
            rows = const.tile([P, 2, hi - lo, O], BF16, name="x2_%d_%d" % (a, lo))
            if hi - lo == 8:
                nc.sync.dma_start(out=rows[:].rearrange("p g c k -> p (g c k)"), in_=x2_whole[a])
            else:
                nc.sync.dma_start(out=rows[:].rearrange("p g c k -> p g (c k)"), in_=x2_view[a, :, :, lo * O : hi * O])
            for gamma in range(2):
                for cl in range(lo, hi):
                    x2_words[(a, gamma, cl)] = rows[:, gamma, cl - lo, :].bitcast(F32)

        for a in range(4):
            load_x2(a, 0, 4)
        load_x2(4, 0, 8)
        for a in range(4):
            load_x2(a, 4, 8)
        for a in (5, 6, 7):
            load_x2(a, 0, 8)

        ident = const.tile([P, P], F32)
        make_identity(nc, ident[:])
        warm_in = const.tile([P, 1], F32)
        nc.vector.memset(warm_in[:], 0.0)
        warm_out = const.tile([P, 1], F32)
        nc.scalar.activation(out=warm_out[:], in_=warm_in[:], func=SIGMOID)
        x1_words = const.tile([P, 2, 4, 16, 8], F32)
        nc.vector.memset(x1_words[:, 1, :, :, :], 0.0)
        w2_grouped = const.tile([P, 2, O, 2, 2], BF16, align_bytes=64, name="w2_grouped")
        w1_grouped = const.tile([P, 2, O, 2, 2], BF16, align_bytes=64, name="w1_grouped")
        nc.vector.memset(w1_grouped[:], 0.0)
        ones = const.tile([P, P], BF16)
        nc.vector.memset(ones[:], 1.0)
        by_partner = const.tile([P, P], F32)
        for gamma in range(2):
            nc.vector.tensor_copy(
                out=by_partner[:, 64 * gamma : 64 * gamma + 64].rearrange("p (b x J) -> p b x J", b=16, x=2, J=2),
                in_=ident[:].rearrange("p (b J g x) -> p g b x J", b=16, J=2, g=2, x=2)[:, gamma, :, :, :],
            )

        w2_codes = const.tile([P, 2 * O], U32, align_bytes=64)
        w2_scales = const.tile([P, 2 * O], U8, align_bytes=64)
        w1_codes = const.tile([P, 2 * O], U32, align_bytes=64)
        w1_scales = const.tile([P, 2 * O], U8, align_bytes=64)
        by_j_codes = const.tile([P, 16, P], U32, align_bytes=64)
        by_j_scales = const.tile([P, 16, P], U8, align_bytes=64)
        by_i_codes = const.tile([P, 8, P], U32, align_bytes=64)
        by_i_scales = const.tile([P, 8, P], U8, align_bytes=64)
        bias = const.tile([P, O], F32)
        row_low = const.tile([P, 4, 2, O], F32)
        row_terms = {a: row_low[:, a, :, :] for a in range(4)}
        repeated, row_psum = {}, {}

        def copy_on(engine, target, source):
            if engine == "vector":
                nc.vector.tensor_copy(out=target, in_=source)
            else:
                nc.scalar.copy(out=target, in_=source)

        def repeat_by_j(u, engine, gammas=(0, 1)):
            if 0 in gammas:
                repeated[("j", u)] = upool.tile([P, 1024], F32, align_bytes=64, name="rep")
            rep = repeated[("j", u)]
            for gamma in gammas:
                q0 = 2 * gamma + u // 2
                r0 = 2 * (u % 2)
                copy_on(
                    engine,
                    rep[:, gamma * 512 : (gamma + 1) * 512].rearrange("p (m I J w) -> p m I J w", m=32, I=4, J=2, w=2),
                    x1_words[:, :, r0 : r0 + 2, :, q0 : q0 + 5 : 4]
                    .rearrange("p w r b J -> p (r b) J w")
                    .unsqueeze(2)
                    .to_broadcast([P, 32, 4, 2, 2]),
                )

        def quantise_by_j(u):
            nc.vector.quantize_mx(
                out=by_j_codes[:, 4 * u : 4 * u + 4, :].rearrange("p c n -> p (c n)").bitcast(FP8X4),
                scales=by_j_scales[:, 4 * u : 4 * u + 4, :].rearrange("p c n -> p (c n)"),
                in_=repeated[("j", u)][:].bitcast(BF16),
            )

        def repeat_by_i(u, engine):
            rep = upool.tile([P, 1024], F32, align_bytes=64, name="rep")
            copy_on(
                engine,
                rep[:].rearrange("p (m J w) -> p m J w", m=256, J=2, w=2),
                x1_words[:, :, :, :, u : u + 7 : 2]
                .rearrange("p w r b I -> p (r b I) w")
                .unsqueeze(2)
                .to_broadcast([P, 256, 2, 2]),
            )
            repeated[("i", u)] = rep

        def quantise_by_i(u):
            nc.vector.quantize_mx(
                out=by_i_codes[:, 4 * u : 4 * u + 4, :].rearrange("p a n -> p (a n)").bitcast(FP8X4),
                scales=by_i_scales[:, 4 * u : 4 * u + 4, :].rearrange("p a n -> p (a n)"),
                in_=repeated[("i", u)][:].bitcast(BF16),
            )

        def row_matmul(a):
            rp = psum_o.tile([P, 2 * O], F32, name="ps")
            nc.tensor.matmul_mx(
                out=rp[:],
                lhsT=by_i_codes[:, a, :].bitcast(FP8X4),
                lhsT_scale=by_i_scales[:, a, :],
                rhs=w1_codes[:].bitcast(FP8X4),
                rhs_scale=w1_scales[:],
                start=True,
                stop=True,
            )
            row_psum[a] = rp

        def row_add_bias(a):
            if a == 4:
                row_high = const.tile([P, 2, 2, O], F32, align_bytes=64, name="w2_grouped")
                row_terms[4] = row_high[:, 0, :, :]
                row_terms[5] = row_high[:, 1, :, :]
            if a == 6:
                row_high = const.tile([P, 2, 2, O], F32, align_bytes=64, name="w1_grouped")
                row_terms[6] = row_high[:, 0, :, :]
                row_terms[7] = row_high[:, 1, :, :]
            nc.vector.tensor_tensor(
                out=row_terms[a],
                in0=row_psum[a][:].rearrange("p (s o) -> p s o", s=2)[:, ::-1, :],
                in1=bias[:].unsqueeze(1).to_broadcast([P, 2, O]),
                op=ADD,
            )

        x1_t = psum_t.tile([P, 4, P], F32, name="xt")
        for r in range(4):
            nc.tensor.transpose(out=x1_t[:, r, :], in_=x1_rows[:, r, :].bitcast(F32), identity=ident[:])
        nc.scalar.copy(
            out=x1_words[:, 0, :, :, :].rearrange("p r b q -> p (r b q)"), in_=x1_t[:].rearrange("p r n -> p (r n)")
        )
        repeat_by_j(0, "scalar")
        repeat_by_i(0, "scalar")
        for x in range(2):
            nc.vector.tensor_copy(
                out=w2_grouped[:, x, :, :, :].rearrange("p (c i) s e -> p c s e i", i=4),
                in_=(w_rows_x2[:, ::-1, :, :] if x == 1 else w_rows_x2[:]).rearrange("p s e (c i) -> p c s e i", i=4),
            )
        for x in range(2):
            nc.vector.tensor_copy(
                out=w1_grouped[:, x, :, 0, :].rearrange("p (c i) e -> p c e i", i=4),
                in_=w_rows_x1[:, 1 - x, :, :].rearrange("p e (c i) -> p c e i", i=4),
            )
        nc.vector.quantize_mx(
            out=w2_codes[:].bitcast(FP8X4),
            scales=w2_scales[:],
            in_=w2_grouped[:].rearrange("p x o s e -> p (x o s e)"),
        )
        quantise_by_j(0)
        nc.vector.quantize_mx(
            out=w1_codes[:].bitcast(FP8X4),
            scales=w1_scales[:],
            in_=w1_grouped[:].rearrange("p x o s e -> p (x o s e)"),
        )
        quantise_by_i(0)
        bias_psum = psum_o.tile([P, 2 * O], F32, name="ps")
        nc.tensor.matmul(out=bias_psum[:, 0:O], lhsT=ones[:], rhs=bias_row[:], start=True, stop=True)
        nc.scalar.copy(out=bias[:], in_=bias_psum[:, 0:O])

        row_terms_in = {3: 0, 4: 1, 5: 2, 7: 3, 12: 4, 14: 5, 16: 6, 19: 7}
        repeats_in = {1: 1, 8: 3}
        quantises_in = {2: 1, 4: 2, 9: 3}

        groups = make_groups()
        n_groups = len(groups)
        transposed, grouped_of, codes_of, scales_of, sums, result_of = {}, {}, {}, {}, {}, {}

        def transposes(g):
            a, cl = groups[g]["a"], groups[g]["cl"]
            xt = psum_t.tile([P, 2, 2, 32, 2, 2], F32)
            for gamma in range(2):
                nc.tensor.transpose(
                    out=xt[:, gamma, 0, :, :, :].rearrange("p m y J -> p (m y J)"),
                    in_=x2_words[(a, gamma, cl)],
                    identity=ident[:],
                )
            for y in range(2):
                nc.tensor.transpose(out=xt[:, :, 1, :, y, :], in_=x2_words[(cl, y, a)], identity=by_partner[:])
            transposed[g] = xt

        def exits(g):
            if g % 2 == 0:
                grouped_of[g // 2] = gpool.tile([P, 2, 2, P, 2], F32, align_bytes=64, name="grouped")
            nc.scalar.copy(
                out=grouped_of[g // 2][:, g % 2, :, :, :], in_=transposed[g][:].rearrange("p g w m y J -> p g (m y J) w")
            )

        def quantise(p):
            codes = cpool.tile([P, 2, 2 * P], U32, align_bytes=64)
            scales = cpool.tile([P, 2, 2 * P], U8, align_bytes=64)
            nc.vector.quantize_mx(
                out=codes[:].rearrange("p h n -> p (h n)").bitcast(FP8X4),
                scales=scales[:].rearrange("p h n -> p (h n)"),
                in_=grouped_of[p][:].rearrange("p h g n w -> p (h g n w)").bitcast(BF16),
            )
            for h in range(2):
                codes_of[2 * p + h] = codes[:, h, :]
                scales_of[2 * p + h] = scales[:, h, :]

        def matmuls(g):
            wide = groups[g]["mirrored"] is not None
            width = 2 * O if wide else O
            for gamma in range(2):
                if wide or gamma == 0:
                    ps = psum_o.tile([P, 2 * O], F32)
                    lo = 0
                else:
                    lo = O
                c = by_j_block(8 * gamma + groups[g]["cl"])
                nc.tensor.matmul_mx(
                    out=ps[:, lo : lo + width],
                    lhsT=codes_of[g][:, gamma * P : (gamma + 1) * P].bitcast(FP8X4),
                    lhsT_scale=scales_of[g][:, gamma * P : (gamma + 1) * P],
                    rhs=w2_codes[:, 0:width].bitcast(FP8X4),
                    rhs_scale=w2_scales[:, 0:width],
                    start=True,
                    stop=False,
                )
                nc.tensor.matmul_mx(
                    out=ps[:, lo : lo + width],
                    lhsT=by_j_codes[:, c, :].bitcast(FP8X4),
                    lhsT_scale=by_j_scales[:, c, :],
                    rhs=w1_codes[:, 0:width].bitcast(FP8X4),
                    rhs_scale=w1_scales[:, 0:width],
                    start=False,
                    stop=True,
                )
                sums[(g, gamma)] = ps

        def result_slots(g):
            direct, mirrored = groups[g]["direct"], groups[g]["mirrored"]
            view = result_of[g][:].rearrange("p (g s) o -> p g s o", g=2)
            if mirrored is None:
                return view[:, :, direct, :]
            return view[:, :, direct : mirrored + 1 : mirrored - direct, :]

        def add_row_terms(g):
            group = groups[g]
            if group.get("first"):
                result_of["now"] = rpool.tile([P, 2 * SLOTS, O], F32, name=group["tag"])
            result_of[g] = result_of["now"]
            a = group["a"]
            if group["mirrored"] is None:
                nc.vector.tensor_tensor(
                    out=result_slots(g),
                    in0=sums[(g, 0)][:].rearrange("p (s o) -> p s o", s=2),
                    in1=row_terms[a][:, 0, :].unsqueeze(1).to_broadcast([P, 2, O]),
                    op=ADD,
                )
                return
            for gamma in range(2):
                nc.vector.tensor_tensor(
                    out=result_slots(g)[:, gamma, :, :],
                    in0=sums[(g, gamma)][:].rearrange("p (s o) -> p s o", s=2),
                    in1=row_terms[a],
                    op=ADD,
                )

        def sigmoids_and_stores(g):
            nc.scalar.activation(out=result_slots(g), in_=result_slots(g), func=SIGMOID)
            result = result_of[g]
            for kind, members, s in groups[g]["stores"]:
                if kind == "n":
                    major, lo, hi = members[0][0], members[0][1], members[-1][1] + 1
                    nc.sync.dma_start(
                        out=out_n[major, :, :, lo * O : hi * O],
                        in_=result[:]
                        .rearrange("p (g s) o -> p g s o", g=2)[:, :, s : s + hi - lo, :]
                        .rearrange("p g s o -> p g (s o)"),
                    )
                else:
                    major, lo, hi = members[0][1], members[0][0], members[-1][0] + 1
                    for gamma in range(2):
                        first = gamma * SLOTS + s
                        for J in range(2):
                            nc.sync.dma_start(
                                out=out_p[8 * gamma + major, J, :, :, lo * O : hi * O],
                                in_=result[J:P:2, first : first + hi - lo, :].rearrange("p s o -> p (s o)"),
                            )

        def in_range(p):
            return [g for g in (2 * p, 2 * p + 1) if 0 <= g < n_groups]

        for p in range(n_groups // 2 + SIGMOID_STORE):
            for g in in_range(p):
                transposes(g)
            for e in range(2):
                for g in in_range(p - SIGMOID_STORE)[e : e + 1]:
                    sigmoids_and_stores(g)
                for g in in_range(p - BIAS_ADD)[e : e + 1]:
                    add_row_terms(g)
                if e == 0 and in_range(p - QUANTISE):
                    quantise(p - QUANTISE)
                if p in row_terms_in:
                    if e == 0:
                        row_matmul(row_terms_in[p])
                    else:
                        row_add_bias(row_terms_in[p])
                for g in in_range(p - EXIT)[e : e + 1]:
                    exits(g)
            for g in in_range(p - MATMUL):
                matmuls(g)
            if p in repeats_in:
                repeat_by_j(repeats_in[p], "vector")
            if p in (2, 3):
                repeat_by_j(2, "scalar", gammas=(p - 2,))
            if p in quantises_in:
                quantise_by_j(quantises_in[p])
            if p == 9:
                repeat_by_i(1, "vector")
            if p == 10:
                quantise_by_i(1)
